import numpy as np
import ml_dtypes


def mxq(x, axis, fmt="e4m3"):
    dtype, down = {"e4m3": (ml_dtypes.float8_e4m3fn, 7), "e5m2": (ml_dtypes.float8_e5m2, 14)}[fmt]
    v = np.moveaxis(np.asarray(x, np.float32).astype(ml_dtypes.bfloat16).astype(np.float64), axis, -1)
    blocks = v.reshape(v.shape[:-1] + (-1, 32))
    amax = np.abs(blocks).max(-1, keepdims=True)
    byte = np.maximum(np.where(amax > 0, np.frexp(amax)[1] - 1 + 127, 0) - down, 1)
    scale = np.exp2(byte - 127.0)
    codes = (blocks / scale).astype(np.float32).astype(dtype).astype(np.float64)
    return np.moveaxis((codes * scale).reshape(v.shape), -1, axis)


WIDE = False


def mx_kscale(k):
    if not WIDE:
        return np.ones(k)
    levels = np.array([10, -10, 5, -5, 0])
    if k % 512:
        return np.exp2(np.random.permutation(np.resize(levels, k // 32))).repeat(32)
    a = np.empty((k // 512, 16))
    for p in range(k // 512):
        a[p, :8] = np.random.permutation(np.resize(levels, 8))
        for g in range(8):
            far = levels[np.abs(levels - a[p, g]) >= 10]
            a[p, g + 8] = far[np.random.randint(len(far))]
    return np.exp2(a.ravel()).repeat(32)


BF16 = ml_dtypes.bfloat16


def bf(x):
    return np.asarray(x, np.float32).astype(BF16)


def f64(x):
    return np.asarray(x).astype(np.float64)


B, S, D, H = 1, 512, 2048, 16
HD = D // H
HALF = HD // 2


def rotary(v, cos, sin):
    p = v.reshape(B, S, H, HALF, 2)
    vr, vi = p[..., 0], p[..., 1]
    c = cos[None, :, None, :]
    s = sin[None, :, None, :]
    return np.stack([vr * c - vi * s, vr * s + vi * c], axis=-1).reshape(B, S, H, HD)


def draw0():
    s = mx_kscale(D)
    inv_freq = 1.0 / (10000.0 ** (np.arange(0, HD, 2) / HD))
    angles = np.arange(S)[:, None] * inv_freq[None, :]
    return {"x": bf(np.random.standard_normal((B, S, D)) * s),
            "freqs_cos": bf(np.cos(angles)), "freqs_sin": bf(np.sin(angles)),
            "wq": bf(np.random.standard_normal((D, D)) * 1.4 / np.sqrt(D) / s[:, None]),
            "wk": bf(np.random.standard_normal((D, D)) * 1.4 / np.sqrt(D) / s[:, None])}


def core(x, freqs_cos, freqs_sin, wq, wk):
    xq = mxq(f64(x), 2, "e4m3")
    q = (xq @ mxq(f64(wq), 0, "e4m3")).reshape(B, S, H, HD)
    k = (xq @ mxq(f64(wk), 0, "e4m3")).reshape(B, S, H, HD)
    c, s = f64(freqs_cos), f64(freqs_sin)
    return rotary(q, c, s), rotary(k, c, s)


def e4m3fn_bytes(y):
    return np.clip(np.asarray(y, np.float64), -448.0, 448.0).astype(np.float32).astype(ml_dtypes.float8_e4m3fn).view(np.uint8)


def e4m3fn_values(b):
    return np.asarray(b, np.uint8).view(ml_dtypes.float8_e4m3fn).astype(np.float64)


def setup_inputs():
    d = draw0()
    x0 = np.asarray(d['wq']).astype(np.float64)
    s = (np.max(np.abs(x0), axis=(1,), keepdims=True) / 448.0).astype(np.float32)
    out = {}
    for k, v in d.items():
        if k == 'wq':
            out['wq_bytes'] = e4m3fn_bytes(x0 / s.astype(np.float64))
            out['wq_scale'] = s
        else:
            out[k] = v
    return out


def reference(x, freqs_cos, freqs_sin, wq_bytes, wq_scale, wk):
    return core(x, freqs_cos, freqs_sin, e4m3fn_values(wq_bytes) * wq_scale.astype(np.float64), wk)

@@ -1,0 +1,186 @@
+from contextlib import ExitStack
+
+import concourse.mybir as mybir
+from concourse.masks import make_identity
+
+F32 = mybir.dt.float32
+BF16 = mybir.dt.bfloat16
+U32 = mybir.dt.uint32
+U8 = mybir.dt.uint8
+FP8 = mybir.dt.float8_e4m3fn
+FP8X4 = mybir.dt.float8_e4m3fn_x4
+ALU = mybir.AluOpType
+ACT = mybir.ActivationFunctionType
+
+P = 128
+S = 512
+D = 2048
+HD = 128
+HALF = 64
+PACK = 4
+K_PASS = P * PACK
+PASSES = D // K_PASS
+M_TILES = S // P
+NW = 512
+CHUNKS = D // NW
+HEADS_PER_CHUNK = NW // HD
+
+FLOPS = 2 * 2 * S * D * D
+
+
+def tile_attention_pa_kernel(tc, x, freqs_cos, freqs_sin, wq_bytes, wq_scale, wk, out_0, out_1):
+    nc = tc.nc
+    x_v = x.rearrange("b (m p) k -> (b m) p k", p=P)
+    wqb_v = wq_bytes.rearrange("(g p t) n -> g p t n", p=P, t=PACK)
+    wk_v = wk.rearrange("(g p t) n -> g p t n", p=P, t=PACK)
+    outs_v = [
+        out_0.rearrange("b (m p) h d -> (b m) p (h d)", p=P),
+        out_1.rearrange("b (m p) h d -> (b m) p (h d)", p=P),
+    ]
+
+    with ExitStack() as ctx:
+        const = ctx.enter_context(tc.tile_pool(name="const", bufs=1))
+        raw = ctx.enter_context(tc.tile_pool(name="raw", bufs=1))
+        stage = ctx.enter_context(tc.tile_pool(name="stage", bufs=3))
+        codes_pool = ctx.enter_context(tc.tile_pool(name="codes", bufs=8))
+        ep = ctx.enter_context(tc.tile_pool(name="ep", bufs=4))
+        psum = ctx.enter_context(tc.psum_pool(name="psum", bufs=8))
+
+        sc = const.tile([P, PASSES, PACK], F32, name="sc")
+        nc.scalar.dma_start(out=sc[:], in_=wq_scale.rearrange("(g p t) o -> p g (t o)", p=P, t=PACK))
+        cos_sb = const.tile([P, M_TILES, HALF], BF16, name="cos_sb")
+        nc.scalar.dma_start(out=cos_sb[:], in_=freqs_cos.rearrange("(m p) i -> p m i", p=P))
+        sin_sb = const.tile([P, M_TILES, HALF], BF16, name="sin_sb")
+        nc.scalar.dma_start(out=sin_sb[:], in_=freqs_sin.rearrange("(m p) i -> p m i", p=P))
+
+        wqb = {}
+        wkr = {}
+        xr = []
+
+        def load_w(n, g):
+            cols = slice(n * NW, (n + 1) * NW)
+            tq = raw.tile([P, PACK, NW], U8, name="wqb_%d_%d" % (n, g))
+            nc.sync.dma_start(out=tq[:], in_=wqb_v[g][:, :, cols])
+            wqb[(n, g)] = tq
+            tk = raw.tile([P, PACK, NW], BF16, name="wkr_%d_%d" % (n, g))
+            nc.sync.dma_start(out=tk[:], in_=wk_v[g][:, :, cols])
+            wkr[(n, g)] = tk
+
+        def load_x(m):
+            t = raw.tile([P, D], BF16, name="xr_%d" % m)
+            nc.sync.dma_start(out=t[:], in_=x_v[m])
+            xr.append(t)
+
+        load_w(0, 0)
+        load_w(0, 1)
+        load_x(0)
+        load_x(1)
+        load_w(0, 2)
+        load_x(2)
+        load_x(3)
+        load_w(0, 3)
+        for n in range(1, CHUNKS):
+            for g in range(PASSES):
+                load_w(n, g)
+
+        ident = const.tile([P, P], F32, name="ident")
+        make_identity(nc, ident[:])
+        cosT = const.tile([P, M_TILES, HALF, 2], F32, name="cosT")
+        sinT = const.tile([P, M_TILES, HALF, 2], F32, name="sinT")
+        for e in range(2):
+            nc.gpsimd.tensor_copy(out=cosT[:, :, :, e], in_=cos_sb[:])
+        nc.gpsimd.tensor_scalar(out=sinT[:, :, :, 0], in0=sin_sb[:], scalar1=-1.0, scalar2=0.0, op0=ALU.mult, op1=ALU.add)
+        nc.gpsimd.tensor_copy(out=sinT[:, :, :, 1], in_=sin_sb[:])
+
+        xc = []
+        xs = []
+
+        def prep_x(m):
+            words = xr[m][:].bitcast(F32)
+            xg = stage.tile([P, PASSES, P, PACK], BF16, name="xg", tag="xg", align_bytes=64)
+            for half in range(2):
+                xt = psum.tile([P, NW], F32, name="xt", tag="bank")
+                for gl in range(2):
+                    g = 2 * half + gl
+                    for u in range(2):
+                        j = 2 * gl + u
+                        nc.tensor.transpose(xt[:, j * P:(j + 1) * P], words[:, 256 * g + u:256 * (g + 1):2], ident[:])
+                dst = xg[:, 2 * half:2 * half + 2].rearrange("p g r t -> p (g r t)").bitcast(F32).rearrange("p (g r u) -> p g r u", g=2, u=2)
+                src = xt[:].rearrange("p (g u r) -> p g r u", g=2, u=2)
+                if half == 0:
+                    nc.vector.tensor_copy(out=dst, in_=src)
+                else:
+                    nc.scalar.copy(out=dst, in_=src)
+            c = const.tile([P, PASSES * P], U32, name="xc_%d" % m, align_bytes=64)
+            s = const.tile([P, PASSES * P], U8, name="xs_%d" % m, align_bytes=64)
+            nc.vector.quantize_mx(out=c[:].bitcast(FP8X4), scales=s[:], in_=xg[:].rearrange("p g r t -> p (g r t)"))
+            xc.append(c)
+            xs.append(s)
+
+        def interleave(eng_copy, dst, src):
+            eng_copy(out=dst[:].rearrange("p (c i) t -> p c t i", i=4), in_=src[:].rearrange("p t (c i) -> p c t i", i=4))
+
+        def quantise(grouped, tagc, tags):
+            c = codes_pool.tile([P, NW], U32, name=tagc, tag=tagc, align_bytes=64)
+            s = codes_pool.tile([P, NW], U8, name=tags, tag=tags, align_bytes=64)
+            nc.vector.quantize_mx(out=c[:].bitcast(FP8X4), scales=s[:], in_=grouped[:].rearrange("p c t -> p (c t)"))
+            return c, s
+
+        def prep_q(n, g):
+            wide = stage.tile([P, PACK, NW], BF16, name="wide", tag="wide")
+            for t in range(PACK):
+                nc.scalar.activation(out=wide[:, t, :], in_=wqb[(n, g)][:, t, :].bitcast(FP8), func=ACT.Copy, scale=sc[:, g, t:t + 1])
+            gq = stage.tile([P, NW, PACK], BF16, name="gq", tag="gq", align_bytes=64)
+            interleave(nc.scalar.copy, gq, wide)
+            return quantise(gq, "qc", "qs")
+
+        def prep_k(n, g):
+            gk = stage.tile([P, NW, PACK], BF16, name="gk", tag="gk", align_bytes=64)
+            interleave(nc.vector.tensor_copy, gk, wkr[(n, g)])
+            return quantise(gk, "kc", "ks")
+
+        def project(ops, which, n):
+            for m in range(M_TILES):
+                acc = psum.tile([P, NW], F32, name="acc", tag="bank")
+                for g in range(PASSES):
+                    c, s = ops[g]
+                    nc.tensor.matmul_mx(
+                        out=acc[:],
+                        lhsT=xc[m][:, g * P:(g + 1) * P].bitcast(FP8X4),
+                        lhsT_scale=xs[m][:, g * P:(g + 1) * P],
+                        rhs=c[:].bitcast(FP8X4),
+                        rhs_scale=s[:],
+                        start=(g == 0),
+                        stop=(g == PASSES - 1),
+                    )
+                a4 = acc[:].rearrange("p (h i e) -> p h i e", h=HEADS_PER_CHUNK, e=2)
+                shape4 = [P, HEADS_PER_CHUNK, HALF, 2]
+                p1 = ep.tile([P, NW], F32, name="p1", tag="p1")
+                p2 = ep.tile([P, NW], F32, name="p2", tag="p2")
+                nc.vector.tensor_tensor(
+                    out=p1[:].rearrange("p (h i e) -> p h i e", h=HEADS_PER_CHUNK, e=2),
+                    in0=a4,
+                    in1=cosT[:, m].unsqueeze(1).to_broadcast(shape4),
+                    op=ALU.mult,
+                )
+                nc.vector.tensor_tensor(
+                    out=p2[:].rearrange("p (h i e) -> p h i e", h=HEADS_PER_CHUNK, e=2),
+                    in0=a4[:, :, :, ::-1],
+                    in1=sinT[:, m].unsqueeze(1).to_broadcast(shape4),
+                    op=ALU.mult,
+                )
+                nc.gpsimd.tensor_tensor(out=p1[:], in0=p1[:], in1=p2[:], op=ALU.add)
+                nc.sync.dma_start(out=outs_v[which][m][:, n * NW:(n + 1) * NW], in_=p1[:])
+
+        q_ops = [prep_q(0, g) for g in range(2)]
+        k_ops = [prep_k(0, g) for g in range(2)]
+        for m in range(M_TILES):
+            prep_x(m)
+        q_ops += [prep_q(0, g) for g in range(2, PASSES)]
+        k_ops += [prep_k(0, g) for g in range(2, PASSES)]
+        for n in range(CHUNKS):
+            if n > 0:
+                k_ops = [prep_k(n, g) for g in range(PASSES)]
+                q_ops = [prep_q(n, g) for g in range(PASSES)]
+            project(k_ops, 1, n)
+            project(q_ops, 0, n)

@@ -27,24 +27,30 @@ HEADS_PER_CHUNK = NW // HD
 
 FLOPS = 2 * 2 * S * D * D
 
+GK_BUFS = 7
+PE_PATH_PASSES = 3
+K_ON_SCALAR = ((1, 3), (2, 2), (2, 3), (3, 3))
+Q_DIRECT_ON_VECTOR = ()
+
 
 def tile_attention_pa_kernel(tc, x, freqs_cos, freqs_sin, wq_bytes, wq_scale, wk, out_0, out_1):
     nc = tc.nc
     x_v = x.rearrange("b (m p) k -> (b m) p k", p=P)
     wqb_v = wq_bytes.rearrange("(g p t) n -> g p t n", p=P, t=PACK)
     wk_v = wk.rearrange("(g p t) n -> g p t n", p=P, t=PACK)
-    outs_v = [
-        out_0.rearrange("b (m p) h d -> (b m) p (h d)", p=P),
-        out_1.rearrange("b (m p) h d -> (b m) p (h d)", p=P),
-    ]
+    outs_v = {
+        "q": out_0.rearrange("b (m p) h d -> (b m) p (h d)", p=P),
+        "k": out_1.rearrange("b (m p) h d -> (b m) p (h d)", p=P),
+    }
 
     with ExitStack() as ctx:
         const = ctx.enter_context(tc.tile_pool(name="const", bufs=1))
         raw = ctx.enter_context(tc.tile_pool(name="raw", bufs=1))
         stage = ctx.enter_context(tc.tile_pool(name="stage", bufs=3))
-        codes_pool = ctx.enter_context(tc.tile_pool(name="codes", bufs=8))
+        codes_pool = ctx.enter_context(tc.tile_pool(name="codes", bufs=4))
         ep = ctx.enter_context(tc.tile_pool(name="ep", bufs=4))
-        psum = ctx.enter_context(tc.psum_pool(name="psum", bufs=8))
+        psum = ctx.enter_context(tc.psum_pool(name="psum", bufs=4))
+        ctx.enter_context(tc.manual_schedule())
 
         sc = const.tile([P, PASSES, PACK], F32, name="sc")
         nc.scalar.dma_start(out=sc[:], in_=wq_scale.rearrange("(g p t) o -> p g (t o)", p=P, t=PACK))
@@ -53,15 +59,22 @@ def tile_attention_pa_kernel(tc, x, freqs_cos, freqs_sin, wq_bytes, wq_scale, wk
         sin_sb = const.tile([P, M_TILES, HALF], BF16, name="sin_sb")
         nc.scalar.dma_start(out=sin_sb[:], in_=freqs_sin.rearrange("(m p) i -> p m i", p=P))
 
+        warm = const.tile([P, 2], F32, name="warm")
+        nc.vector.memset(warm[:, 0:1], 0.0)
+        nc.scalar.activation(out=warm[:, 1:2], in_=warm[:, 0:1], func=ACT.Copy)
+
         wqb = {}
         wkr = {}
         xr = []
 
-        def load_w(n, g):
+        def load_wq(n, g):
             cols = slice(n * NW, (n + 1) * NW)
             tq = raw.tile([P, PACK, NW], U8, name="wqb_%d_%d" % (n, g))
             nc.sync.dma_start(out=tq[:], in_=wqb_v[g][:, :, cols])
             wqb[(n, g)] = tq
+
+        def load_wk(n, g):
+            cols = slice(n * NW, (n + 1) * NW)
             tk = raw.tile([P, PACK, NW], BF16, name="wkr_%d_%d" % (n, g))
             nc.sync.dma_start(out=tk[:], in_=wk_v[g][:, :, cols])
             wkr[(n, g)] = tk
@@ -71,116 +84,263 @@ def tile_attention_pa_kernel(tc, x, freqs_cos, freqs_sin, wq_bytes, wq_scale, wk
             nc.sync.dma_start(out=t[:], in_=x_v[m])
             xr.append(t)
 
-        load_w(0, 0)
-        load_w(0, 1)
+        load_wq(0, 0)
+        load_wk(0, 0)
+        load_wq(0, 1)
+        load_wk(0, 1)
+        load_wq(0, 2)
+        load_wk(0, 2)
+        load_wk(0, 3)
         load_x(0)
+        load_wq(0, 3)
         load_x(1)
-        load_w(0, 2)
         load_x(2)
         load_x(3)
-        load_w(0, 3)
-        for n in range(1, CHUNKS):
+        for n in range(1, CHUNKS - 1):
             for g in range(PASSES):
-                load_w(n, g)
+                load_wq(n, g)
+                load_wk(n, g)
+        late_loads = [(CHUNKS - 1, g) for g in range(PASSES)]
 
         ident = const.tile([P, P], F32, name="ident")
         make_identity(nc, ident[:])
+        ident_bf = const.tile([P, P], BF16, name="ident_bf")
+        make_identity(nc, ident_bf[:])
         cosT = const.tile([P, M_TILES, HALF, 2], F32, name="cosT")
         sinT = const.tile([P, M_TILES, HALF, 2], F32, name="sinT")
         for e in range(2):
-            nc.gpsimd.tensor_copy(out=cosT[:, :, :, e], in_=cos_sb[:])
-        nc.gpsimd.tensor_scalar(out=sinT[:, :, :, 0], in0=sin_sb[:], scalar1=-1.0, scalar2=0.0, op0=ALU.mult, op1=ALU.add)
-        nc.gpsimd.tensor_copy(out=sinT[:, :, :, 1], in_=sin_sb[:])
+            nc.vector.tensor_copy(out=cosT[:, :, :, e], in_=cos_sb[:])
+        nc.vector.tensor_scalar(out=sinT[:, :, :, 0], in0=sin_sb[:], scalar1=-1.0, scalar2=None, op0=ALU.mult)
+        nc.vector.tensor_copy(out=sinT[:, :, :, 1], in_=sin_sb[:])
 
-        xc = []
-        xs = []
+        xt_tiles = {}
+        xg_tiles = {}
+        xc = {}
+        xs = {}
 
-        def prep_x(m):
+        def x_transpose(m):
             words = xr[m][:].bitcast(F32)
-            xg = stage.tile([P, PASSES, P, PACK], BF16, name="xg", tag="xg", align_bytes=64)
             for half in range(2):
-                xt = psum.tile([P, NW], F32, name="xt", tag="bank")
+                xt = psum.tile([P, NW], F32, name="xt", tag=("il" if m == 2 else "acc"))
                 for gl in range(2):
                     g = 2 * half + gl
                     for u in range(2):
                         j = 2 * gl + u
                         nc.tensor.transpose(xt[:, j * P:(j + 1) * P], words[:, 256 * g + u:256 * (g + 1):2], ident[:])
-                dst = xg[:, 2 * half:2 * half + 2].rearrange("p g r t -> p (g r t)").bitcast(F32).rearrange("p (g r u) -> p g r u", g=2, u=2)
-                src = xt[:].rearrange("p (g u r) -> p g r u", g=2, u=2)
-                if half == 0:
-                    nc.vector.tensor_copy(out=dst, in_=src)
-                else:
-                    nc.scalar.copy(out=dst, in_=src)
+                xt_tiles[(m, half)] = xt
+
+        def x_evac(m, half, copy):
+            if half == 0:
+                xg_tiles[m] = stage.tile([P, PASSES, P, PACK], BF16, name="xg", tag="gk", bufs=GK_BUFS, align_bytes=64)
+            xg = xg_tiles[m]
+            dst = xg[:, 2 * half:2 * half + 2].rearrange("p g r t -> p (g r t)").bitcast(F32).rearrange("p (g r u) -> p g r u", g=2, u=2)
+            copy(out=dst, in_=xt_tiles[(m, half)][:].rearrange("p (g u r) -> p g r u", g=2, u=2))
+
+        def x_quant(m):
             c = const.tile([P, PASSES * P], U32, name="xc_%d" % m, align_bytes=64)
             s = const.tile([P, PASSES * P], U8, name="xs_%d" % m, align_bytes=64)
-            nc.vector.quantize_mx(out=c[:].bitcast(FP8X4), scales=s[:], in_=xg[:].rearrange("p g r t -> p (g r t)"))
-            xc.append(c)
-            xs.append(s)
+            nc.vector.quantize_mx(out=c[:].bitcast(FP8X4), scales=s[:], in_=xg_tiles[m][:].rearrange("p g r t -> p (g r t)"))
+            xc[m] = c
+            xs[m] = s
 
-        def interleave(eng_copy, dst, src):
-            eng_copy(out=dst[:].rearrange("p (c i) t -> p c t i", i=4), in_=src[:].rearrange("p t (c i) -> p c t i", i=4))
+        wide_t = {}
+        il_t = {}
+        grouped = {}
+        ops = {}
 
-        def quantise(grouped, tagc, tags):
-            c = codes_pool.tile([P, NW], U32, name=tagc, tag=tagc, align_bytes=64)
-            s = codes_pool.tile([P, NW], U8, name=tags, tag=tags, align_bytes=64)
-            nc.vector.quantize_mx(out=c[:].bitcast(FP8X4), scales=s[:], in_=grouped[:].rearrange("p c t -> p (c t)"))
-            return c, s
+        def direct(copy, dst, src):
+            copy(out=dst[:].rearrange("p (c i) t -> p c t i", i=4), in_=src[:].rearrange("p t (c i) -> p c t i", i=4))
 
-        def prep_q(n, g):
-            wide = stage.tile([P, PACK, NW], BF16, name="wide", tag="wide")
+        def widen(n, g):
+            wide = stage.tile([P, PACK, NW], BF16, name="wide", tag="wide", bufs=4)
             for t in range(PACK):
                 nc.scalar.activation(out=wide[:, t, :], in_=wqb[(n, g)][:, t, :].bitcast(FP8), func=ACT.Copy, scale=sc[:, g, t:t + 1])
-            gq = stage.tile([P, NW, PACK], BF16, name="gq", tag="gq", align_bytes=64)
-            interleave(nc.scalar.copy, gq, wide)
-            return quantise(gq, "qc", "qs")
+            wide_t[(n, g)] = wide
 
-        def prep_k(n, g):
-            gk = stage.tile([P, NW, PACK], BF16, name="gk", tag="gk", align_bytes=64)
-            interleave(nc.vector.tensor_copy, gk, wkr[(n, g)])
-            return quantise(gk, "kc", "ks")
-
-        def project(ops, which, n):
-            for m in range(M_TILES):
-                acc = psum.tile([P, NW], F32, name="acc", tag="bank")
-                for g in range(PASSES):
-                    c, s = ops[g]
-                    nc.tensor.matmul_mx(
-                        out=acc[:],
-                        lhsT=xc[m][:, g * P:(g + 1) * P].bitcast(FP8X4),
-                        lhsT_scale=xs[m][:, g * P:(g + 1) * P],
-                        rhs=c[:].bitcast(FP8X4),
-                        rhs_scale=s[:],
-                        start=(g == 0),
-                        stop=(g == PASSES - 1),
+        def pe_interleave(n, g):
+            wide = wide_t[(n, g)]
+            banks = []
+            for b in range(2):
+                il = psum.tile([P, 2 * NW], BF16, name="il", tag="il")
+                for h in range(2):
+                    c0 = (2 * b + h) * P
+                    nc.tensor.matmul(
+                        out=il[:, h * NW:(h + 1) * NW].rearrange("p (c t) -> p c t", t=PACK),
+                        lhsT=ident_bf[:],
+                        rhs=wide[:, :, c0:c0 + P].rearrange("p t c -> p c t"),
+                        start=True,
+                        stop=True,
                     )
-                a4 = acc[:].rearrange("p (h i e) -> p h i e", h=HEADS_PER_CHUNK, e=2)
-                shape4 = [P, HEADS_PER_CHUNK, HALF, 2]
-                p1 = ep.tile([P, NW], F32, name="p1", tag="p1")
-                p2 = ep.tile([P, NW], F32, name="p2", tag="p2")
-                nc.vector.tensor_tensor(
-                    out=p1[:].rearrange("p (h i e) -> p h i e", h=HEADS_PER_CHUNK, e=2),
-                    in0=a4,
-                    in1=cosT[:, m].unsqueeze(1).to_broadcast(shape4),
-                    op=ALU.mult,
-                )
-                nc.vector.tensor_tensor(
-                    out=p2[:].rearrange("p (h i e) -> p h i e", h=HEADS_PER_CHUNK, e=2),
-                    in0=a4[:, :, :, ::-1],
-                    in1=sinT[:, m].unsqueeze(1).to_broadcast(shape4),
-                    op=ALU.mult,
-                )
-                nc.gpsimd.tensor_tensor(out=p1[:], in0=p1[:], in1=p2[:], op=ALU.add)
-                nc.sync.dma_start(out=outs_v[which][m][:, n * NW:(n + 1) * NW], in_=p1[:])
+                banks.append(il)
+            il_t[(n, g)] = banks
 
-        q_ops = [prep_q(0, g) for g in range(2)]
-        k_ops = [prep_k(0, g) for g in range(2)]
-        for m in range(M_TILES):
-            prep_x(m)
-        q_ops += [prep_q(0, g) for g in range(2, PASSES)]
-        k_ops += [prep_k(0, g) for g in range(2, PASSES)]
+        def new_gq(n, g):
+            grouped[("q", n, g)] = stage.tile([P, NW, PACK], BF16, name="gq", tag="gq", bufs=6, align_bytes=64)
+            return grouped[("q", n, g)]
+
+        def evac(n, g):
+            gq = new_gq(n, g)
+            flat = gq[:].rearrange("p c t -> p (c t)")
+            for b in range(2):
+                nc.scalar.copy(out=flat[:, b * 2 * NW:(b + 1) * 2 * NW], in_=il_t[(n, g)][b][:])
+
+        def q_direct(n, g):
+            copy = nc.vector.tensor_copy if n in Q_DIRECT_ON_VECTOR else nc.scalar.copy
+            direct(copy, new_gq(n, g), wide_t[(n, g)])
+
+        def k_interleave(n, g):
+            gk = stage.tile([P, NW, PACK], BF16, name="gk", tag="gk", bufs=GK_BUFS, align_bytes=64)
+            copy = nc.scalar.copy if (n, g) in K_ON_SCALAR else nc.vector.tensor_copy
+            direct(copy, gk, wkr[(n, g)])
+            grouped[("k", n, g)] = gk
+
+        def quant(w, n, g):
+            c = codes_pool.tile([P, NW], U32, name=w + "c", tag=w + "c", align_bytes=64)
+            s = codes_pool.tile([P, NW], U8, name=w + "s", tag=w + "s", align_bytes=64)
+            nc.vector.quantize_mx(out=c[:].bitcast(FP8X4), scales=s[:], in_=grouped[(w, n, g)][:].rearrange("p c t -> p (c t)"))
+            ops[(w, n, g)] = (c, s)
+
+        acc_t = {}
+        prod = {}
+        shape4 = [P, HEADS_PER_CHUNK, HALF, 2]
+
+        def as4(ap):
+            return ap.rearrange("p (h i e) -> p h i e", h=HEADS_PER_CHUNK, e=2)
+
+        def mm(w, n, m):
+            acc = psum.tile([P, NW], F32, name="acc", tag="acc")
+            for g in range(PASSES):
+                c, s = ops[(w, n, g)]
+                nc.tensor.matmul_mx(
+                    out=acc[:],
+                    lhsT=xc[m][:, g * P:(g + 1) * P].bitcast(FP8X4),
+                    lhsT_scale=xs[m][:, g * P:(g + 1) * P],
+                    rhs=c[:].bitcast(FP8X4),
+                    rhs_scale=s[:],
+                    start=(g == 0),
+                    stop=(g == PASSES - 1),
+                )
+            acc_t[(w, n, m)] = acc
+
+        def rot(w, n, m):
+            a4 = as4(acc_t[(w, n, m)][:])
+            p1 = ep.tile([P, NW], F32, name="p1", tag="p1")
+            p2 = ep.tile([P, NW], F32, name="p2", tag="p2")
+            nc.vector.tensor_tensor(out=as4(p1[:]), in0=a4, in1=cosT[:, m].unsqueeze(1).to_broadcast(shape4), op=ALU.mult)
+            nc.vector.tensor_tensor(out=as4(p2[:]), in0=a4[:, :, :, ::-1], in1=sinT[:, m].unsqueeze(1).to_broadcast(shape4), op=ALU.mult)
+            prod[(w, n, m)] = (p1, p2)
+
+        def add_store(eng, w, n, m):
+            p1, p2 = prod[(w, n, m)]
+            eng.tensor_tensor(out=p1[:], in0=p1[:], in1=p2[:], op=ALU.add)
+            nc.sync.dma_start(out=outs_v[w][m][:, n * NW:(n + 1) * NW], in_=p1[:])
+
+        chunks = []
         for n in range(CHUNKS):
-            if n > 0:
-                k_ops = [prep_k(n, g) for g in range(PASSES)]
-                q_ops = [prep_q(n, g) for g in range(PASSES)]
-            project(k_ops, 1, n)
-            project(q_ops, 0, n)
+            chunks.append(("k", n))
+            chunks.append(("q", n))
+
+        def seg_a(n):
+            evac(n, 0)
+            evac(n, 1)
+            widen(n, 2)
+            widen(n, 3)
+            q_direct(n, 3)
+
+        def seg_b(n):
+            evac(n, 2)
+            if n + 1 < CHUNKS:
+                widen(n + 1, 0)
+                widen(n + 1, 1)
+            for u in K_ON_SCALAR:
+                if u[0] == n + 1:
+                    k_interleave(u[0], u[1])
+
+        def k_on_vector(n, gs):
+            return [(n, g) for g in gs if n < CHUNKS and (n, g) not in K_ON_SCALAR]
+
+        vcopy = nc.vector.tensor_copy
+        widen(0, 0)
+        widen(0, 1)
+        pe_interleave(0, 0)
+        pe_interleave(0, 1)
+        widen(0, 2)
+        evac(0, 0)
+        pe_interleave(0, 2)
+        evac(0, 1)
+        widen(0, 3)
+        evac(0, 2)
+        q_direct(0, 3)
+        widen(1, 0)
+        widen(1, 1)
+        k_interleave(0, 0)
+        k_interleave(0, 1)
+        quant("k", 0, 0)
+        k_interleave(0, 2)
+        quant("k", 0, 1)
+        k_interleave(0, 3)
+        quant("k", 0, 2)
+        for u in K_ON_SCALAR:
+            if u[0] == 1:
+                k_interleave(u[0], u[1])
+        x_transpose(0)
+        x_transpose(1)
+        x_transpose(2)
+        x_evac(0, 0, vcopy)
+        x_evac(0, 1, vcopy)
+        x_transpose(3)
+        quant("k", 0, 3)
+        x_evac(1, 0, vcopy)
+        x_quant(0)
+        x_evac(1, 1, vcopy)
+        x_evac(2, 0, vcopy)
+        x_quant(1)
+        x_evac(2, 1, vcopy)
+        x_evac(3, 0, vcopy)
+        x_quant(2)
+        x_evac(3, 1, vcopy)
+        pend = k_on_vector(1, (0, 1))
+        k_interleave(pend[0][0], pend[0][1])
+        x_quant(3)
+        for u in pend[1:]:
+            k_interleave(u[0], u[1])
+        for m in range(M_TILES):
+            mm("k", 0, m)
+        pe_interleave(1, 0)
+        pe_interleave(1, 1)
+        deferred = [(seg_a, 1)]
+
+        for c in range(len(chunks)):
+            w, n = chunks[c]
+            nxt = chunks[c + 1] if c + 1 < len(chunks) else None
+            if nxt is not None:
+                for g in range(PASSES):
+                    quant(nxt[0], nxt[1], g)
+            for seg, j in deferred:
+                seg(j)
+            deferred.clear()
+            for m in range(M_TILES):
+                rot(w, n, m)
+                if nxt is not None:
+                    mm(nxt[0], nxt[1], m)
+                if m > 0:
+                    add_store(nc.gpsimd, w, n, m - 1)
+            if w == "k":
+                if n + 1 < CHUNKS:
+                    pe_interleave(n + 1, 2)
+                    deferred.append((seg_b, n + 1))
+                pend = k_on_vector(n + 1, (2, 3))
+            else:
+                if n + 2 < CHUNKS:
+                    pe_interleave(n + 2, 0)
+                    pe_interleave(n + 2, 1)
+                    deferred.append((seg_a, n + 2))
+                pend = k_on_vector(n + 2, (0, 1))
+            if pend:
+                k_interleave(pend[0][0], pend[0][1])
+            add_store(nc.vector, w, n, M_TILES - 1)
+            for u in pend[1:]:
+                k_interleave(u[0], u[1])
+            for u in late_loads[2 * c:2 * c + 2]:
+                load_wq(u[0], u[1])
+                load_wk(u[0], u[1])

@@ -27,10 +27,8 @@ HEADS_PER_CHUNK = NW // HD
 
 FLOPS = 2 * 2 * S * D * D
 
-GK_BUFS = 7
 PE_PATH_PASSES = 3
-K_ON_SCALAR = ((1, 3), (2, 2), (2, 3), (3, 3))
-Q_DIRECT_ON_VECTOR = ()
+K_ON_SCALAR = ((1, 2), (1, 3), (2, 2), (2, 3), (3, 2), (3, 3))
 
 
 def tile_attention_pa_kernel(tc, x, freqs_cos, freqs_sin, wq_bytes, wq_scale, wk, out_0, out_1):
@@ -38,19 +36,18 @@ def tile_attention_pa_kernel(tc, x, freqs_cos, freqs_sin, wq_bytes, wq_scale, wk
     x_v = x.rearrange("b (m p) k -> (b m) p k", p=P)
     wqb_v = wq_bytes.rearrange("(g p t) n -> g p t n", p=P, t=PACK)
     wk_v = wk.rearrange("(g p t) n -> g p t n", p=P, t=PACK)
-    outs_v = {
-        "q": out_0.rearrange("b (m p) h d -> (b m) p (h d)", p=P),
-        "k": out_1.rearrange("b (m p) h d -> (b m) p (h d)", p=P),
-    }
+    outs_v = [
+        out_0.rearrange("b (m p) h d -> (b m) p (h d)", p=P),
+        out_1.rearrange("b (m p) h d -> (b m) p (h d)", p=P),
+    ]
 
     with ExitStack() as ctx:
         const = ctx.enter_context(tc.tile_pool(name="const", bufs=1))
         raw = ctx.enter_context(tc.tile_pool(name="raw", bufs=1))
         stage = ctx.enter_context(tc.tile_pool(name="stage", bufs=3))
-        codes_pool = ctx.enter_context(tc.tile_pool(name="codes", bufs=4))
+        codes_pool = ctx.enter_context(tc.tile_pool(name="codes", bufs=8))
         ep = ctx.enter_context(tc.tile_pool(name="ep", bufs=4))
-        psum = ctx.enter_context(tc.psum_pool(name="psum", bufs=4))
-        ctx.enter_context(tc.manual_schedule())
+        psum = ctx.enter_context(tc.psum_pool(name="psum", bufs=8))
 
         sc = const.tile([P, PASSES, PACK], F32, name="sc")
         nc.scalar.dma_start(out=sc[:], in_=wq_scale.rearrange("(g p t) o -> p g (t o)", p=P, t=PACK))
@@ -59,22 +56,15 @@ def tile_attention_pa_kernel(tc, x, freqs_cos, freqs_sin, wq_bytes, wq_scale, wk
         sin_sb = const.tile([P, M_TILES, HALF], BF16, name="sin_sb")
         nc.scalar.dma_start(out=sin_sb[:], in_=freqs_sin.rearrange("(m p) i -> p m i", p=P))
 
-        warm = const.tile([P, 2], F32, name="warm")
-        nc.vector.memset(warm[:, 0:1], 0.0)
-        nc.scalar.activation(out=warm[:, 1:2], in_=warm[:, 0:1], func=ACT.Copy)
-
         wqb = {}
         wkr = {}
         xr = []
 
-        def load_wq(n, g):
+        def load_w(n, g):
             cols = slice(n * NW, (n + 1) * NW)
             tq = raw.tile([P, PACK, NW], U8, name="wqb_%d_%d" % (n, g))
             nc.sync.dma_start(out=tq[:], in_=wqb_v[g][:, :, cols])
             wqb[(n, g)] = tq
-
-        def load_wk(n, g):
-            cols = slice(n * NW, (n + 1) * NW)
             tk = raw.tile([P, PACK, NW], BF16, name="wkr_%d_%d" % (n, g))
             nc.sync.dma_start(out=tk[:], in_=wk_v[g][:, :, cols])
             wkr[(n, g)] = tk
@@ -84,23 +74,17 @@ def tile_attention_pa_kernel(tc, x, freqs_cos, freqs_sin, wq_bytes, wq_scale, wk
             nc.sync.dma_start(out=t[:], in_=x_v[m])
             xr.append(t)
 
-        load_wq(0, 0)
-        load_wk(0, 0)
-        load_wq(0, 1)
-        load_wk(0, 1)
-        load_wq(0, 2)
-        load_wk(0, 2)
-        load_wk(0, 3)
+        load_w(0, 0)
+        load_w(0, 1)
         load_x(0)
-        load_wq(0, 3)
         load_x(1)
+        load_w(0, 2)
         load_x(2)
         load_x(3)
-        for n in range(1, CHUNKS - 1):
+        load_w(0, 3)
+        for n in range(1, CHUNKS):
             for g in range(PASSES):
-                load_wq(n, g)
-                load_wk(n, g)
-        late_loads = [(CHUNKS - 1, g) for g in range(PASSES)]
+                load_w(n, g)
 
         ident = const.tile([P, P], F32, name="ident")
         make_identity(nc, ident[:])
@@ -109,238 +93,114 @@ def tile_attention_pa_kernel(tc, x, freqs_cos, freqs_sin, wq_bytes, wq_scale, wk
         cosT = const.tile([P, M_TILES, HALF, 2], F32, name="cosT")
         sinT = const.tile([P, M_TILES, HALF, 2], F32, name="sinT")
         for e in range(2):
-            nc.vector.tensor_copy(out=cosT[:, :, :, e], in_=cos_sb[:])
-        nc.vector.tensor_scalar(out=sinT[:, :, :, 0], in0=sin_sb[:], scalar1=-1.0, scalar2=None, op0=ALU.mult)
-        nc.vector.tensor_copy(out=sinT[:, :, :, 1], in_=sin_sb[:])
+            nc.gpsimd.tensor_copy(out=cosT[:, :, :, e], in_=cos_sb[:])
+        nc.gpsimd.tensor_scalar(out=sinT[:, :, :, 0], in0=sin_sb[:], scalar1=-1.0, scalar2=0.0, op0=ALU.mult, op1=ALU.add)
+        nc.gpsimd.tensor_copy(out=sinT[:, :, :, 1], in_=sin_sb[:])
 
-        xt_tiles = {}
-        xg_tiles = {}
-        xc = {}
-        xs = {}
+        xc = []
+        xs = []
 
-        def x_transpose(m):
+        def prep_x(m):
             words = xr[m][:].bitcast(F32)
+            xg = stage.tile([P, PASSES, P, PACK], BF16, name="xg", tag="xg", align_bytes=64)
             for half in range(2):
-                xt = psum.tile([P, NW], F32, name="xt", tag=("il" if m == 2 else "acc"))
+                xt = psum.tile([P, NW], F32, name="xt", tag="bank")
                 for gl in range(2):
                     g = 2 * half + gl
                     for u in range(2):
                         j = 2 * gl + u
                         nc.tensor.transpose(xt[:, j * P:(j + 1) * P], words[:, 256 * g + u:256 * (g + 1):2], ident[:])
-                xt_tiles[(m, half)] = xt
-
-        def x_evac(m, half, copy):
-            if half == 0:
-                xg_tiles[m] = stage.tile([P, PASSES, P, PACK], BF16, name="xg", tag="gk", bufs=GK_BUFS, align_bytes=64)
-            xg = xg_tiles[m]
-            dst = xg[:, 2 * half:2 * half + 2].rearrange("p g r t -> p (g r t)").bitcast(F32).rearrange("p (g r u) -> p g r u", g=2, u=2)
-            copy(out=dst, in_=xt_tiles[(m, half)][:].rearrange("p (g u r) -> p g r u", g=2, u=2))
-
-        def x_quant(m):
+                dst = xg[:, 2 * half:2 * half + 2].rearrange("p g r t -> p (g r t)").bitcast(F32).rearrange("p (g r u) -> p g r u", g=2, u=2)
+                src = xt[:].rearrange("p (g u r) -> p g r u", g=2, u=2)
+                if half == 0:
+                    nc.vector.tensor_copy(out=dst, in_=src)
+                else:
+                    nc.scalar.copy(out=dst, in_=src)
             c = const.tile([P, PASSES * P], U32, name="xc_%d" % m, align_bytes=64)
             s = const.tile([P, PASSES * P], U8, name="xs_%d" % m, align_bytes=64)
-            nc.vector.quantize_mx(out=c[:].bitcast(FP8X4), scales=s[:], in_=xg_tiles[m][:].rearrange("p g r t -> p (g r t)"))
-            xc[m] = c
-            xs[m] = s
+            nc.vector.quantize_mx(out=c[:].bitcast(FP8X4), scales=s[:], in_=xg[:].rearrange("p g r t -> p (g r t)"))
+            xc.append(c)
+            xs.append(s)
 
-        wide_t = {}
-        il_t = {}
-        grouped = {}
-        ops = {}
+        def interleave(eng_copy, dst, src):
+            eng_copy(out=dst[:].rearrange("p (c i) t -> p c t i", i=4), in_=src[:].rearrange("p t (c i) -> p c t i", i=4))
 
-        def direct(copy, dst, src):
-            copy(out=dst[:].rearrange("p (c i) t -> p c t i", i=4), in_=src[:].rearrange("p t (c i) -> p c t i", i=4))
+        def quantise(grouped, tagc, tags):
+            c = codes_pool.tile([P, NW], U32, name=tagc, tag=tagc, align_bytes=64)
+            s = codes_pool.tile([P, NW], U8, name=tags, tag=tags, align_bytes=64)
+            nc.vector.quantize_mx(out=c[:].bitcast(FP8X4), scales=s[:], in_=grouped[:].rearrange("p c t -> p (c t)"))
+            return c, s
 
-        def widen(n, g):
-            wide = stage.tile([P, PACK, NW], BF16, name="wide", tag="wide", bufs=4)
+        def prep_q(n, g):
+            wide = stage.tile([P, PACK, NW], BF16, name="wide", tag="wide")
             for t in range(PACK):
                 nc.scalar.activation(out=wide[:, t, :], in_=wqb[(n, g)][:, t, :].bitcast(FP8), func=ACT.Copy, scale=sc[:, g, t:t + 1])
-            wide_t[(n, g)] = wide
-
-        def pe_interleave(n, g):
-            wide = wide_t[(n, g)]
-            banks = []
-            for b in range(2):
-                il = psum.tile([P, 2 * NW], BF16, name="il", tag="il")
-                for h in range(2):
-                    c0 = (2 * b + h) * P
-                    nc.tensor.matmul(
-                        out=il[:, h * NW:(h + 1) * NW].rearrange("p (c t) -> p c t", t=PACK),
-                        lhsT=ident_bf[:],
-                        rhs=wide[:, :, c0:c0 + P].rearrange("p t c -> p c t"),
-                        start=True,
-                        stop=True,
-                    )
-                banks.append(il)
-            il_t[(n, g)] = banks
-
-        def new_gq(n, g):
-            grouped[("q", n, g)] = stage.tile([P, NW, PACK], BF16, name="gq", tag="gq", bufs=6, align_bytes=64)
-            return grouped[("q", n, g)]
-
-        def evac(n, g):
-            gq = new_gq(n, g)
-            flat = gq[:].rearrange("p c t -> p (c t)")
-            for b in range(2):
-                nc.scalar.copy(out=flat[:, b * 2 * NW:(b + 1) * 2 * NW], in_=il_t[(n, g)][b][:])
-
-        def q_direct(n, g):
-            copy = nc.vector.tensor_copy if n in Q_DIRECT_ON_VECTOR else nc.scalar.copy
-            direct(copy, new_gq(n, g), wide_t[(n, g)])
-
-        def k_interleave(n, g):
-            gk = stage.tile([P, NW, PACK], BF16, name="gk", tag="gk", bufs=GK_BUFS, align_bytes=64)
-            copy = nc.scalar.copy if (n, g) in K_ON_SCALAR else nc.vector.tensor_copy
-            direct(copy, gk, wkr[(n, g)])
-            grouped[("k", n, g)] = gk
-
-        def quant(w, n, g):
-            c = codes_pool.tile([P, NW], U32, name=w + "c", tag=w + "c", align_bytes=64)
-            s = codes_pool.tile([P, NW], U8, name=w + "s", tag=w + "s", align_bytes=64)
-            nc.vector.quantize_mx(out=c[:].bitcast(FP8X4), scales=s[:], in_=grouped[(w, n, g)][:].rearrange("p c t -> p (c t)"))
-            ops[(w, n, g)] = (c, s)
-
-        acc_t = {}
-        prod = {}
-        shape4 = [P, HEADS_PER_CHUNK, HALF, 2]
-
-        def as4(ap):
-            return ap.rearrange("p (h i e) -> p h i e", h=HEADS_PER_CHUNK, e=2)
-
-        def mm(w, n, m):
-            acc = psum.tile([P, NW], F32, name="acc", tag="acc")
-            for g in range(PASSES):
-                c, s = ops[(w, n, g)]
-                nc.tensor.matmul_mx(
-                    out=acc[:],
-                    lhsT=xc[m][:, g * P:(g + 1) * P].bitcast(FP8X4),
-                    lhsT_scale=xs[m][:, g * P:(g + 1) * P],
-                    rhs=c[:].bitcast(FP8X4),
-                    rhs_scale=s[:],
-                    start=(g == 0),
-                    stop=(g == PASSES - 1),
-                )
-            acc_t[(w, n, m)] = acc
-
-        def rot(w, n, m):
-            a4 = as4(acc_t[(w, n, m)][:])
-            p1 = ep.tile([P, NW], F32, name="p1", tag="p1")
-            p2 = ep.tile([P, NW], F32, name="p2", tag="p2")
-            nc.vector.tensor_tensor(out=as4(p1[:]), in0=a4, in1=cosT[:, m].unsqueeze(1).to_broadcast(shape4), op=ALU.mult)
-            nc.vector.tensor_tensor(out=as4(p2[:]), in0=a4[:, :, :, ::-1], in1=sinT[:, m].unsqueeze(1).to_broadcast(shape4), op=ALU.mult)
-            prod[(w, n, m)] = (p1, p2)
-
-        def add_store(eng, w, n, m):
-            p1, p2 = prod[(w, n, m)]
-            eng.tensor_tensor(out=p1[:], in0=p1[:], in1=p2[:], op=ALU.add)
-            nc.sync.dma_start(out=outs_v[w][m][:, n * NW:(n + 1) * NW], in_=p1[:])
-
-        chunks = []
-        for n in range(CHUNKS):
-            chunks.append(("k", n))
-            chunks.append(("q", n))
-
-        def seg_a(n):
-            evac(n, 0)
-            evac(n, 1)
-            widen(n, 2)
-            widen(n, 3)
-            q_direct(n, 3)
-
-        def seg_b(n):
-            evac(n, 2)
-            if n + 1 < CHUNKS:
-                widen(n + 1, 0)
-                widen(n + 1, 1)
-            for u in K_ON_SCALAR:
-                if u[0] == n + 1:
-                    k_interleave(u[0], u[1])
-
-        def k_on_vector(n, gs):
-            return [(n, g) for g in gs if n < CHUNKS and (n, g) not in K_ON_SCALAR]
-
-        vcopy = nc.vector.tensor_copy
-        widen(0, 0)
-        widen(0, 1)
-        pe_interleave(0, 0)
-        pe_interleave(0, 1)
-        widen(0, 2)
-        evac(0, 0)
-        pe_interleave(0, 2)
-        evac(0, 1)
-        widen(0, 3)
-        evac(0, 2)
-        q_direct(0, 3)
-        widen(1, 0)
-        widen(1, 1)
-        k_interleave(0, 0)
-        k_interleave(0, 1)
-        quant("k", 0, 0)
-        k_interleave(0, 2)
-        quant("k", 0, 1)
-        k_interleave(0, 3)
-        quant("k", 0, 2)
-        for u in K_ON_SCALAR:
-            if u[0] == 1:
-                k_interleave(u[0], u[1])
-        x_transpose(0)
-        x_transpose(1)
-        x_transpose(2)
-        x_evac(0, 0, vcopy)
-        x_evac(0, 1, vcopy)
-        x_transpose(3)
-        quant("k", 0, 3)
-        x_evac(1, 0, vcopy)
-        x_quant(0)
-        x_evac(1, 1, vcopy)
-        x_evac(2, 0, vcopy)
-        x_quant(1)
-        x_evac(2, 1, vcopy)
-        x_evac(3, 0, vcopy)
-        x_quant(2)
-        x_evac(3, 1, vcopy)
-        pend = k_on_vector(1, (0, 1))
-        k_interleave(pend[0][0], pend[0][1])
-        x_quant(3)
-        for u in pend[1:]:
-            k_interleave(u[0], u[1])
-        for m in range(M_TILES):
-            mm("k", 0, m)
-        pe_interleave(1, 0)
-        pe_interleave(1, 1)
-        deferred = [(seg_a, 1)]
-
-        for c in range(len(chunks)):
-            w, n = chunks[c]
-            nxt = chunks[c + 1] if c + 1 < len(chunks) else None
-            if nxt is not None:
-                for g in range(PASSES):
-                    quant(nxt[0], nxt[1], g)
-            for seg, j in deferred:
-                seg(j)
-            deferred.clear()
-            for m in range(M_TILES):
-                rot(w, n, m)
-                if nxt is not None:
-                    mm(nxt[0], nxt[1], m)
-                if m > 0:
-                    add_store(nc.gpsimd, w, n, m - 1)
-            if w == "k":
-                if n + 1 < CHUNKS:
-                    pe_interleave(n + 1, 2)
-                    deferred.append((seg_b, n + 1))
-                pend = k_on_vector(n + 1, (2, 3))
+            gq = stage.tile([P, NW, PACK], BF16, name="gq", tag="gq", align_bytes=64)
+            if g < PE_PATH_PASSES:
+                flat = gq[:].rearrange("p c t -> p (c t)")
+                for b in range(2):
+                    il = psum.tile([P, 2 * NW], BF16, name="il", tag="bank")
+                    for h in range(2):
+                        c0 = (2 * b + h) * P
+                        nc.tensor.matmul(
+                            out=il[:, h * NW:(h + 1) * NW].rearrange("p (c t) -> p c t", t=PACK),
+                            lhsT=ident_bf[:],
+                            rhs=wide[:, :, c0:c0 + P].rearrange("p t c -> p c t"),
+                            start=True,
+                            stop=True,
+                        )
+                    nc.scalar.copy(out=flat[:, b * 2 * NW:(b + 1) * 2 * NW], in_=il[:])
             else:
-                if n + 2 < CHUNKS:
-                    pe_interleave(n + 2, 0)
-                    pe_interleave(n + 2, 1)
-                    deferred.append((seg_a, n + 2))
-                pend = k_on_vector(n + 2, (0, 1))
-            if pend:
-                k_interleave(pend[0][0], pend[0][1])
-            add_store(nc.vector, w, n, M_TILES - 1)
-            for u in pend[1:]:
-                k_interleave(u[0], u[1])
-            for u in late_loads[2 * c:2 * c + 2]:
-                load_wq(u[0], u[1])
-                load_wk(u[0], u[1])
+                interleave(nc.scalar.copy, gq, wide)
+            return quantise(gq, "qc", "qs")
+
+        def prep_k(n, g):
+            gk = stage.tile([P, NW, PACK], BF16, name="gk", tag="gk", align_bytes=64)
+            interleave(nc.scalar.copy if (n, g) in K_ON_SCALAR else nc.vector.tensor_copy, gk, wkr[(n, g)])
+            return quantise(gk, "kc", "ks")
+
+        def project(ops, which, n):
+            for m in range(M_TILES):
+                acc = psum.tile([P, NW], F32, name="acc", tag="bank")
+                for g in range(PASSES):
+                    c, s = ops[g]
+                    nc.tensor.matmul_mx(
+                        out=acc[:],
+                        lhsT=xc[m][:, g * P:(g + 1) * P].bitcast(FP8X4),
+                        lhsT_scale=xs[m][:, g * P:(g + 1) * P],
+                        rhs=c[:].bitcast(FP8X4),
+                        rhs_scale=s[:],
+                        start=(g == 0),
+                        stop=(g == PASSES - 1),
+                    )
+                a4 = acc[:].rearrange("p (h i e) -> p h i e", h=HEADS_PER_CHUNK, e=2)
+                shape4 = [P, HEADS_PER_CHUNK, HALF, 2]
+                p1 = ep.tile([P, NW], F32, name="p1", tag="p1")
+                p2 = ep.tile([P, NW], F32, name="p2", tag="p2")
+                nc.vector.tensor_tensor(
+                    out=p1[:].rearrange("p (h i e) -> p h i e", h=HEADS_PER_CHUNK, e=2),
+                    in0=a4,
+                    in1=cosT[:, m].unsqueeze(1).to_broadcast(shape4),
+                    op=ALU.mult,
+                )
+                nc.vector.tensor_tensor(
+                    out=p2[:].rearrange("p (h i e) -> p h i e", h=HEADS_PER_CHUNK, e=2),
+                    in0=a4[:, :, :, ::-1],
+                    in1=sinT[:, m].unsqueeze(1).to_broadcast(shape4),
+                    op=ALU.mult,
+                )
+                nc.gpsimd.tensor_tensor(out=p1[:], in0=p1[:], in1=p2[:], op=ALU.add)
+                nc.sync.dma_start(out=outs_v[which][m][:, n * NW:(n + 1) * NW], in_=p1[:])
+
+        q_ops = [prep_q(0, g) for g in range(2)]
+        k_ops = [prep_k(0, g) for g in range(2)]
+        for m in range(M_TILES):
+            prep_x(m)
+        q_ops += [prep_q(0, g) for g in range(2, PASSES)]
+        k_ops += [prep_k(0, g) for g in range(2, PASSES)]
+        for n in range(CHUNKS):
+            if n > 0:
+                k_ops = [prep_k(n, g) for g in range(PASSES)]
+                q_ops = [prep_q(n, g) for g in range(PASSES)]
+            project(k_ops, 1, n)
+            project(q_ops, 0, n)

@@ -27,8 +27,13 @@ HEADS_PER_CHUNK = NW // HD
 
 FLOPS = 2 * 2 * S * D * D
 
+GK_BUFS = 7
+RAW_BUFS = 12
 PE_PATH_PASSES = 3
-K_ON_SCALAR = ((1, 2), (1, 3), (2, 2), (2, 3), (3, 2), (3, 3))
+K_ON_SCALAR = ((1, 3), (2, 2), (2, 3), (3, 3))
+Q_DIRECT_ON_VECTOR = ()
+X_EVAC_ON_SCALAR = ()
+LAST_CHUNK = ("q", CHUNKS - 1)
 
 
 def tile_attention_pa_kernel(tc, x, freqs_cos, freqs_sin, wq_bytes, wq_scale, wk, out_0, out_1):
@@ -36,18 +41,24 @@ def tile_attention_pa_kernel(tc, x, freqs_cos, freqs_sin, wq_bytes, wq_scale, wk
     x_v = x.rearrange("b (m p) k -> (b m) p k", p=P)
     wqb_v = wq_bytes.rearrange("(g p t) n -> g p t n", p=P, t=PACK)
     wk_v = wk.rearrange("(g p t) n -> g p t n", p=P, t=PACK)
-    outs_v = [
-        out_0.rearrange("b (m p) h d -> (b m) p (h d)", p=P),
-        out_1.rearrange("b (m p) h d -> (b m) p (h d)", p=P),
-    ]
+    outs_v = {
+        "q": out_0.rearrange("b (m p) h d -> (b m) p (h d)", p=P),
+        "k": out_1.rearrange("b (m p) h d -> (b m) p (h d)", p=P),
+    }
+
+    outs_3d = {
+        "q": out_0.rearrange("b (m p) h d -> p (b m) (h d)", p=P),
+        "k": out_1.rearrange("b (m p) h d -> p (b m) (h d)", p=P),
+    }
 
     with ExitStack() as ctx:
         const = ctx.enter_context(tc.tile_pool(name="const", bufs=1))
         raw = ctx.enter_context(tc.tile_pool(name="raw", bufs=1))
         stage = ctx.enter_context(tc.tile_pool(name="stage", bufs=3))
-        codes_pool = ctx.enter_context(tc.tile_pool(name="codes", bufs=8))
-        ep = ctx.enter_context(tc.tile_pool(name="ep", bufs=4))
-        psum = ctx.enter_context(tc.psum_pool(name="psum", bufs=8))
+        codes_pool = ctx.enter_context(tc.tile_pool(name="codes", bufs=4))
+        big = ctx.enter_context(tc.tile_pool(name="big", bufs=6))
+        psum = ctx.enter_context(tc.psum_pool(name="psum", bufs=4))
+        ctx.enter_context(tc.manual_schedule())
 
         sc = const.tile([P, PASSES, PACK], F32, name="sc")
         nc.scalar.dma_start(out=sc[:], in_=wq_scale.rearrange("(g p t) o -> p g (t o)", p=P, t=PACK))
@@ -56,35 +67,50 @@ def tile_attention_pa_kernel(tc, x, freqs_cos, freqs_sin, wq_bytes, wq_scale, wk
         sin_sb = const.tile([P, M_TILES, HALF], BF16, name="sin_sb")
         nc.scalar.dma_start(out=sin_sb[:], in_=freqs_sin.rearrange("(m p) i -> p m i", p=P))
 
+        warm = const.tile([P, 2], F32, name="warm")
+        nc.vector.memset(warm[:, 0:1], 0.0)
+        nc.scalar.activation(out=warm[:, 1:2], in_=warm[:, 0:1], func=ACT.Copy)
+
+        junk = const.tile([P, 1], U32, name="junk")
+
         wqb = {}
         wkr = {}
         xr = []
 
-        def load_w(n, g):
+        def load_wq(n, g):
             cols = slice(n * NW, (n + 1) * NW)
-            tq = raw.tile([P, PACK, NW], U8, name="wqb_%d_%d" % (n, g))
+            tq = raw.tile([P, PACK, NW], U8, name="wqb", tag="wqb", bufs=RAW_BUFS)
             nc.sync.dma_start(out=tq[:], in_=wqb_v[g][:, :, cols])
             wqb[(n, g)] = tq
-            tk = raw.tile([P, PACK, NW], BF16, name="wkr_%d_%d" % (n, g))
+
+        def load_wk(n, g):
+            cols = slice(n * NW, (n + 1) * NW)
+            tk = raw.tile([P, PACK, NW], BF16, name="wkr", tag="wkr", bufs=RAW_BUFS)
             nc.sync.dma_start(out=tk[:], in_=wk_v[g][:, :, cols])
             wkr[(n, g)] = tk
 
         def load_x(m):
-            t = raw.tile([P, D], BF16, name="xr_%d" % m)
+            t = big.tile([P, D], BF16, name="xr", tag="big")
             nc.sync.dma_start(out=t[:], in_=x_v[m])
             xr.append(t)
 
-        load_w(0, 0)
-        load_w(0, 1)
+        load_wq(0, 0)
+        load_wk(0, 0)
+        load_wq(0, 1)
+        load_wk(0, 1)
+        load_wq(0, 2)
+        load_wk(0, 2)
+        load_wk(0, 3)
         load_x(0)
+        load_wq(0, 3)
         load_x(1)
-        load_w(0, 2)
         load_x(2)
         load_x(3)
-        load_w(0, 3)
-        for n in range(1, CHUNKS):
+        for n in range(1, CHUNKS - 1):
             for g in range(PASSES):
-                load_w(n, g)
+                load_wk(n, g)
+                load_wq(n, g)
+        late_loads = [(CHUNKS - 1, g) for g in range(PASSES)]
 
         ident = const.tile([P, P], F32, name="ident")
         make_identity(nc, ident[:])
@@ -93,114 +119,283 @@ def tile_attention_pa_kernel(tc, x, freqs_cos, freqs_sin, wq_bytes, wq_scale, wk
         cosT = const.tile([P, M_TILES, HALF, 2], F32, name="cosT")
         sinT = const.tile([P, M_TILES, HALF, 2], F32, name="sinT")
         for e in range(2):
-            nc.gpsimd.tensor_copy(out=cosT[:, :, :, e], in_=cos_sb[:])
-        nc.gpsimd.tensor_scalar(out=sinT[:, :, :, 0], in0=sin_sb[:], scalar1=-1.0, scalar2=0.0, op0=ALU.mult, op1=ALU.add)
-        nc.gpsimd.tensor_copy(out=sinT[:, :, :, 1], in_=sin_sb[:])
+            nc.vector.tensor_copy(out=cosT[:, :, :, e], in_=cos_sb[:])
+        nc.vector.tensor_scalar(out=sinT[:, :, :, 0], in0=sin_sb[:], scalar1=-1.0, scalar2=None, op0=ALU.mult)
+        nc.vector.tensor_copy(out=sinT[:, :, :, 1], in_=sin_sb[:])
 
-        xc = []
-        xs = []
+        xt_tiles = {}
+        xg_tiles = {}
+        xc = {}
+        xs = {}
 
-        def prep_x(m):
+        def x_transpose(m):
             words = xr[m][:].bitcast(F32)
-            xg = stage.tile([P, PASSES, P, PACK], BF16, name="xg", tag="xg", align_bytes=64)
             for half in range(2):
-                xt = psum.tile([P, NW], F32, name="xt", tag="bank")
+                xt = psum.tile([P, NW], F32, name="xt", tag=("il" if m == 2 else "acc"))
                 for gl in range(2):
                     g = 2 * half + gl
                     for u in range(2):
                         j = 2 * gl + u
                         nc.tensor.transpose(xt[:, j * P:(j + 1) * P], words[:, 256 * g + u:256 * (g + 1):2], ident[:])
-                dst = xg[:, 2 * half:2 * half + 2].rearrange("p g r t -> p (g r t)").bitcast(F32).rearrange("p (g r u) -> p g r u", g=2, u=2)
-                src = xt[:].rearrange("p (g u r) -> p g r u", g=2, u=2)
-                if half == 0:
-                    nc.vector.tensor_copy(out=dst, in_=src)
-                else:
-                    nc.scalar.copy(out=dst, in_=src)
+                xt_tiles[(m, half)] = xt
+
+        def x_evac(m, half, copy):
+            if half == 0:
+                xg_tiles[m] = stage.tile([P, PASSES, P, PACK], BF16, name="xg", tag="gk", bufs=GK_BUFS, align_bytes=64)
+            xg = xg_tiles[m]
+            dst = xg[:, 2 * half:2 * half + 2].rearrange("p g r t -> p (g r t)").bitcast(F32).rearrange("p (g r u) -> p g r u", g=2, u=2)
+            copy(out=dst, in_=xt_tiles[(m, half)][:].rearrange("p (g u r) -> p g r u", g=2, u=2))
+
+        def x_quant(m):
             c = const.tile([P, PASSES * P], U32, name="xc_%d" % m, align_bytes=64)
             s = const.tile([P, PASSES * P], U8, name="xs_%d" % m, align_bytes=64)
-            nc.vector.quantize_mx(out=c[:].bitcast(FP8X4), scales=s[:], in_=xg[:].rearrange("p g r t -> p (g r t)"))
-            xc.append(c)
-            xs.append(s)
+            nc.vector.quantize_mx(out=c[:].bitcast(FP8X4), scales=s[:], in_=xg_tiles[m][:].rearrange("p g r t -> p (g r t)"))
+            xc[m] = c
+            xs[m] = s
 
-        def interleave(eng_copy, dst, src):
-            eng_copy(out=dst[:].rearrange("p (c i) t -> p c t i", i=4), in_=src[:].rearrange("p t (c i) -> p c t i", i=4))
+        wide_t = {}
+        il_t = {}
+        grouped = {}
+        ops = {}
 
-        def quantise(grouped, tagc, tags):
-            c = codes_pool.tile([P, NW], U32, name=tagc, tag=tagc, align_bytes=64)
-            s = codes_pool.tile([P, NW], U8, name=tags, tag=tags, align_bytes=64)
-            nc.vector.quantize_mx(out=c[:].bitcast(FP8X4), scales=s[:], in_=grouped[:].rearrange("p c t -> p (c t)"))
-            return c, s
+        def direct(copy, dst, src):
+            copy(out=dst[:].rearrange("p (c i) t -> p c t i", i=4), in_=src[:].rearrange("p t (c i) -> p c t i", i=4))
 
-        def prep_q(n, g):
-            wide = stage.tile([P, PACK, NW], BF16, name="wide", tag="wide")
+        def widen(n, g):
+            wide = stage.tile([P, PACK, NW], BF16, name="wide", tag="wide", bufs=4)
             for t in range(PACK):
                 nc.scalar.activation(out=wide[:, t, :], in_=wqb[(n, g)][:, t, :].bitcast(FP8), func=ACT.Copy, scale=sc[:, g, t:t + 1])
-            gq = stage.tile([P, NW, PACK], BF16, name="gq", tag="gq", align_bytes=64)
-            if g < PE_PATH_PASSES:
-                flat = gq[:].rearrange("p c t -> p (c t)")
-                for b in range(2):
-                    il = psum.tile([P, 2 * NW], BF16, name="il", tag="bank")
-                    for h in range(2):
-                        c0 = (2 * b + h) * P
-                        nc.tensor.matmul(
-                            out=il[:, h * NW:(h + 1) * NW].rearrange("p (c t) -> p c t", t=PACK),
-                            lhsT=ident_bf[:],
-                            rhs=wide[:, :, c0:c0 + P].rearrange("p t c -> p c t"),
-                            start=True,
-                            stop=True,
-                        )
-                    nc.scalar.copy(out=flat[:, b * 2 * NW:(b + 1) * 2 * NW], in_=il[:])
-            else:
-                interleave(nc.scalar.copy, gq, wide)
-            return quantise(gq, "qc", "qs")
+            wide_t[(n, g)] = wide
 
-        def prep_k(n, g):
-            gk = stage.tile([P, NW, PACK], BF16, name="gk", tag="gk", align_bytes=64)
-            interleave(nc.scalar.copy if (n, g) in K_ON_SCALAR else nc.vector.tensor_copy, gk, wkr[(n, g)])
-            return quantise(gk, "kc", "ks")
+        def pe_interleave(n, g):
+            wide = wide_t[(n, g)]
+            banks = []
+            for b in range(2):
+                il = psum.tile([P, 2 * NW], BF16, name="il", tag="il")
+                for h in range(2):
+                    c0 = (2 * b + h) * P
+                    nc.tensor.matmul(
+                        out=il[:, h * NW:(h + 1) * NW].rearrange("p (c i t) -> p c t i", i=4, t=PACK),
+                        lhsT=ident_bf[:],
+                        rhs=wide[:, :, c0:c0 + P].rearrange("p t (c i) -> p c t i", i=4),
+                        start=True,
+                        stop=True,
+                    )
+                banks.append(il)
+            il_t[(n, g)] = banks
 
-        def project(ops, which, n):
-            for m in range(M_TILES):
-                acc = psum.tile([P, NW], F32, name="acc", tag="bank")
-                for g in range(PASSES):
-                    c, s = ops[g]
+        def new_gq(n, g):
+            grouped[("q", n, g)] = stage.tile([P, NW, PACK], BF16, name="gq", tag="gq", bufs=6, align_bytes=64)
+            return grouped[("q", n, g)]
+
+        def evac(n, g):
+            gq = new_gq(n, g)
+            flat = gq[:].rearrange("p c t -> p (c t)")
+            for b in range(2):
+                nc.scalar.copy(out=flat[:, b * 2 * NW:(b + 1) * 2 * NW], in_=il_t[(n, g)][b][:])
+
+        def q_direct(n, g):
+            copy = nc.vector.tensor_copy if n in Q_DIRECT_ON_VECTOR else nc.scalar.copy
+            direct(copy, new_gq(n, g), wide_t[(n, g)])
+
+        def k_interleave(n, g):
+            gk = stage.tile([P, NW, PACK], BF16, name="gk", tag="gk", bufs=GK_BUFS, align_bytes=64)
+            copy = nc.scalar.copy if (n, g) in K_ON_SCALAR else nc.vector.tensor_copy
+            direct(copy, gk, wkr[(n, g)])
+            grouped[("k", n, g)] = gk
+
+        def quant(w, n, g):
+            c = codes_pool.tile([P, NW], U32, name=w + "c", tag=w + "c", align_bytes=64)
+            s = codes_pool.tile([P, NW], U8, name=w + "s", tag=w + "s", align_bytes=64)
+            nc.vector.quantize_mx(out=c[:].bitcast(FP8X4), scales=s[:], in_=grouped[(w, n, g)][:].rearrange("p c t -> p (c t)"))
+            ops[(w, n, g)] = (c, s)
+
+        acc_t = {}
+        prod = {}
+        shape4 = [P, HEADS_PER_CHUNK, HALF, 2]
+
+        def as4(ap):
+            return ap.rearrange("p (h i e) -> p h i e", h=HEADS_PER_CHUNK, e=2)
+
+        def mm_last(gs, first, final):
+            w, n = LAST_CHUNK
+            for g in gs:
+                c, s = ops[(w, n, g)]
+                for m in range(M_TILES):
+                    if (w, n, m) not in acc_t:
+                        acc_t[(w, n, m)] = psum.tile([P, NW], F32, name="accl", tag="il")
                     nc.tensor.matmul_mx(
-                        out=acc[:],
+                        out=acc_t[(w, n, m)][:],
                         lhsT=xc[m][:, g * P:(g + 1) * P].bitcast(FP8X4),
                         lhsT_scale=xs[m][:, g * P:(g + 1) * P],
                         rhs=c[:].bitcast(FP8X4),
                         rhs_scale=s[:],
-                        start=(g == 0),
-                        stop=(g == PASSES - 1),
+                        start=(first and g == gs[0]),
+                        stop=final,
                     )
-                a4 = acc[:].rearrange("p (h i e) -> p h i e", h=HEADS_PER_CHUNK, e=2)
-                shape4 = [P, HEADS_PER_CHUNK, HALF, 2]
-                p1 = ep.tile([P, NW], F32, name="p1", tag="p1")
-                p2 = ep.tile([P, NW], F32, name="p2", tag="p2")
-                nc.vector.tensor_tensor(
-                    out=p1[:].rearrange("p (h i e) -> p h i e", h=HEADS_PER_CHUNK, e=2),
-                    in0=a4,
-                    in1=cosT[:, m].unsqueeze(1).to_broadcast(shape4),
-                    op=ALU.mult,
-                )
-                nc.vector.tensor_tensor(
-                    out=p2[:].rearrange("p (h i e) -> p h i e", h=HEADS_PER_CHUNK, e=2),
-                    in0=a4[:, :, :, ::-1],
-                    in1=sinT[:, m].unsqueeze(1).to_broadcast(shape4),
-                    op=ALU.mult,
-                )
-                nc.gpsimd.tensor_tensor(out=p1[:], in0=p1[:], in1=p2[:], op=ALU.add)
-                nc.sync.dma_start(out=outs_v[which][m][:, n * NW:(n + 1) * NW], in_=p1[:])
 
-        q_ops = [prep_q(0, g) for g in range(2)]
-        k_ops = [prep_k(0, g) for g in range(2)]
-        for m in range(M_TILES):
-            prep_x(m)
-        q_ops += [prep_q(0, g) for g in range(2, PASSES)]
-        k_ops += [prep_k(0, g) for g in range(2, PASSES)]
+        def mm(w, n, m):
+            acc = psum.tile([P, NW], F32, name="acc", tag="acc")
+            for g in range(PASSES):
+                c, s = ops[(w, n, g)]
+                nc.tensor.matmul_mx(
+                    out=acc[:],
+                    lhsT=xc[m][:, g * P:(g + 1) * P].bitcast(FP8X4),
+                    lhsT_scale=xs[m][:, g * P:(g + 1) * P],
+                    rhs=c[:].bitcast(FP8X4),
+                    rhs_scale=s[:],
+                    start=(g == 0),
+                    stop=(g == PASSES - 1),
+                )
+            acc_t[(w, n, m)] = acc
+
+        def rot(w, n, m):
+            if m == 0:
+                prod[(w, n)] = (
+                    big.tile([P, M_TILES, NW], F32, name="p1", tag="big"),
+                    big.tile([P, M_TILES, NW], F32, name="p2", tag="big"),
+                )
+            prod[(w, n, m)] = (prod[(w, n)][0][:, m, :], prod[(w, n)][1][:, m, :])
+            p1, p2 = prod[(w, n, m)]
+            a4 = as4(acc_t[(w, n, m)][:])
+            nc.vector.tensor_tensor(out=as4(p1), in0=a4, in1=cosT[:, m].unsqueeze(1).to_broadcast(shape4), op=ALU.mult)
+            nc.vector.tensor_tensor(out=as4(p2), in0=a4[:, :, :, ::-1], in1=sinT[:, m].unsqueeze(1).to_broadcast(shape4), op=ALU.mult)
+
+        def trigger(w, n, g):
+            nc.gpsimd.tensor_copy(out=junk[:], in_=ops[(w, n, g)][0][:, 0:1])
+
+        def add_chunk(w, n):
+            p1, p2 = prod[(w, n)]
+            nc.gpsimd.tensor_tensor(out=p1[:], in0=p1[:], in1=p2[:], op=ALU.add)
+            nc.sync.dma_start(out=outs_3d[w][:, :, n * NW:(n + 1) * NW], in_=p1[:])
+
+        def add_bank(eng, w, n, m):
+            p1, p2 = prod[(w, n, m)]
+            eng.tensor_tensor(out=p1, in0=p1, in1=p2, op=ALU.add)
+            nc.sync.dma_start(out=outs_v[w][m][:, n * NW:(n + 1) * NW], in_=p1)
+
+        chunks = []
         for n in range(CHUNKS):
-            if n > 0:
-                k_ops = [prep_k(n, g) for g in range(PASSES)]
-                q_ops = [prep_q(n, g) for g in range(PASSES)]
-            project(k_ops, 1, n)
-            project(q_ops, 0, n)
+            chunks.append(("k", n))
+            chunks.append(("q", n))
+
+        def seg_a(n):
+            evac(n, 0)
+            evac(n, 1)
+            widen(n, 2)
+            if n < CHUNKS - 1:
+                widen(n, 3)
+                q_direct(n, 3)
+
+        def seg_b(n):
+            if n == CHUNKS - 1:
+                widen(n, 3)
+            evac(n, 2)
+            if n == CHUNKS - 1:
+                q_direct(n, 3)
+            if n + 1 < CHUNKS:
+                widen(n + 1, 0)
+                widen(n + 1, 1)
+            for u in K_ON_SCALAR:
+                if u[0] == n + 1:
+                    k_interleave(u[0], u[1])
+
+        def k_on_vector(n, gs):
+            return [(n, g) for g in gs if n < CHUNKS and (n, g) not in K_ON_SCALAR]
+
+        def xe(m, half):
+            x_evac(m, half, nc.scalar.copy if m in X_EVAC_ON_SCALAR else nc.vector.tensor_copy)
+
+        widen(0, 0)
+        widen(0, 1)
+        pe_interleave(0, 0)
+        pe_interleave(0, 1)
+        widen(0, 2)
+        evac(0, 0)
+        pe_interleave(0, 2)
+        evac(0, 1)
+        widen(0, 3)
+        evac(0, 2)
+        q_direct(0, 3)
+        widen(1, 0)
+        widen(1, 1)
+        k_interleave(0, 0)
+        k_interleave(0, 1)
+        quant("k", 0, 0)
+        k_interleave(0, 2)
+        quant("k", 0, 1)
+        k_interleave(0, 3)
+        quant("k", 0, 2)
+        for u in K_ON_SCALAR:
+            if u[0] == 1:
+                k_interleave(u[0], u[1])
+        x_transpose(0)
+        x_transpose(1)
+        x_transpose(2)
+        xe(0, 0)
+        xe(0, 1)
+        x_transpose(3)
+        quant("k", 0, 3)
+        xe(1, 0)
+        x_quant(0)
+        xe(1, 1)
+        xe(2, 0)
+        x_quant(1)
+        xe(2, 1)
+        xe(3, 0)
+        x_quant(2)
+        xe(3, 1)
+        pend = k_on_vector(1, (0, 1, 2, 3))
+        k_interleave(pend[0][0], pend[0][1])
+        x_quant(3)
+        k_interleave(pend[1][0], pend[1][1])
+        for m in range(M_TILES):
+            mm("k", 0, m)
+        pe_interleave(1, 0)
+        pe_interleave(1, 1)
+        deferred = [(seg_a, 1)]
+        carry = pend[2:]
+
+        for c in range(len(chunks)):
+            w, n = chunks[c]
+            nxt = chunks[c + 1] if c + 1 < len(chunks) else None
+            last = nxt is None
+            early = (0, 1, 2) if nxt == LAST_CHUNK else (0, 1, 2, 3)
+            if not last:
+                for g in early:
+                    quant(nxt[0], nxt[1], g)
+                trigger(nxt[0], nxt[1], early[-1])
+            if c > 0:
+                add_chunk(chunks[c - 1][0], chunks[c - 1][1])
+            for seg, j in deferred:
+                seg(j)
+            deferred.clear()
+            if nxt == LAST_CHUNK:
+                mm_last(early, True, False)
+            for m in range(M_TILES):
+                rot(w, n, m)
+                if not last and nxt != LAST_CHUNK:
+                    mm(nxt[0], nxt[1], m)
+            if nxt == LAST_CHUNK:
+                quant(nxt[0], nxt[1], 3)
+                mm_last((3,), False, True)
+            if w == "k":
+                if n + 1 < CHUNKS:
+                    pe_interleave(n + 1, 2)
+                    deferred.append((seg_b, n + 1))
+                pend = carry + k_on_vector(n + 1, (2, 3)) if n > 0 else carry
+            else:
+                if n + 2 < CHUNKS:
+                    pe_interleave(n + 2, 0)
+                    pe_interleave(n + 2, 1)
+                    deferred.append((seg_a, n + 2))
+                pend = k_on_vector(n + 2, (0, 1))
+            carry = []
+            for u in pend:
+                k_interleave(u[0], u[1])
+            for u in late_loads[2 * c:2 * c + 2]:
+                load_wq(u[0], u[1])
+                load_wk(u[0], u[1])
+            if last:
+                for m in range(M_TILES):
+                    add_bank(nc.vector, w, n, m)

@@ -204,6 +204,11 @@ def tile_attention_pa_kernel(tc, x, freqs_cos, freqs_sin, wq_bytes, wq_scale, wk
             direct(copy, gk, wkr[(n, g)])
             grouped[("k", n, g)] = gk
 
+        def k_interleave_gpsimd(n, g):
+            gk = stage.tile([P, NW, PACK], BF16, name="gk", tag="gk", bufs=GK_BUFS, align_bytes=64)
+            nc.gpsimd.tensor_scalar(out=gk[:], in0=wkr[(n, g)][:].rearrange("p t c -> p c t"), scalar1=1.0, scalar2=0.0, op0=ALU.mult, op1=ALU.add)
+            grouped[("k", n, g)] = gk
+
         def quant(w, n, g):
             c = codes_pool.tile([P, NW], U32, name=w + "c", tag=w + "c", align_bytes=64)
             s = codes_pool.tile([P, NW], U8, name=w + "s", tag=w + "s", align_bytes=64)
@@ -312,9 +317,11 @@ def tile_attention_pa_kernel(tc, x, freqs_cos, freqs_sin, wq_bytes, wq_scale, wk
         pe_interleave(0, 1)
         widen(0, 2)
         evac(0, 0)
-        pe_interleave(0, 2)
         evac(0, 1)
         widen(0, 3)
+        x_transpose(0)
+        x_transpose(1)
+        pe_interleave(0, 2)
         evac(0, 2)
         q_direct(0, 3)
         widen(1, 0)
@@ -329,8 +336,6 @@ def tile_attention_pa_kernel(tc, x, freqs_cos, freqs_sin, wq_bytes, wq_scale, wk
         for u in K_ON_SCALAR:
             if u[0] == 1:
                 k_interleave(u[0], u[1])
-        x_transpose(0)
-        x_transpose(1)
         x_transpose(2)
         xe(0, 0)
         xe(0, 1)
@@ -367,6 +372,9 @@ def tile_attention_pa_kernel(tc, x, freqs_cos, freqs_sin, wq_bytes, wq_scale, wk
                 trigger(nxt[0], nxt[1], early[-1])
             if c > 0:
                 add_chunk(chunks[c - 1][0], chunks[c - 1][1])
+            else:
+                k_interleave_gpsimd(carry[0][0], carry[0][1])
+                carry = carry[1:]
             for seg, j in deferred:
                 seg(j)
             deferred.clear()

@@ -27,13 +27,20 @@ HEADS_PER_CHUNK = NW // HD
 
 FLOPS = 2 * 2 * S * D * D
 
-GK_BUFS = 7
 RAW_BUFS = 12
+GK_BUFS = 9
+GQ_BUFS = 6
+WIDE_BUFS = 4
+CODE_BUFS = 4
+BIG_BUFS = 6
+BANKS = 4
 PE_PATH_PASSES = 3
-K_ON_SCALAR = ((1, 3), (2, 2), (2, 3), (3, 3))
-Q_DIRECT_ON_VECTOR = ()
-X_EVAC_ON_SCALAR = ()
-LAST_CHUNK = ("q", CHUNKS - 1)
+K_ON_SCALAR = ((2, 3), (3, 3))
+K_ON_GPSIMD = ((1, 2),)
+HEAD_KI = 6
+STEP_KI = 2
+SEQ = tuple([(w, n) for n in range(CHUNKS) for w in ("k", "q")])
+LAST = len(SEQ) - 1
 
 
 def tile_attention_pa_kernel(tc, x, freqs_cos, freqs_sin, wq_bytes, wq_scale, wk, out_0, out_1):
@@ -45,7 +52,6 @@ def tile_attention_pa_kernel(tc, x, freqs_cos, freqs_sin, wq_bytes, wq_scale, wk
         "q": out_0.rearrange("b (m p) h d -> (b m) p (h d)", p=P),
         "k": out_1.rearrange("b (m p) h d -> (b m) p (h d)", p=P),
     }
-
     outs_3d = {
         "q": out_0.rearrange("b (m p) h d -> p (b m) (h d)", p=P),
         "k": out_1.rearrange("b (m p) h d -> p (b m) (h d)", p=P),
@@ -54,10 +60,10 @@ def tile_attention_pa_kernel(tc, x, freqs_cos, freqs_sin, wq_bytes, wq_scale, wk
     with ExitStack() as ctx:
         const = ctx.enter_context(tc.tile_pool(name="const", bufs=1))
         raw = ctx.enter_context(tc.tile_pool(name="raw", bufs=1))
-        stage = ctx.enter_context(tc.tile_pool(name="stage", bufs=3))
-        codes_pool = ctx.enter_context(tc.tile_pool(name="codes", bufs=4))
-        big = ctx.enter_context(tc.tile_pool(name="big", bufs=6))
-        psum = ctx.enter_context(tc.psum_pool(name="psum", bufs=4))
+        stage = ctx.enter_context(tc.tile_pool(name="stage", bufs=1))
+        codes_pool = ctx.enter_context(tc.tile_pool(name="codes", bufs=CODE_BUFS))
+        big = ctx.enter_context(tc.tile_pool(name="big", bufs=BIG_BUFS))
+        psum = ctx.enter_context(tc.psum_pool(name="psum", bufs=BANKS))
         ctx.enter_context(tc.manual_schedule())
 
         sc = const.tile([P, PASSES, PACK], F32, name="sc")
@@ -72,66 +78,53 @@ def tile_attention_pa_kernel(tc, x, freqs_cos, freqs_sin, wq_bytes, wq_scale, wk
         nc.scalar.activation(out=warm[:, 1:2], in_=warm[:, 0:1], func=ACT.Copy)
 
         junk = const.tile([P, 1], U32, name="junk")
+        ident = const.tile([P, P], F32, name="ident")
+        make_identity(nc, ident[:])
+        ident_bf = const.tile([P, P], BF16, name="ident_bf")
+        make_identity(nc, ident_bf[:])
+        sinT = const.tile([P, M_TILES, HALF, 2], BF16, name="sinT")
 
         wqb = {}
         wkr = {}
-        xr = []
+        xr = {}
+        xt_tiles = {}
+        xg_tiles = {}
+        xc = {}
+        xs = {}
+        wide_t = {}
+        il_t = {}
+        grouped = {}
+        ops = {}
+        acc_t = {}
+        prod = {}
+        shape4 = [P, HEADS_PER_CHUNK, HALF, 2]
 
         def load_wq(n, g):
-            cols = slice(n * NW, (n + 1) * NW)
             tq = raw.tile([P, PACK, NW], U8, name="wqb", tag="wqb", bufs=RAW_BUFS)
-            nc.sync.dma_start(out=tq[:], in_=wqb_v[g][:, :, cols])
+            nc.sync.dma_start(out=tq[:], in_=wqb_v[g][:, :, n * NW:(n + 1) * NW])
             wqb[(n, g)] = tq
 
         def load_wk(n, g):
-            cols = slice(n * NW, (n + 1) * NW)
             tk = raw.tile([P, PACK, NW], BF16, name="wkr", tag="wkr", bufs=RAW_BUFS)
-            nc.sync.dma_start(out=tk[:], in_=wk_v[g][:, :, cols])
+            nc.sync.dma_start(out=tk[:], in_=wk_v[g][:, :, n * NW:(n + 1) * NW])
             wkr[(n, g)] = tk
 
         def load_x(m):
             t = big.tile([P, D], BF16, name="xr", tag="big")
             nc.sync.dma_start(out=t[:], in_=x_v[m])
-            xr.append(t)
+            xr[m] = t
 
-        load_wq(0, 0)
-        load_wk(0, 0)
-        load_wq(0, 1)
-        load_wk(0, 1)
-        load_wq(0, 2)
-        load_wk(0, 2)
-        load_wk(0, 3)
-        load_x(0)
-        load_wq(0, 3)
-        load_x(1)
-        load_x(2)
-        load_x(3)
-        for n in range(1, CHUNKS - 1):
-            for g in range(PASSES):
-                load_wk(n, g)
-                load_wq(n, g)
-        late_loads = [(CHUNKS - 1, g) for g in range(PASSES)]
+        def sin_table():
+            nc.vector.tensor_scalar(out=sinT[:, :, :, 0], in0=sin_sb[:], scalar1=-1.0, scalar2=None, op0=ALU.mult)
+            nc.vector.tensor_copy(out=sinT[:, :, :, 1], in_=sin_sb[:])
 
-        ident = const.tile([P, P], F32, name="ident")
-        make_identity(nc, ident[:])
-        ident_bf = const.tile([P, P], BF16, name="ident_bf")
-        make_identity(nc, ident_bf[:])
-        cosT = const.tile([P, M_TILES, HALF, 2], F32, name="cosT")
-        sinT = const.tile([P, M_TILES, HALF, 2], F32, name="sinT")
-        for e in range(2):
-            nc.vector.tensor_copy(out=cosT[:, :, :, e], in_=cos_sb[:])
-        nc.vector.tensor_scalar(out=sinT[:, :, :, 0], in0=sin_sb[:], scalar1=-1.0, scalar2=None, op0=ALU.mult)
-        nc.vector.tensor_copy(out=sinT[:, :, :, 1], in_=sin_sb[:])
-
-        xt_tiles = {}
-        xg_tiles = {}
-        xc = {}
-        xs = {}
+        def x_tag(m):
+            return "il" if m == 2 else "acc"
 
         def x_transpose(m):
             words = xr[m][:].bitcast(F32)
             for half in range(2):
-                xt = psum.tile([P, NW], F32, name="xt", tag=("il" if m == 2 else "acc"))
+                xt = psum.tile([P, NW], F32, name="xt", tag=x_tag(m))
                 for gl in range(2):
                     g = 2 * half + gl
                     for u in range(2):
@@ -139,12 +132,12 @@ def tile_attention_pa_kernel(tc, x, freqs_cos, freqs_sin, wq_bytes, wq_scale, wk
                         nc.tensor.transpose(xt[:, j * P:(j + 1) * P], words[:, 256 * g + u:256 * (g + 1):2], ident[:])
                 xt_tiles[(m, half)] = xt
 
-        def x_evac(m, half, copy):
-            if half == 0:
-                xg_tiles[m] = stage.tile([P, PASSES, P, PACK], BF16, name="xg", tag="gk", bufs=GK_BUFS, align_bytes=64)
-            xg = xg_tiles[m]
-            dst = xg[:, 2 * half:2 * half + 2].rearrange("p g r t -> p (g r t)").bitcast(F32).rearrange("p (g r u) -> p g r u", g=2, u=2)
-            copy(out=dst, in_=xt_tiles[(m, half)][:].rearrange("p (g u r) -> p g r u", g=2, u=2))
+        def x_evac(m):
+            xg = stage.tile([P, PASSES, P, PACK], BF16, name="xg", tag="gk", bufs=GK_BUFS, align_bytes=64)
+            xg_tiles[m] = xg
+            for half in range(2):
+                dst = xg[:, 2 * half:2 * half + 2].rearrange("p g r t -> p (g r t)").bitcast(F32).rearrange("p (g r u) -> p g r u", g=2, u=2)
+                nc.scalar.copy(out=dst, in_=xt_tiles[(m, half)][:].rearrange("p (g u r) -> p g r u", g=2, u=2))
 
         def x_quant(m):
             c = const.tile([P, PASSES * P], U32, name="xc_%d" % m, align_bytes=64)
@@ -153,16 +146,11 @@ def tile_attention_pa_kernel(tc, x, freqs_cos, freqs_sin, wq_bytes, wq_scale, wk
             xc[m] = c
             xs[m] = s
 
-        wide_t = {}
-        il_t = {}
-        grouped = {}
-        ops = {}
-
         def direct(copy, dst, src):
             copy(out=dst[:].rearrange("p (c i) t -> p c t i", i=4), in_=src[:].rearrange("p t (c i) -> p c t i", i=4))
 
         def widen(n, g):
-            wide = stage.tile([P, PACK, NW], BF16, name="wide", tag="wide", bufs=4)
+            wide = stage.tile([P, PACK, NW], BF16, name="wide", tag="wide", bufs=WIDE_BUFS)
             for t in range(PACK):
                 nc.scalar.activation(out=wide[:, t, :], in_=wqb[(n, g)][:, t, :].bitcast(FP8), func=ACT.Copy, scale=sc[:, g, t:t + 1])
             wide_t[(n, g)] = wide
@@ -185,28 +173,23 @@ def tile_attention_pa_kernel(tc, x, freqs_cos, freqs_sin, wq_bytes, wq_scale, wk
             il_t[(n, g)] = banks
 
         def new_gq(n, g):
-            grouped[("q", n, g)] = stage.tile([P, NW, PACK], BF16, name="gq", tag="gq", bufs=6, align_bytes=64)
+            grouped[("q", n, g)] = stage.tile([P, NW, PACK], BF16, name="gq", tag="gq", bufs=GQ_BUFS, align_bytes=64)
             return grouped[("q", n, g)]
 
         def evac(n, g):
-            gq = new_gq(n, g)
-            flat = gq[:].rearrange("p c t -> p (c t)")
+            flat = new_gq(n, g)[:].rearrange("p c t -> p (c t)")
             for b in range(2):
                 nc.scalar.copy(out=flat[:, b * 2 * NW:(b + 1) * 2 * NW], in_=il_t[(n, g)][b][:])
 
         def q_direct(n, g):
-            copy = nc.vector.tensor_copy if n in Q_DIRECT_ON_VECTOR else nc.scalar.copy
-            direct(copy, new_gq(n, g), wide_t[(n, g)])
+            direct(nc.scalar.copy, new_gq(n, g), wide_t[(n, g)])
 
         def k_interleave(n, g):
             gk = stage.tile([P, NW, PACK], BF16, name="gk", tag="gk", bufs=GK_BUFS, align_bytes=64)
-            copy = nc.scalar.copy if (n, g) in K_ON_SCALAR else nc.vector.tensor_copy
-            direct(copy, gk, wkr[(n, g)])
-            grouped[("k", n, g)] = gk
-
-        def k_interleave_gpsimd(n, g):
-            gk = stage.tile([P, NW, PACK], BF16, name="gk", tag="gk", bufs=GK_BUFS, align_bytes=64)
-            nc.gpsimd.tensor_scalar(out=gk[:], in0=wkr[(n, g)][:].rearrange("p t c -> p c t"), scalar1=1.0, scalar2=0.0, op0=ALU.mult, op1=ALU.add)
+            if (n, g) in K_ON_GPSIMD:
+                nc.gpsimd.tensor_scalar(out=gk[:], in0=wkr[(n, g)][:].rearrange("p t c -> p c t"), scalar1=1.0, scalar2=0.0, op0=ALU.mult, op1=ALU.add)
+            else:
+                direct(nc.scalar.copy if (n, g) in K_ON_SCALAR else nc.vector.tensor_copy, gk, wkr[(n, g)])
             grouped[("k", n, g)] = gk
 
         def quant(w, n, g):
@@ -215,195 +198,194 @@ def tile_attention_pa_kernel(tc, x, freqs_cos, freqs_sin, wq_bytes, wq_scale, wk
             nc.vector.quantize_mx(out=c[:].bitcast(FP8X4), scales=s[:], in_=grouped[(w, n, g)][:].rearrange("p c t -> p (c t)"))
             ops[(w, n, g)] = (c, s)
 
-        acc_t = {}
-        prod = {}
-        shape4 = [P, HEADS_PER_CHUNK, HALF, 2]
-
         def as4(ap):
             return ap.rearrange("p (h i e) -> p h i e", h=HEADS_PER_CHUNK, e=2)
 
-        def mm_last(gs, first, final):
-            w, n = LAST_CHUNK
+        def mm(c, m, gs):
+            w, n = SEQ[c]
+            if gs[0] == 0:
+                acc_t[(c, m)] = psum.tile([P, NW], F32, name="acc", tag=("il" if c == LAST else "acc"))
             for g in gs:
-                c, s = ops[(w, n, g)]
-                for m in range(M_TILES):
-                    if (w, n, m) not in acc_t:
-                        acc_t[(w, n, m)] = psum.tile([P, NW], F32, name="accl", tag="il")
-                    nc.tensor.matmul_mx(
-                        out=acc_t[(w, n, m)][:],
-                        lhsT=xc[m][:, g * P:(g + 1) * P].bitcast(FP8X4),
-                        lhsT_scale=xs[m][:, g * P:(g + 1) * P],
-                        rhs=c[:].bitcast(FP8X4),
-                        rhs_scale=s[:],
-                        start=(first and g == gs[0]),
-                        stop=final,
-                    )
-
-        def mm(w, n, m):
-            acc = psum.tile([P, NW], F32, name="acc", tag="acc")
-            for g in range(PASSES):
-                c, s = ops[(w, n, g)]
+                cd, s = ops[(w, n, g)]
                 nc.tensor.matmul_mx(
-                    out=acc[:],
+                    out=acc_t[(c, m)][:],
                     lhsT=xc[m][:, g * P:(g + 1) * P].bitcast(FP8X4),
                     lhsT_scale=xs[m][:, g * P:(g + 1) * P],
-                    rhs=c[:].bitcast(FP8X4),
+                    rhs=cd[:].bitcast(FP8X4),
                     rhs_scale=s[:],
                     start=(g == 0),
                     stop=(g == PASSES - 1),
                 )
-            acc_t[(w, n, m)] = acc
 
-        def rot(w, n, m):
+        def rot(c, m):
             if m == 0:
-                prod[(w, n)] = (
+                prod[c] = (
                     big.tile([P, M_TILES, NW], F32, name="p1", tag="big"),
                     big.tile([P, M_TILES, NW], F32, name="p2", tag="big"),
                 )
-            prod[(w, n, m)] = (prod[(w, n)][0][:, m, :], prod[(w, n)][1][:, m, :])
-            p1, p2 = prod[(w, n, m)]
-            a4 = as4(acc_t[(w, n, m)][:])
-            nc.vector.tensor_tensor(out=as4(p1), in0=a4, in1=cosT[:, m].unsqueeze(1).to_broadcast(shape4), op=ALU.mult)
+            p1, p2 = prod[c][0][:, m, :], prod[c][1][:, m, :]
+            a4 = as4(acc_t[(c, m)][:])
+            nc.vector.tensor_tensor(out=as4(p1), in0=a4, in1=cos_sb[:, m].unsqueeze(1).unsqueeze(3).to_broadcast(shape4), op=ALU.mult)
             nc.vector.tensor_tensor(out=as4(p2), in0=a4[:, :, :, ::-1], in1=sinT[:, m].unsqueeze(1).to_broadcast(shape4), op=ALU.mult)
 
-        def trigger(w, n, g):
+        def trigger(c):
+            w, n = SEQ[c + 1]
+            g = PASSES - 2 if c + 1 == LAST else PASSES - 1
             nc.gpsimd.tensor_copy(out=junk[:], in_=ops[(w, n, g)][0][:, 0:1])
 
-        def add_chunk(w, n):
-            p1, p2 = prod[(w, n)]
+        def add_chunk(c):
+            p1, p2 = prod[c]
             nc.gpsimd.tensor_tensor(out=p1[:], in0=p1[:], in1=p2[:], op=ALU.add)
-            nc.sync.dma_start(out=outs_3d[w][:, :, n * NW:(n + 1) * NW], in_=p1[:])
 
-        def add_bank(eng, w, n, m):
-            p1, p2 = prod[(w, n, m)]
-            eng.tensor_tensor(out=p1, in0=p1, in1=p2, op=ALU.add)
-            nc.sync.dma_start(out=outs_v[w][m][:, n * NW:(n + 1) * NW], in_=p1)
+        def store_chunk(c):
+            w, n = SEQ[c]
+            nc.sync.dma_start(out=outs_3d[w][:, :, n * NW:(n + 1) * NW], in_=prod[c][0][:])
 
-        chunks = []
-        for n in range(CHUNKS):
-            chunks.append(("k", n))
-            chunks.append(("q", n))
+        def add_bank(c, m):
+            p1, p2 = prod[c][0][:, m, :], prod[c][1][:, m, :]
+            nc.vector.tensor_tensor(out=p1, in0=p1, in1=p2, op=ALU.add)
 
-        def seg_a(n):
-            evac(n, 0)
-            evac(n, 1)
-            widen(n, 2)
-            if n < CHUNKS - 1:
-                widen(n, 3)
-                q_direct(n, 3)
+        def store_bank(c, m):
+            w, n = SEQ[c]
+            nc.sync.dma_start(out=outs_v[w][m][:, n * NW:(n + 1) * NW], in_=prod[c][0][:, m, :])
 
-        def seg_b(n):
-            if n == CHUNKS - 1:
-                widen(n, 3)
-            evac(n, 2)
-            if n == CHUNKS - 1:
-                q_direct(n, 3)
-            if n + 1 < CHUNKS:
-                widen(n + 1, 0)
-                widen(n + 1, 1)
-            for u in K_ON_SCALAR:
-                if u[0] == n + 1:
-                    k_interleave(u[0], u[1])
-
-        def k_on_vector(n, gs):
-            return [(n, g) for g in gs if n < CHUNKS and (n, g) not in K_ON_SCALAR]
-
-        def xe(m, half):
-            x_evac(m, half, nc.scalar.copy if m in X_EVAC_ON_SCALAR else nc.vector.tensor_copy)
-
-        widen(0, 0)
-        widen(0, 1)
-        pe_interleave(0, 0)
-        pe_interleave(0, 1)
-        widen(0, 2)
-        evac(0, 0)
-        evac(0, 1)
-        widen(0, 3)
-        x_transpose(0)
-        x_transpose(1)
-        pe_interleave(0, 2)
-        evac(0, 2)
-        q_direct(0, 3)
-        widen(1, 0)
-        widen(1, 1)
-        k_interleave(0, 0)
-        k_interleave(0, 1)
-        quant("k", 0, 0)
-        k_interleave(0, 2)
-        quant("k", 0, 1)
-        k_interleave(0, 3)
-        quant("k", 0, 2)
-        for u in K_ON_SCALAR:
-            if u[0] == 1:
-                k_interleave(u[0], u[1])
-        x_transpose(2)
-        xe(0, 0)
-        xe(0, 1)
-        x_transpose(3)
-        quant("k", 0, 3)
-        xe(1, 0)
-        x_quant(0)
-        xe(1, 1)
-        xe(2, 0)
-        x_quant(1)
-        xe(2, 1)
-        xe(3, 0)
-        x_quant(2)
-        xe(3, 1)
-        pend = k_on_vector(1, (0, 1, 2, 3))
-        k_interleave(pend[0][0], pend[0][1])
-        x_quant(3)
-        k_interleave(pend[1][0], pend[1][1])
-        for m in range(M_TILES):
-            mm("k", 0, m)
-        pe_interleave(1, 0)
-        pe_interleave(1, 1)
-        deferred = [(seg_a, 1)]
-        carry = pend[2:]
-
-        for c in range(len(chunks)):
-            w, n = chunks[c]
-            nxt = chunks[c + 1] if c + 1 < len(chunks) else None
-            last = nxt is None
-            early = (0, 1, 2) if nxt == LAST_CHUNK else (0, 1, 2, 3)
-            if not last:
-                for g in early:
-                    quant(nxt[0], nxt[1], g)
-                trigger(nxt[0], nxt[1], early[-1])
-            if c > 0:
-                add_chunk(chunks[c - 1][0], chunks[c - 1][1])
-            else:
-                k_interleave_gpsimd(carry[0][0], carry[0][1])
-                carry = carry[1:]
-            for seg, j in deferred:
-                seg(j)
-            deferred.clear()
-            if nxt == LAST_CHUNK:
-                mm_last(early, True, False)
-            for m in range(M_TILES):
-                rot(w, n, m)
-                if not last and nxt != LAST_CHUNK:
-                    mm(nxt[0], nxt[1], m)
-            if nxt == LAST_CHUNK:
-                quant(nxt[0], nxt[1], 3)
-                mm_last((3,), False, True)
+        def src_of(w, n, g):
             if w == "k":
-                if n + 1 < CHUNKS:
-                    pe_interleave(n + 1, 2)
-                    deferred.append((seg_b, n + 1))
-                pend = carry + k_on_vector(n + 1, (2, 3)) if n > 0 else carry
+                return ("KI", n, g)
+            return ("EV", n, g) if g < PE_PATH_PASSES else ("QD", n, g)
+
+        def e_lq(n, g):
+            return (("LQ", n, g), load_wq, (n, g), (), {"wqb": 1}, {})
+
+        def e_lk(n, g):
+            return (("LK", n, g), load_wk, (n, g), (), {"wkr": 1}, {})
+
+        def e_lx(m):
+            return (("LX", m), load_x, (m,), (), {"big": 1}, {})
+
+        def e_w(n, g):
+            return (("W", n, g), widen, (n, g), (("LQ", n, g),), {"wide": 1}, {"wqb": 1})
+
+        def e_pi(n, g):
+            return (("PI", n, g), pe_interleave, (n, g), (("W", n, g),), {"il": 2}, {"wide": 1})
+
+        def e_ev(n, g):
+            return (("EV", n, g), evac, (n, g), (("PI", n, g),), {"gq": 1}, {"il": 2})
+
+        def e_qd(n, g):
+            return (("QD", n, g), q_direct, (n, g), (("W", n, g),), {"gq": 1}, {"wide": 1})
+
+        def e_ki(n, g):
+            return (("KI", n, g), k_interleave, (n, g), (("LK", n, g),), {"gk": 1}, {"wkr": 1})
+
+        def e_xt(m):
+            return (("XT", m), x_transpose, (m,), (("LX", m),), {x_tag(m): 2}, {"big": 1})
+
+        def e_xe(m):
+            return (("XE", m), x_evac, (m,), (("XT", m),), {"gk": 1}, {x_tag(m): 2})
+
+        def e_xq(m):
+            return (("XQ", m), x_quant, (m,), (("XE", m),), {}, {"gk": 1})
+
+        def e_q(w, n, g):
+            return (("Q", w, n, g), quant, (w, n, g), (src_of(w, n, g),), {w + "c": 1}, {"g" + w: 1})
+
+        def e_mm(c, m, gs):
+            w, n = SEQ[c]
+            need = tuple([("Q", w, n, g) for g in gs]) + (("XQ", m),)
+            takes = {("il" if c == LAST else "acc"): 1} if gs[0] == 0 else {}
+            gives = {w + "c": len(gs)} if m == M_TILES - 1 else {}
+            return (("MM", c, m, gs[-1]), mm, (c, m, gs), need, takes, gives)
+
+        def e_rot(c, m):
+            return (("ROT", c, m), rot, (c, m), (("MM", c, m, PASSES - 1),), {"big": 2} if m == 0 else {}, {("il" if c == LAST else "acc"): 1})
+
+        every = tuple(range(PASSES))
+        vk = [(n, g) for n in range(CHUNKS) for g in range(PASSES) if (n, g) not in K_ON_SCALAR and (n, g) not in K_ON_GPSIMD]
+
+        q_vector = [e_ki(0, 0)]
+        for g in range(PASSES):
+            q_vector.append(e_ki(vk[g + 1][0], vk[g + 1][1]))
+            q_vector.append(e_q("k", 0, g))
+        rest = vk[PASSES + 1:]
+        head = rest[:HEAD_KI - 1]
+        rest = rest[HEAD_KI - 1:]
+        q_vector.extend([e_ki(u[0], u[1]) for u in head[:2]])
+        q_vector.append((("SIN",), sin_table, (), (), {}, {}))
+        q_vector.extend((e_xq(0), e_xq(1)))
+        q_vector.extend([e_ki(u[0], u[1]) for u in head[2:4]])
+        q_vector.extend((e_xq(2), e_xq(3)))
+        q_vector.extend([e_ki(u[0], u[1]) for u in head[4:]])
+        for c in range(len(SEQ)):
+            if c < LAST:
+                w, n = SEQ[c + 1]
+                q_vector.extend([e_q(w, n, g) for g in (every[:-1] if c + 1 == LAST else every)])
+            q_vector.extend([e_rot(c, m) for m in range(M_TILES)])
+            if c + 1 == LAST:
+                q_vector.append(e_q(w, n, PASSES - 1))
+            q_vector.extend([e_ki(u[0], u[1]) for u in rest[:STEP_KI]])
+            rest = rest[STEP_KI:]
+        q_vector.extend([(("AB", m), add_bank, (LAST, m), (("ROT", LAST, m),), {}, {}) for m in range(M_TILES)])
+
+        q_scalar = [e_w(0, 0), e_w(0, 1), e_w(0, 2), e_ev(0, 0), e_ev(0, 1), e_xe(0), e_xe(1), e_w(0, 3), e_ev(0, 2), e_xe(2), e_xe(3), e_qd(0, 3)]
+        for n in range(1, CHUNKS):
+            q_scalar.extend((e_w(n, 0), e_w(n, 1)))
+            q_scalar.extend([e_ki(u[0], u[1]) for u in K_ON_SCALAR if u[0] == n])
+            q_scalar.extend((e_ev(n, 0), e_ev(n, 1), e_w(n, 2), e_w(n, 3)))
+            q_scalar.extend((e_qd(n, 3), e_ev(n, 2)) if n < CHUNKS - 1 else (e_ev(n, 2), e_qd(n, 3)))
+
+        q_tensor = [e_pi(0, 0), e_pi(0, 1), e_xt(0), e_xt(1), e_pi(0, 2), e_xt(2), e_xt(3)]
+        q_tensor.extend([e_mm(0, m, every) for m in range(M_TILES)])
+        q_tensor.extend((e_pi(1, 0), e_pi(1, 1)))
+        for c in range(LAST):
+            w, n = SEQ[c]
+            if c + 1 < LAST:
+                q_tensor.extend([e_mm(c + 1, m, every) for m in range(M_TILES)])
             else:
-                if n + 2 < CHUNKS:
-                    pe_interleave(n + 2, 0)
-                    pe_interleave(n + 2, 1)
-                    deferred.append((seg_a, n + 2))
-                pend = k_on_vector(n + 2, (0, 1))
-            carry = []
-            for u in pend:
-                k_interleave(u[0], u[1])
-            for u in late_loads[2 * c:2 * c + 2]:
-                load_wq(u[0], u[1])
-                load_wk(u[0], u[1])
-            if last:
-                for m in range(M_TILES):
-                    add_bank(nc.vector, w, n, m)
+                q_tensor.extend([e_mm(LAST, m, every[:-1]) for m in range(M_TILES)])
+                q_tensor.extend([e_mm(LAST, m, every[-1:]) for m in range(M_TILES)])
+            if w == "k" and n + 1 < CHUNKS:
+                q_tensor.append(e_pi(n + 1, 2))
+            if w == "q" and n + 2 < CHUNKS:
+                q_tensor.extend((e_pi(n + 2, 0), e_pi(n + 2, 1)))
+
+        q_gpsimd = []
+        for c in range(LAST):
+            w, n = SEQ[c + 1]
+            q_gpsimd.append((("TRG", c), trigger, (c,), (("Q", w, n, PASSES - 2 if c + 1 == LAST else PASSES - 1),), {}, {}))
+            if c == 0:
+                q_gpsimd.extend([e_ki(u[0], u[1]) for u in K_ON_GPSIMD])
+            else:
+                q_gpsimd.append((("ADD", c - 1), add_chunk, (c - 1,), (("ROT", c - 1, M_TILES - 1),), {}, {"big": 1}))
+        q_gpsimd.append((("ADD", LAST - 1), add_chunk, (LAST - 1,), (("ROT", LAST - 1, M_TILES - 1),), {}, {"big": 1}))
+
+        q_sync = [e_lq(0, 0), e_lk(0, 0), e_lq(0, 1), e_lk(0, 1), e_lk(0, 2), e_lq(0, 2), e_lk(0, 3), e_lx(0), e_lk(1, 0), e_lx(1), e_lq(0, 3),
+                  e_lk(1, 1), e_lx(2), e_lk(1, 3), e_lx(3), e_lk(2, 0), e_lk(2, 1), e_lq(1, 0), e_lk(2, 2), e_lq(1, 1), e_lk(1, 2), e_lq(1, 2), e_lq(1, 3), e_lk(2, 3)]
+        q_sync.extend([e_lq(2, g) for g in range(PASSES)])
+        for g in range(PASSES):
+            q_sync.extend((e_lk(3, g), e_lq(3, g)))
+        q_sync.extend([(("ST", c), store_chunk, (c,), (("ADD", c),), {}, {"big": 1}) for c in range(LAST)])
+        q_sync.extend([(("SB", m), store_bank, (LAST, m), (("AB", m),), {}, {}) for m in range(M_TILES)])
+
+        room = {"wqb": RAW_BUFS, "wkr": RAW_BUFS, "big": BIG_BUFS, "wide": WIDE_BUFS, "il": BANKS, "acc": BANKS,
+                "gq": GQ_BUFS, "gk": GK_BUFS, "kc": CODE_BUFS, "qc": CODE_BUFS}
+        queues = [q_sync, q_scalar, q_tensor, q_vector, q_gpsimd]
+        at = [0] * len(queues)
+        written = set()
+        moved = True
+        while moved:
+            moved = False
+            for j in range(len(queues)):
+                while at[j] < len(queues[j]):
+                    key, fn, args, need, takes, gives = queues[j][at[j]]
+                    if not all([k in written for k in need]) or not all([room[t] >= takes[t] for t in takes]):
+                        break
+                    fn(*args)
+                    written.add(key)
+                    for t in takes:
+                        room[t] -= takes[t]
+                    for t in gives:
+                        room[t] += gives[t]
+                    at[j] += 1
+                    moved = True
+        assert all([at[j] == len(queues[j]) for j in range(len(queues))])

@@ -233,6 +233,10 @@ def tile_attention_pa_kernel(tc, x, freqs_cos, freqs_sin, wq_bytes, wq_scale, wk
             g = PASSES - 2 if c + 1 == LAST else PASSES - 1
             nc.gpsimd.tensor_copy(out=junk[:], in_=ops[(w, n, g)][0][:, 0:1])
 
+        def touch(c):
+            word = prod[c][1][:, M_TILES - 1, NW - 1:NW]
+            nc.vector.tensor_copy(out=word, in_=word)
+
         def add_chunk(c):
             p1, p2 = prod[c]
             nc.gpsimd.tensor_tensor(out=p1[:], in0=p1[:], in1=p2[:], op=ALU.add)
@@ -303,7 +307,7 @@ def tile_attention_pa_kernel(tc, x, freqs_cos, freqs_sin, wq_bytes, wq_scale, wk
         every = tuple(range(PASSES))
         vk = [(n, g) for n in range(CHUNKS) for g in range(PASSES) if (n, g) not in K_ON_SCALAR and (n, g) not in K_ON_GPSIMD]
 
-        q_vector = [e_ki(0, 0)]
+        q_vector = [(("SIN",), sin_table, (), (), {}, {}), e_ki(0, 0)]
         for g in range(PASSES):
             q_vector.append(e_ki(vk[g + 1][0], vk[g + 1][1]))
             q_vector.append(e_q("k", 0, g))
@@ -311,7 +315,6 @@ def tile_attention_pa_kernel(tc, x, freqs_cos, freqs_sin, wq_bytes, wq_scale, wk
         head = rest[:HEAD_KI - 1]
         rest = rest[HEAD_KI - 1:]
         q_vector.extend([e_ki(u[0], u[1]) for u in head[:2]])
-        q_vector.append((("SIN",), sin_table, (), (), {}, {}))
         q_vector.extend((e_xq(0), e_xq(1)))
         q_vector.extend([e_ki(u[0], u[1]) for u in head[2:4]])
         q_vector.extend((e_xq(2), e_xq(3)))
@@ -320,6 +323,8 @@ def tile_attention_pa_kernel(tc, x, freqs_cos, freqs_sin, wq_bytes, wq_scale, wk
             if c < LAST:
                 w, n = SEQ[c + 1]
                 q_vector.extend([e_q(w, n, g) for g in (every[:-1] if c + 1 == LAST else every)])
+            if 0 < c:
+                q_vector.append((("TCH", c - 1), touch, (c - 1,), (("ROT", c - 1, M_TILES - 1),), {}, {}))
             q_vector.extend([e_rot(c, m) for m in range(M_TILES)])
             if c + 1 == LAST:
                 q_vector.append(e_q(w, n, PASSES - 1))
@@ -350,14 +355,10 @@ def tile_attention_pa_kernel(tc, x, freqs_cos, freqs_sin, wq_bytes, wq_scale, wk
                 q_tensor.extend((e_pi(n + 2, 0), e_pi(n + 2, 1)))
 
         q_gpsimd = []
-        for c in range(LAST):
-            w, n = SEQ[c + 1]
-            q_gpsimd.append((("TRG", c), trigger, (c,), (("Q", w, n, PASSES - 2 if c + 1 == LAST else PASSES - 1),), {}, {}))
-            if c == 0:
-                q_gpsimd.extend([e_ki(u[0], u[1]) for u in K_ON_GPSIMD])
-            else:
-                q_gpsimd.append((("ADD", c - 1), add_chunk, (c - 1,), (("ROT", c - 1, M_TILES - 1),), {}, {"big": 1}))
-        q_gpsimd.append((("ADD", LAST - 1), add_chunk, (LAST - 1,), (("ROT", LAST - 1, M_TILES - 1),), {}, {"big": 1}))
+        w, n = SEQ[1]
+        q_gpsimd.append((("TRG", 0), trigger, (0,), (("Q", w, n, PASSES - 1),), {}, {}))
+        q_gpsimd.extend([e_ki(u[0], u[1]) for u in K_ON_GPSIMD])
+        q_gpsimd.extend([(("ADD", c), add_chunk, (c,), (("TCH", c),), {}, {"big": 1}) for c in range(LAST)])
 
         q_sync = [e_lq(0, 0), e_lk(0, 0), e_lq(0, 1), e_lk(0, 1), e_lk(0, 2), e_lq(0, 2), e_lk(0, 3), e_lx(0), e_lk(1, 0), e_lx(1), e_lq(0, 3),
                   e_lk(1, 1), e_lx(2), e_lk(1, 3), e_lx(3), e_lk(2, 0), e_lk(2, 1), e_lq(1, 0), e_lk(2, 2), e_lq(1, 1), e_lk(1, 2), e_lq(1, 2), e_lq(1, 3), e_lk(2, 3)]

@@ -230,20 +230,19 @@ def tile_attention_pa_kernel(tc, x, freqs_cos, freqs_sin, wq_bytes, wq_scale, wk
 
         def trigger(c):
             w, n = SEQ[c + 1]
-            g = PASSES - 2 if c + 1 == LAST else PASSES - 1
-            nc.gpsimd.tensor_copy(out=junk[:], in_=ops[(w, n, g)][0][:, 0:1])
+            nc.gpsimd.tensor_copy(out=junk[:], in_=ops[(w, n, 0)][0][:, 0:1])
 
         def touch(c):
-            word = prod[c][1][:, M_TILES - 1, NW - 1:NW]
+            word = prod[c][1][:, 0, 0:1]
             nc.vector.tensor_copy(out=word, in_=word)
 
-        def add_chunk(c):
+        def add_chunk(c, m0=0, m1=M_TILES):
             p1, p2 = prod[c]
-            nc.gpsimd.tensor_tensor(out=p1[:], in0=p1[:], in1=p2[:], op=ALU.add)
+            nc.gpsimd.tensor_tensor(out=p1[:, m0:m1, :], in0=p1[:, m0:m1, :], in1=p2[:, m0:m1, :], op=ALU.add)
 
-        def store_chunk(c):
+        def store_chunk(c, m0=0, m1=M_TILES):
             w, n = SEQ[c]
-            nc.sync.dma_start(out=outs_3d[w][:, :, n * NW:(n + 1) * NW], in_=prod[c][0][:])
+            nc.sync.dma_start(out=outs_3d[w][:, m0:m1, n * NW:(n + 1) * NW], in_=prod[c][0][:, m0:m1, :])
 
         def add_bank(c, m):
             p1, p2 = prod[c][0][:, m, :], prod[c][1][:, m, :]
@@ -320,11 +319,14 @@ def tile_attention_pa_kernel(tc, x, freqs_cos, freqs_sin, wq_bytes, wq_scale, wk
         q_vector.extend((e_xq(2), e_xq(3)))
         q_vector.extend([e_ki(u[0], u[1]) for u in head[4:]])
         for c in range(len(SEQ)):
+            tch = [(("TCH", c - 1), touch, (c - 1,), (("ROT", c - 1, M_TILES - 1),), {}, {})] if c > 0 else []
             if c < LAST:
                 w, n = SEQ[c + 1]
-                q_vector.extend([e_q(w, n, g) for g in (every[:-1] if c + 1 == LAST else every)])
-            if 0 < c:
-                q_vector.append((("TCH", c - 1), touch, (c - 1,), (("ROT", c - 1, M_TILES - 1),), {}, {}))
+                q_vector.extend([e_q(w, n, g) for g in (every[1:-1] if c + 1 == LAST else every[1:])])
+                q_vector.extend(tch)
+                q_vector.append(e_q(w, n, 0))
+            else:
+                q_vector.extend(tch)
             q_vector.extend([e_rot(c, m) for m in range(M_TILES)])
             if c + 1 == LAST:
                 q_vector.append(e_q(w, n, PASSES - 1))
@@ -356,16 +358,20 @@ def tile_attention_pa_kernel(tc, x, freqs_cos, freqs_sin, wq_bytes, wq_scale, wk
 
         q_gpsimd = []
         w, n = SEQ[1]
-        q_gpsimd.append((("TRG", 0), trigger, (0,), (("Q", w, n, PASSES - 1),), {}, {}))
+        q_gpsimd.append((("TRG", 0), trigger, (0,), (("Q", w, n, 0),), {}, {}))
         q_gpsimd.extend([e_ki(u[0], u[1]) for u in K_ON_GPSIMD])
-        q_gpsimd.extend([(("ADD", c), add_chunk, (c,), (("TCH", c),), {}, {"big": 1}) for c in range(LAST)])
+        q_gpsimd.extend([(("ADD", c), add_chunk, (c,), (("TCH", c),), {}, {"big": 1}) for c in range(LAST - 1)])
+        q_gpsimd.append((("ADDa", LAST - 1), add_chunk, (LAST - 1, 0, 2), (("TCH", LAST - 1),), {}, {}))
+        q_gpsimd.append((("ADD", LAST - 1), add_chunk, (LAST - 1, 2, M_TILES), (("TCH", LAST - 1),), {}, {"big": 1}))
 
         q_sync = [e_lq(0, 0), e_lk(0, 0), e_lq(0, 1), e_lk(0, 1), e_lk(0, 2), e_lq(0, 2), e_lk(0, 3), e_lx(0), e_lk(1, 0), e_lx(1), e_lq(0, 3),
                   e_lk(1, 1), e_lx(2), e_lk(1, 3), e_lx(3), e_lk(2, 0), e_lk(2, 1), e_lq(1, 0), e_lk(2, 2), e_lq(1, 1), e_lk(1, 2), e_lq(1, 2), e_lq(1, 3), e_lk(2, 3)]
         q_sync.extend([e_lq(2, g) for g in range(PASSES)])
         for g in range(PASSES):
             q_sync.extend((e_lk(3, g), e_lq(3, g)))
-        q_sync.extend([(("ST", c), store_chunk, (c,), (("ADD", c),), {}, {"big": 1}) for c in range(LAST)])
+        q_sync.extend([(("ST", c), store_chunk, (c,), (("ADD", c),), {}, {"big": 1}) for c in range(LAST - 1)])
+        q_sync.append((("STa", LAST - 1), store_chunk, (LAST - 1, 0, 2), (("ADDa", LAST - 1),), {}, {}))
+        q_sync.append((("ST", LAST - 1), store_chunk, (LAST - 1, 2, M_TILES), (("ADD", LAST - 1),), {}, {"big": 1}))
         q_sync.extend([(("SB", m), store_bank, (LAST, m), (("AB", m),), {}, {}) for m in range(M_TILES)])
 
         room = {"wqb": RAW_BUFS, "wkr": RAW_BUFS, "big": BIG_BUFS, "wide": WIDE_BUFS, "il": BANKS, "acc": BANKS,

@@ -27,17 +27,17 @@ HEADS_PER_CHUNK = NW // HD
 
 FLOPS = 2 * 2 * S * D * D
 
-RAW_BUFS = 12
-GK_BUFS = 9
+WK_BUFS = 12
+WQ_BUFS = 10
+GK_BUFS = 8
 GQ_BUFS = 6
 WIDE_BUFS = 4
-CODE_BUFS = 4
+CODE_BUFS = {"k": 8, "q": 4}
 BIG_BUFS = 6
 BANKS = 4
 PE_PATH_PASSES = 3
-K_ON_SCALAR = ((2, 3), (3, 3))
-K_ON_GPSIMD = ((1, 2),)
-HEAD_KI = 6
+K_ON_SCALAR = ((3, 3),)
+K_ON_GPSIMD = ((2, 2),)
 STEP_KI = 2
 SEQ = tuple([(w, n) for n in range(CHUNKS) for w in ("k", "q")])
 LAST = len(SEQ) - 1
@@ -61,7 +61,7 @@ def tile_attention_pa_kernel(tc, x, freqs_cos, freqs_sin, wq_bytes, wq_scale, wk
         const = ctx.enter_context(tc.tile_pool(name="const", bufs=1))
         raw = ctx.enter_context(tc.tile_pool(name="raw", bufs=1))
         stage = ctx.enter_context(tc.tile_pool(name="stage", bufs=1))
-        codes_pool = ctx.enter_context(tc.tile_pool(name="codes", bufs=CODE_BUFS))
+        codes_pool = ctx.enter_context(tc.tile_pool(name="codes", bufs=1))
         big = ctx.enter_context(tc.tile_pool(name="big", bufs=BIG_BUFS))
         psum = ctx.enter_context(tc.psum_pool(name="psum", bufs=BANKS))
         ctx.enter_context(tc.manual_schedule())
@@ -100,12 +100,12 @@ def tile_attention_pa_kernel(tc, x, freqs_cos, freqs_sin, wq_bytes, wq_scale, wk
         shape4 = [P, HEADS_PER_CHUNK, HALF, 2]
 
         def load_wq(n, g):
-            tq = raw.tile([P, PACK, NW], U8, name="wqb", tag="wqb", bufs=RAW_BUFS)
+            tq = raw.tile([P, PACK, NW], U8, name="wqb", tag="wqb", bufs=WQ_BUFS)
             nc.sync.dma_start(out=tq[:], in_=wqb_v[g][:, :, n * NW:(n + 1) * NW])
             wqb[(n, g)] = tq
 
         def load_wk(n, g):
-            tk = raw.tile([P, PACK, NW], BF16, name="wkr", tag="wkr", bufs=RAW_BUFS)
+            tk = raw.tile([P, PACK, NW], BF16, name="wkr", tag="wkr", bufs=WK_BUFS)
             nc.sync.dma_start(out=tk[:], in_=wk_v[g][:, :, n * NW:(n + 1) * NW])
             wkr[(n, g)] = tk
 
@@ -193,8 +193,8 @@ def tile_attention_pa_kernel(tc, x, freqs_cos, freqs_sin, wq_bytes, wq_scale, wk
             grouped[("k", n, g)] = gk
 
         def quant(w, n, g):
-            c = codes_pool.tile([P, NW], U32, name=w + "c", tag=w + "c", align_bytes=64)
-            s = codes_pool.tile([P, NW], U8, name=w + "s", tag=w + "s", align_bytes=64)
+            c = codes_pool.tile([P, NW], U32, name=w + "c", tag=w + "c", bufs=CODE_BUFS[w], align_bytes=64)
+            s = codes_pool.tile([P, NW], U8, name=w + "s", tag=w + "s", bufs=CODE_BUFS[w], align_bytes=64)
             nc.vector.quantize_mx(out=c[:].bitcast(FP8X4), scales=s[:], in_=grouped[(w, n, g)][:].rearrange("p c t -> p (c t)"))
             ops[(w, n, g)] = (c, s)
 
@@ -306,42 +306,34 @@ def tile_attention_pa_kernel(tc, x, freqs_cos, freqs_sin, wq_bytes, wq_scale, wk
         every = tuple(range(PASSES))
         vk = [(n, g) for n in range(CHUNKS) for g in range(PASSES) if (n, g) not in K_ON_SCALAR and (n, g) not in K_ON_GPSIMD]
 
+        first = [(n, g) for n in range(2) for g in every]
         q_vector = [(("SIN",), sin_table, (), (), {}, {}), e_ki(0, 0)]
-        for g in range(PASSES):
-            q_vector.append(e_ki(vk[g + 1][0], vk[g + 1][1]))
-            q_vector.append(e_q("k", 0, g))
-        rest = vk[PASSES + 1:]
-        head = rest[:HEAD_KI - 1]
-        rest = rest[HEAD_KI - 1:]
-        q_vector.extend([e_ki(u[0], u[1]) for u in head[:2]])
-        q_vector.extend((e_xq(0), e_xq(1)))
-        q_vector.extend([e_ki(u[0], u[1]) for u in head[2:4]])
-        q_vector.extend((e_xq(2), e_xq(3)))
-        q_vector.extend([e_ki(u[0], u[1]) for u in head[4:]])
+        for j in range(1, len(first)):
+            q_vector.extend((e_ki(first[j][0], first[j][1]), e_q("k", first[j - 1][0], first[j - 1][1])))
+        q_vector.extend((e_xq(0), e_xq(1), e_q("k", 1, PASSES - 1)))
+        rest = [u for u in vk if u not in first]
+        phase = [e_q("q", 0, g) for g in every[1:]] + [e_xq(2), e_xq(3), e_q("q", 0, 0)]
         for c in range(len(SEQ)):
             tch = [(("TCH", c - 1), touch, (c - 1,), (("ROT", c - 1, M_TILES - 1),), {}, {})] if c > 0 else []
-            if c < LAST:
-                w, n = SEQ[c + 1]
-                q_vector.extend([e_q(w, n, g) for g in (every[1:-1] if c + 1 == LAST else every[1:])])
-                q_vector.extend(tch)
-                q_vector.append(e_q(w, n, 0))
-            else:
-                q_vector.extend(tch)
+            q_vector.extend((phase + tch) if c == LAST else (phase[:-1] + tch + phase[-1:]))
             q_vector.extend([e_rot(c, m) for m in range(M_TILES)])
-            if c + 1 == LAST:
-                q_vector.append(e_q(w, n, PASSES - 1))
-            q_vector.extend([e_ki(u[0], u[1]) for u in rest[:STEP_KI]])
+            phase = [e_ki(u[0], u[1]) for u in rest[:STEP_KI]]
             rest = rest[STEP_KI:]
+            if c + 2 <= LAST and c + 2 > 2:
+                w, n = SEQ[c + 2]
+                phase.extend([e_q(w, n, g) for g in (every[1:-1] if c + 2 == LAST else every[1:])] + [e_q(w, n, 0)])
+            if c + 1 == LAST:
+                phase = [e_q(SEQ[LAST][0], SEQ[LAST][1], PASSES - 1)]
         q_vector.extend([(("AB", m), add_bank, (LAST, m), (("ROT", LAST, m),), {}, {}) for m in range(M_TILES)])
 
-        q_scalar = [e_w(0, 0), e_w(0, 1), e_w(0, 2), e_ev(0, 0), e_ev(0, 1), e_xe(0), e_xe(1), e_w(0, 3), e_ev(0, 2), e_xe(2), e_xe(3), e_qd(0, 3)]
+        q_scalar = [e_w(0, 0), e_w(0, 1), e_w(0, 2), e_ev(0, 0), e_ev(0, 1), e_w(0, 3), e_ev(0, 2), e_xe(0), e_xe(1), e_qd(0, 3), e_xe(2), e_xe(3)]
         for n in range(1, CHUNKS):
             q_scalar.extend((e_w(n, 0), e_w(n, 1)))
             q_scalar.extend([e_ki(u[0], u[1]) for u in K_ON_SCALAR if u[0] == n])
             q_scalar.extend((e_ev(n, 0), e_ev(n, 1), e_w(n, 2), e_w(n, 3)))
             q_scalar.extend((e_qd(n, 3), e_ev(n, 2)) if n < CHUNKS - 1 else (e_ev(n, 2), e_qd(n, 3)))
 
-        q_tensor = [e_pi(0, 0), e_pi(0, 1), e_xt(0), e_xt(1), e_pi(0, 2), e_xt(2), e_xt(3)]
+        q_tensor = [e_pi(0, 0), e_pi(0, 1), e_pi(0, 2), e_xt(0), e_xt(1), e_xt(2), e_xt(3)]
         q_tensor.extend([e_mm(0, m, every) for m in range(M_TILES)])
         q_tensor.extend((e_pi(1, 0), e_pi(1, 1)))
         for c in range(LAST):
@@ -364,8 +356,8 @@ def tile_attention_pa_kernel(tc, x, freqs_cos, freqs_sin, wq_bytes, wq_scale, wk
         q_gpsimd.append((("ADDa", LAST - 1), add_chunk, (LAST - 1, 0, 2), (("TCH", LAST - 1),), {}, {}))
         q_gpsimd.append((("ADD", LAST - 1), add_chunk, (LAST - 1, 2, M_TILES), (("TCH", LAST - 1),), {}, {"big": 1}))
 
-        q_sync = [e_lq(0, 0), e_lk(0, 0), e_lq(0, 1), e_lk(0, 1), e_lk(0, 2), e_lq(0, 2), e_lk(0, 3), e_lx(0), e_lk(1, 0), e_lx(1), e_lq(0, 3),
-                  e_lk(1, 1), e_lx(2), e_lk(1, 3), e_lx(3), e_lk(2, 0), e_lk(2, 1), e_lq(1, 0), e_lk(2, 2), e_lq(1, 1), e_lk(1, 2), e_lq(1, 2), e_lq(1, 3), e_lk(2, 3)]
+        q_sync = [e_lq(0, 0), e_lk(0, 0), e_lq(0, 1), e_lk(0, 1), e_lk(0, 2), e_lq(0, 2), e_lk(0, 3), e_lk(1, 0), e_lq(0, 3), e_lk(1, 1), e_lk(1, 2),
+                  e_lx(0), e_lx(1), e_lk(1, 3), e_lx(2), e_lx(3), e_lk(2, 0), e_lk(2, 1), e_lq(1, 0), e_lq(1, 1), e_lk(2, 2), e_lq(1, 2), e_lq(1, 3), e_lk(2, 3)]
         q_sync.extend([e_lq(2, g) for g in range(PASSES)])
         for g in range(PASSES):
             q_sync.extend((e_lk(3, g), e_lq(3, g)))
@@ -374,8 +366,8 @@ def tile_attention_pa_kernel(tc, x, freqs_cos, freqs_sin, wq_bytes, wq_scale, wk
         q_sync.append((("ST", LAST - 1), store_chunk, (LAST - 1, 2, M_TILES), (("ADD", LAST - 1),), {}, {"big": 1}))
         q_sync.extend([(("SB", m), store_bank, (LAST, m), (("AB", m),), {}, {}) for m in range(M_TILES)])
 
-        room = {"wqb": RAW_BUFS, "wkr": RAW_BUFS, "big": BIG_BUFS, "wide": WIDE_BUFS, "il": BANKS, "acc": BANKS,
-                "gq": GQ_BUFS, "gk": GK_BUFS, "kc": CODE_BUFS, "qc": CODE_BUFS}
+        room = {"wqb": WQ_BUFS, "wkr": WK_BUFS, "big": BIG_BUFS, "wide": WIDE_BUFS, "il": BANKS, "acc": BANKS,
+                "gq": GQ_BUFS, "gk": GK_BUFS, "kc": CODE_BUFS["k"], "qc": CODE_BUFS["q"]}
         queues = [q_sync, q_scalar, q_tensor, q_vector, q_gpsimd]
         at = [0] * len(queues)
         written = set()

@@ -36,7 +36,7 @@ CODE_BUFS = {"k": 8, "q": 4}
 BIG_BUFS = 6
 BANKS = 4
 PE_PATH_PASSES = 3
-K_ON_SCALAR = ((3, 3),)
+K_ON_SCALAR = ((2, 3), (3, 3))
 K_ON_GPSIMD = ((2, 2),)
 STEP_KI = 2
 SEQ = tuple([(w, n) for n in range(CHUNKS) for w in ("k", "q")])
@@ -330,8 +330,8 @@ def tile_attention_pa_kernel(tc, x, freqs_cos, freqs_sin, wq_bytes, wq_scale, wk
         for n in range(1, CHUNKS):
             q_scalar.extend((e_w(n, 0), e_w(n, 1)))
             q_scalar.extend([e_ki(u[0], u[1]) for u in K_ON_SCALAR if u[0] == n])
-            q_scalar.extend((e_ev(n, 0), e_ev(n, 1), e_w(n, 2), e_w(n, 3)))
-            q_scalar.extend((e_qd(n, 3), e_ev(n, 2)) if n < CHUNKS - 1 else (e_ev(n, 2), e_qd(n, 3)))
+            q_scalar.extend((e_w(n, 2), e_ev(n, 0), e_ev(n, 1)))
+            q_scalar.extend((e_w(n, 3), e_qd(n, 3), e_ev(n, 2)) if n < CHUNKS - 1 else (e_w(n, 3), e_ev(n, 2), e_qd(n, 3)))
 
         q_tensor = [e_pi(0, 0), e_pi(0, 1), e_pi(0, 2), e_xt(0), e_xt(1), e_xt(2), e_xt(3)]
         q_tensor.extend([e_mm(0, m, every) for m in range(M_TILES)])
@@ -356,8 +356,8 @@ def tile_attention_pa_kernel(tc, x, freqs_cos, freqs_sin, wq_bytes, wq_scale, wk
         q_gpsimd.append((("ADDa", LAST - 1), add_chunk, (LAST - 1, 0, 2), (("TCH", LAST - 1),), {}, {}))
         q_gpsimd.append((("ADD", LAST - 1), add_chunk, (LAST - 1, 2, M_TILES), (("TCH", LAST - 1),), {}, {"big": 1}))
 
-        q_sync = [e_lq(0, 0), e_lk(0, 0), e_lq(0, 1), e_lk(0, 1), e_lk(0, 2), e_lq(0, 2), e_lk(0, 3), e_lk(1, 0), e_lq(0, 3), e_lk(1, 1), e_lk(1, 2),
-                  e_lx(0), e_lx(1), e_lk(1, 3), e_lx(2), e_lx(3), e_lk(2, 0), e_lk(2, 1), e_lq(1, 0), e_lq(1, 1), e_lk(2, 2), e_lq(1, 2), e_lq(1, 3), e_lk(2, 3)]
+        q_sync = [e_lq(0, 0), e_lk(0, 0), e_lq(0, 1), e_lk(0, 1), e_lq(0, 2), e_lk(0, 2), e_lk(0, 3), e_lk(1, 0), e_lq(0, 3), e_lk(1, 1), e_lk(1, 2),
+                  e_lx(0), e_lx(1), e_lk(1, 3), e_lx(2), e_lx(3), e_lq(1, 0), e_lk(2, 0), e_lq(1, 1), e_lk(2, 1), e_lk(2, 2), e_lq(1, 2), e_lq(1, 3), e_lk(2, 3)]
         q_sync.extend([e_lq(2, g) for g in range(PASSES)])
         for g in range(PASSES):
             q_sync.extend((e_lk(3, g), e_lq(3, g)))

@@ -324,7 +324,8 @@ def tile_attention_pa_kernel(tc, x, freqs_cos, freqs_sin, wq_bytes, wq_scale, wk
                 phase.extend([e_q(w, n, g) for g in (every[1:-1] if c + 2 == LAST else every[1:])] + [e_q(w, n, 0)])
             if c + 1 == LAST:
                 phase = [e_q(SEQ[LAST][0], SEQ[LAST][1], PASSES - 1)]
-        q_vector.extend([(("AB", m), add_bank, (LAST, m), (("ROT", LAST, m),), {}, {}) for m in range(M_TILES)])
+                phase.extend([(("AV", m), add_bank, (c, m), (("ROT", c, m),), {}, {}) for m in range(2, M_TILES)])
+        q_vector.extend([(("AB", m), add_bank, (LAST, m), (("ROT", LAST, m),), {}, {}) for m in range(1, M_TILES)])
 
         q_scalar = [e_w(0, 0), e_w(0, 1), e_w(0, 2), e_ev(0, 0), e_ev(0, 1), e_w(0, 3), e_ev(0, 2), e_xe(0), e_xe(1), e_qd(0, 3), e_xe(2), e_xe(3)]
         for n in range(1, CHUNKS):
@@ -353,8 +354,8 @@ def tile_attention_pa_kernel(tc, x, freqs_cos, freqs_sin, wq_bytes, wq_scale, wk
         q_gpsimd.append((("TRG", 0), trigger, (0,), (("Q", w, n, 0),), {}, {}))
         q_gpsimd.extend([e_ki(u[0], u[1]) for u in K_ON_GPSIMD])
         q_gpsimd.extend([(("ADD", c), add_chunk, (c,), (("TCH", c),), {}, {"big": 1}) for c in range(LAST - 1)])
-        q_gpsimd.append((("ADDa", LAST - 1), add_chunk, (LAST - 1, 0, 2), (("TCH", LAST - 1),), {}, {}))
-        q_gpsimd.append((("ADD", LAST - 1), add_chunk, (LAST - 1, 2, M_TILES), (("TCH", LAST - 1),), {}, {"big": 1}))
+        q_gpsimd.append((("ADD", LAST - 1), add_chunk, (LAST - 1, 0, 2), (("TCH", LAST - 1),), {}, {"big": 1}))
+        q_gpsimd.append((("AB", 0), add_chunk, (LAST, 0, 1), (("ROT", LAST, 0),), {}, {}))
 
         q_sync = [e_lq(0, 0), e_lk(0, 0), e_lq(0, 1), e_lk(0, 1), e_lq(0, 2), e_lk(0, 2), e_lk(0, 3), e_lk(1, 0), e_lq(0, 3), e_lk(1, 1), e_lk(1, 2),
                   e_lx(0), e_lx(1), e_lk(1, 3), e_lx(2), e_lx(3), e_lq(1, 0), e_lk(2, 0), e_lq(1, 1), e_lk(2, 1), e_lk(2, 2), e_lq(1, 2), e_lq(1, 3), e_lk(2, 3)]
@@ -362,8 +363,8 @@ def tile_attention_pa_kernel(tc, x, freqs_cos, freqs_sin, wq_bytes, wq_scale, wk
         for g in range(PASSES):
             q_sync.extend((e_lk(3, g), e_lq(3, g)))
         q_sync.extend([(("ST", c), store_chunk, (c,), (("ADD", c),), {}, {"big": 1}) for c in range(LAST - 1)])
-        q_sync.append((("STa", LAST - 1), store_chunk, (LAST - 1, 0, 2), (("ADDa", LAST - 1),), {}, {}))
-        q_sync.append((("ST", LAST - 1), store_chunk, (LAST - 1, 2, M_TILES), (("ADD", LAST - 1),), {}, {"big": 1}))
+        q_sync.append((("STa", LAST - 1), store_chunk, (LAST - 1, 2, M_TILES), (("AV", M_TILES - 1),), {}, {}))
+        q_sync.append((("ST", LAST - 1), store_chunk, (LAST - 1, 0, 2), (("ADD", LAST - 1),), {}, {"big": 1}))
         q_sync.extend([(("SB", m), store_bank, (LAST, m), (("AB", m),), {}, {}) for m in range(M_TILES)])
 
         room = {"wqb": WQ_BUFS, "wkr": WK_BUFS, "big": BIG_BUFS, "wide": WIDE_BUFS, "il": BANKS, "acc": BANKS,

@@ -38,6 +38,7 @@ BANKS = 4
 PE_PATH_PASSES = 3
 K_ON_SCALAR = ((2, 3), (3, 3))
 K_ON_GPSIMD = ((2, 2),)
+RUN = 8
 STEP_KI = 2
 SEQ = tuple([(w, n) for n in range(CHUNKS) for w in ("k", "q")])
 LAST = len(SEQ) - 1
@@ -147,7 +148,7 @@ def tile_attention_pa_kernel(tc, x, freqs_cos, freqs_sin, wq_bytes, wq_scale, wk
             xs[m] = s
 
         def direct(copy, dst, src):
-            copy(out=dst[:].rearrange("p (c i) t -> p c t i", i=4), in_=src[:].rearrange("p t (c i) -> p c t i", i=4))
+            copy(out=dst[:].rearrange("p (c i) t -> p c t i", i=RUN), in_=src[:].rearrange("p t (c i) -> p c t i", i=RUN))
 
         def widen(n, g):
             wide = stage.tile([P, PACK, NW], BF16, name="wide", tag="wide", bufs=WIDE_BUFS)

@@ -116,8 +116,8 @@ def tile_attention_pa_kernel(tc, x, freqs_cos, freqs_sin, wq_bytes, wq_scale, wk
             xr[m] = t
 
         def sin_table():
-            nc.vector.tensor_scalar(out=sinT[:, :, :, 0], in0=sin_sb[:], scalar1=-1.0, scalar2=None, op0=ALU.mult)
-            nc.vector.tensor_copy(out=sinT[:, :, :, 1], in_=sin_sb[:])
+            nc.vector.tensor_copy(out=sinT[:, :, :, 0], in_=sin_sb[:])
+            nc.vector.tensor_scalar(out=sinT[:, :, :, 1], in0=sin_sb[:], scalar1=-1.0, scalar2=None, op0=ALU.mult)
 
         def x_tag(m):
             return "il" if m == 2 else "acc"
@@ -227,7 +227,7 @@ def tile_attention_pa_kernel(tc, x, freqs_cos, freqs_sin, wq_bytes, wq_scale, wk
             p1, p2 = prod[c][0][:, m, :], prod[c][1][:, m, :]
             a4 = as4(acc_t[(c, m)][:])
             nc.vector.tensor_tensor(out=as4(p1), in0=a4, in1=cos_sb[:, m].unsqueeze(1).unsqueeze(3).to_broadcast(shape4), op=ALU.mult)
-            nc.vector.tensor_tensor(out=as4(p2), in0=a4[:, :, :, ::-1], in1=sinT[:, m].unsqueeze(1).to_broadcast(shape4), op=ALU.mult)
+            nc.vector.tensor_tensor(out=as4(p2), in0=a4, in1=sinT[:, m].unsqueeze(1).to_broadcast(shape4), op=ALU.mult)
 
         def trigger(c):
             w, n = SEQ[c + 1]
@@ -237,17 +237,19 @@ def tile_attention_pa_kernel(tc, x, freqs_cos, freqs_sin, wq_bytes, wq_scale, wk
             word = prod[c][1][:, 0, 0:1]
             nc.vector.tensor_copy(out=word, in_=word)
 
+        def add_swapped(engine, c, m0, m1):
+            p1, p2 = [t[:, m0:m1, :].rearrange("p m (j e) -> p (m j) e", e=2) for t in prod[c]]
+            engine.tensor_tensor(out=p1, in0=p1, in1=p2[:, :, ::-1], op=ALU.add)
+
         def add_chunk(c, m0=0, m1=M_TILES):
-            p1, p2 = prod[c]
-            nc.gpsimd.tensor_tensor(out=p1[:, m0:m1, :], in0=p1[:, m0:m1, :], in1=p2[:, m0:m1, :], op=ALU.add)
+            add_swapped(nc.gpsimd, c, m0, m1)
 
         def store_chunk(c, m0=0, m1=M_TILES):
             w, n = SEQ[c]
             nc.sync.dma_start(out=outs_3d[w][:, m0:m1, n * NW:(n + 1) * NW], in_=prod[c][0][:, m0:m1, :])
 
         def add_bank(c, m):
-            p1, p2 = prod[c][0][:, m, :], prod[c][1][:, m, :]
-            nc.vector.tensor_tensor(out=p1, in0=p1, in1=p2, op=ALU.add)
+            add_swapped(nc.vector, c, m, m + 1)
 
         def store_bank(c, m):
             w, n = SEQ[c]

@@ -33,7 +33,7 @@ GK_BUFS = 8
 GQ_BUFS = 6
 WIDE_BUFS = 4
 CODE_BUFS = {"k": 8, "q": 4}
-BIG_BUFS = 6
+BIG_BUFS = 3
 BANKS = 4
 PE_PATH_PASSES = 3
 K_ON_SCALAR = ((2, 3), (3, 3))
@@ -83,7 +83,7 @@ def tile_attention_pa_kernel(tc, x, freqs_cos, freqs_sin, wq_bytes, wq_scale, wk
         make_identity(nc, ident[:])
         ident_bf = const.tile([P, P], BF16, name="ident_bf")
         make_identity(nc, ident_bf[:])
-        sinT = const.tile([P, M_TILES, HALF, 2], BF16, name="sinT")
+        tab = const.tile([P, M_TILES, 2, HALF, 2], BF16, name="tab")
 
         wqb = {}
         wkr = {}
@@ -98,7 +98,7 @@ def tile_attention_pa_kernel(tc, x, freqs_cos, freqs_sin, wq_bytes, wq_scale, wk
         ops = {}
         acc_t = {}
         prod = {}
-        shape4 = [P, HEADS_PER_CHUNK, HALF, 2]
+        shape4 = [P, 2, HEADS_PER_CHUNK, HD]
 
         def load_wq(n, g):
             tq = raw.tile([P, PACK, NW], U8, name="wqb", tag="wqb", bufs=WQ_BUFS)
@@ -111,19 +111,21 @@ def tile_attention_pa_kernel(tc, x, freqs_cos, freqs_sin, wq_bytes, wq_scale, wk
             wkr[(n, g)] = tk
 
         def load_x(m):
-            t = big.tile([P, D], BF16, name="xr", tag="big")
-            nc.sync.dma_start(out=t[:], in_=x_v[m])
-            xr[m] = t
+            if m == 0:
+                xr["all"] = big.tile([P, M_TILES, D], BF16, name="xr", tag="big")
+            xr[m] = xr["all"][:, m, :]
+            nc.sync.dma_start(out=xr[m], in_=x_v[m])
 
         def sin_table():
-            nc.vector.tensor_copy(out=sinT[:, :, :, 0], in_=sin_sb[:])
-            nc.vector.tensor_scalar(out=sinT[:, :, :, 1], in0=sin_sb[:], scalar1=-1.0, scalar2=None, op0=ALU.mult)
+            nc.vector.tensor_copy(out=tab[:, :, 0], in_=cos_sb[:].unsqueeze(3).to_broadcast([P, M_TILES, HALF, 2]))
+            nc.vector.tensor_copy(out=tab[:, :, 1, :, 0], in_=sin_sb[:])
+            nc.vector.tensor_scalar(out=tab[:, :, 1, :, 1], in0=sin_sb[:], scalar1=-1.0, scalar2=None, op0=ALU.mult)
 
         def x_tag(m):
             return "il" if m == 2 else "acc"
 
         def x_transpose(m):
-            words = xr[m][:].bitcast(F32)
+            words = xr[m].bitcast(F32)
             for half in range(2):
                 xt = psum.tile([P, NW], F32, name="xt", tag=x_tag(m))
                 for gl in range(2):
@@ -199,9 +201,6 @@ def tile_attention_pa_kernel(tc, x, freqs_cos, freqs_sin, wq_bytes, wq_scale, wk
             nc.vector.quantize_mx(out=c[:].bitcast(FP8X4), scales=s[:], in_=grouped[(w, n, g)][:].rearrange("p c t -> p (c t)"))
             ops[(w, n, g)] = (c, s)
 
-        def as4(ap):
-            return ap.rearrange("p (h i e) -> p h i e", h=HEADS_PER_CHUNK, e=2)
-
         def mm(c, m, gs):
             w, n = SEQ[c]
             if gs[0] == 0:
@@ -220,40 +219,39 @@ def tile_attention_pa_kernel(tc, x, freqs_cos, freqs_sin, wq_bytes, wq_scale, wk
 
         def rot(c, m):
             if m == 0:
-                prod[c] = (
-                    big.tile([P, M_TILES, NW], F32, name="p1", tag="big"),
-                    big.tile([P, M_TILES, NW], F32, name="p2", tag="big"),
-                )
-            p1, p2 = prod[c][0][:, m, :], prod[c][1][:, m, :]
-            a4 = as4(acc_t[(c, m)][:])
-            nc.vector.tensor_tensor(out=as4(p1), in0=a4, in1=cos_sb[:, m].unsqueeze(1).unsqueeze(3).to_broadcast(shape4), op=ALU.mult)
-            nc.vector.tensor_tensor(out=as4(p2), in0=a4, in1=sinT[:, m].unsqueeze(1).to_broadcast(shape4), op=ALU.mult)
+                prod[c] = big.tile([P, M_TILES, 2, NW], F32, name="prod", tag="big")
+            nc.vector.tensor_tensor(
+                out=prod[c][:, m].rearrange("p u (h d) -> p u h d", d=HD),
+                in0=acc_t[(c, m)][:].rearrange("p (h d) -> p h d", d=HD).unsqueeze(1).to_broadcast(shape4),
+                in1=tab[:, m].rearrange("p u i e -> p u (i e)").unsqueeze(2).to_broadcast(shape4),
+                op=ALU.mult,
+            )
 
         def trigger(c):
             w, n = SEQ[c + 1]
             nc.gpsimd.tensor_copy(out=junk[:], in_=ops[(w, n, 0)][0][:, 0:1])
 
         def touch(c):
-            word = prod[c][1][:, 0, 0:1]
+            word = prod[c][:, 0, 1, 0:1]
             nc.vector.tensor_copy(out=word, in_=word)
 
         def add_swapped(engine, c, m0, m1):
-            p1, p2 = [t[:, m0:m1, :].rearrange("p m (j e) -> p (m j) e", e=2) for t in prod[c]]
-            engine.tensor_tensor(out=p1, in0=p1, in1=p2[:, :, ::-1], op=ALU.add)
+            p1, p2 = [prod[c][:, m0:m1, u].rearrange("p m (j e) -> p m j e", e=2) for u in range(2)]
+            engine.tensor_tensor(out=p1, in0=p1, in1=p2[:, :, :, ::-1], op=ALU.add)
 
         def add_chunk(c, m0=0, m1=M_TILES):
             add_swapped(nc.gpsimd, c, m0, m1)
 
         def store_chunk(c, m0=0, m1=M_TILES):
             w, n = SEQ[c]
-            nc.sync.dma_start(out=outs_3d[w][:, m0:m1, n * NW:(n + 1) * NW], in_=prod[c][0][:, m0:m1, :])
+            nc.sync.dma_start(out=outs_3d[w][:, m0:m1, n * NW:(n + 1) * NW], in_=prod[c][:, m0:m1, 0])
 
         def add_bank(c, m):
             add_swapped(nc.vector, c, m, m + 1)
 
         def store_bank(c, m):
             w, n = SEQ[c]
-            nc.sync.dma_start(out=outs_v[w][m][:, n * NW:(n + 1) * NW], in_=prod[c][0][:, m, :])
+            nc.sync.dma_start(out=outs_v[w][m][:, n * NW:(n + 1) * NW], in_=prod[c][:, m, 0])
 
         def src_of(w, n, g):
             if w == "k":
@@ -267,7 +265,7 @@ def tile_attention_pa_kernel(tc, x, freqs_cos, freqs_sin, wq_bytes, wq_scale, wk
             return (("LK", n, g), load_wk, (n, g), (), {"wkr": 1}, {})
 
         def e_lx(m):
-            return (("LX", m), load_x, (m,), (), {"big": 1}, {})
+            return (("LX", m), load_x, (m,), (), {"big": 1} if m == 0 else {}, {})
 
         def e_w(n, g):
             return (("W", n, g), widen, (n, g), (("LQ", n, g),), {"wide": 1}, {"wqb": 1})
@@ -285,7 +283,7 @@ def tile_attention_pa_kernel(tc, x, freqs_cos, freqs_sin, wq_bytes, wq_scale, wk
             return (("KI", n, g), k_interleave, (n, g), (("LK", n, g),), {"gk": 1}, {"wkr": 1})
 
         def e_xt(m):
-            return (("XT", m), x_transpose, (m,), (("LX", m),), {x_tag(m): 2}, {"big": 1})
+            return (("XT", m), x_transpose, (m,), (("LX", m),), {x_tag(m): 2}, {"big": 1} if m == M_TILES - 1 else {})
 
         def e_xe(m):
             return (("XE", m), x_evac, (m,), (("XT", m),), {"gk": 1}, {x_tag(m): 2})
@@ -304,7 +302,7 @@ def tile_attention_pa_kernel(tc, x, freqs_cos, freqs_sin, wq_bytes, wq_scale, wk
             return (("MM", c, m, gs[-1]), mm, (c, m, gs), need, takes, gives)
 
         def e_rot(c, m):
-            return (("ROT", c, m), rot, (c, m), (("MM", c, m, PASSES - 1),), {"big": 2} if m == 0 else {}, {("il" if c == LAST else "acc"): 1})
+            return (("ROT", c, m), rot, (c, m), (("MM", c, m, PASSES - 1),), {"big": 1} if m == 0 else {}, {("il" if c == LAST else "acc"): 1})
 
         every = tuple(range(PASSES))
         vk = [(n, g) for n in range(CHUNKS) for g in range(PASSES) if (n, g) not in K_ON_SCALAR and (n, g) not in K_ON_GPSIMD]
@@ -356,8 +354,8 @@ def tile_attention_pa_kernel(tc, x, freqs_cos, freqs_sin, wq_bytes, wq_scale, wk
         w, n = SEQ[1]
         q_gpsimd.append((("TRG", 0), trigger, (0,), (("Q", w, n, 0),), {}, {}))
         q_gpsimd.extend([e_ki(u[0], u[1]) for u in K_ON_GPSIMD])
-        q_gpsimd.extend([(("ADD", c), add_chunk, (c,), (("TCH", c),), {}, {"big": 1}) for c in range(LAST - 1)])
-        q_gpsimd.append((("ADD", LAST - 1), add_chunk, (LAST - 1, 0, 2), (("TCH", LAST - 1),), {}, {"big": 1}))
+        q_gpsimd.extend([(("ADD", c), add_chunk, (c,), (("TCH", c),), {}, {}) for c in range(LAST - 1)])
+        q_gpsimd.append((("ADD", LAST - 1), add_chunk, (LAST - 1, 0, 2), (("TCH", LAST - 1),), {}, {}))
         q_gpsimd.append((("AB", 0), add_chunk, (LAST, 0, 1), (("ROT", LAST, 0),), {}, {}))
 
         q_sync = [e_lq(0, 0), e_lk(0, 0), e_lq(0, 1), e_lk(0, 1), e_lq(0, 2), e_lk(0, 2), e_lk(0, 3), e_lk(1, 0), e_lq(0, 3), e_lk(1, 1), e_lk(1, 2),

@@ -36,7 +36,7 @@ CODE_BUFS = {"k": 8, "q": 4}
 BIG_BUFS = 3
 BANKS = 4
 PE_PATH_PASSES = 3
-K_ON_SCALAR = ((2, 3), (3, 3))
+K_ON_SCALAR = ((3, 3),)
 K_ON_GPSIMD = ((2, 2),)
 RUN = 8
 STEP_KI = 2

@@ -35,8 +35,8 @@ WIDE_BUFS = 4
 CODE_BUFS = {"k": 8, "q": 4}
 BIG_BUFS = 3
 BANKS = 4
-PE_PATH_PASSES = 3
-K_ON_SCALAR = ((3, 3),)
+PE_PASSES = (3, 3, 2, 2)
+K_ON_SCALAR = ()
 K_ON_GPSIMD = ((2, 2),)
 RUN = 8
 STEP_KI = 2
@@ -256,7 +256,7 @@ def tile_attention_pa_kernel(tc, x, freqs_cos, freqs_sin, wq_bytes, wq_scale, wk
         def src_of(w, n, g):
             if w == "k":
                 return ("KI", n, g)
-            return ("EV", n, g) if g < PE_PATH_PASSES else ("QD", n, g)
+            return ("EV", n, g) if g < PE_PASSES[n] else ("QD", n, g)
 
         def e_lq(n, g):
             return (("LQ", n, g), load_wq, (n, g), (), {"wqb": 1}, {})
@@ -328,12 +328,15 @@ def tile_attention_pa_kernel(tc, x, freqs_cos, freqs_sin, wq_bytes, wq_scale, wk
                 phase.extend([(("AV", m), add_bank, (c, m), (("ROT", c, m),), {}, {}) for m in range(2, M_TILES)])
         q_vector.extend([(("AB", m), add_bank, (LAST, m), (("ROT", LAST, m),), {}, {}) for m in range(1, M_TILES)])
 
-        q_scalar = [e_w(0, 0), e_w(0, 1), e_w(0, 2), e_ev(0, 0), e_ev(0, 1), e_w(0, 3), e_ev(0, 2), e_xe(0), e_xe(1), e_qd(0, 3), e_xe(2), e_xe(3)]
+        def out_of(n, g):
+            return e_ev(n, g) if g < PE_PASSES[n] else e_qd(n, g)
+
+        q_scalar = [e_w(0, 0), e_w(0, 1), e_w(0, 2), out_of(0, 0), out_of(0, 1), e_w(0, 3), out_of(0, 2), e_xe(0), e_xe(1), e_qd(0, 3), e_xe(2), e_xe(3)]
         for n in range(1, CHUNKS):
             q_scalar.extend((e_w(n, 0), e_w(n, 1)))
             q_scalar.extend([e_ki(u[0], u[1]) for u in K_ON_SCALAR if u[0] == n])
-            q_scalar.extend((e_w(n, 2), e_ev(n, 0), e_ev(n, 1)))
-            q_scalar.extend((e_w(n, 3), e_qd(n, 3), e_ev(n, 2)) if n < CHUNKS - 1 else (e_w(n, 3), e_ev(n, 2), e_qd(n, 3)))
+            q_scalar.extend((e_w(n, 2), out_of(n, 0), out_of(n, 1)))
+            q_scalar.extend((e_w(n, 3), e_qd(n, 3), out_of(n, 2)) if n < CHUNKS - 1 else (e_w(n, 3), out_of(n, 2), e_qd(n, 3)))
 
         q_tensor = [e_pi(0, 0), e_pi(0, 1), e_pi(0, 2), e_xt(0), e_xt(1), e_xt(2), e_xt(3)]
         q_tensor.extend([e_mm(0, m, every) for m in range(M_TILES)])
@@ -349,6 +352,8 @@ def tile_attention_pa_kernel(tc, x, freqs_cos, freqs_sin, wq_bytes, wq_scale, wk
                 q_tensor.append(e_pi(n + 1, 2))
             if w == "q" and n + 2 < CHUNKS:
                 q_tensor.extend((e_pi(n + 2, 0), e_pi(n + 2, 1)))
+
+        q_tensor = [e for e in q_tensor if e[0][0] != "PI" or e[0][2] < PE_PASSES[e[0][1]]]
 
         q_gpsimd = []
         w, n = SEQ[1]

@@ -36,9 +36,10 @@ CODE_BUFS = {"k": 8, "q": 4}
 BIG_BUFS = 3
 BANKS = 4
 PE_PASSES = (3, 3, 2, 2)
-K_ON_SCALAR = ()
+K_ON_SCALAR = ((3, 3),)
 K_ON_GPSIMD = ((2, 2),)
 RUN = 8
+LATE = 2
 STEP_KI = 2
 SEQ = tuple([(w, n) for n in range(CHUNKS) for w in ("k", "q")])
 LAST = len(SEQ) - 1
@@ -322,9 +323,9 @@ def tile_attention_pa_kernel(tc, x, freqs_cos, freqs_sin, wq_bytes, wq_scale, wk
             rest = rest[STEP_KI:]
             if c + 2 <= LAST and c + 2 > 2:
                 w, n = SEQ[c + 2]
-                phase.extend([e_q(w, n, g) for g in (every[1:-1] if c + 2 == LAST else every[1:])] + [e_q(w, n, 0)])
+                phase.extend([e_q(w, n, g) for g in (every[1:LATE] if c + 2 == LAST else every[1:])] + [e_q(w, n, 0)])
             if c + 1 == LAST:
-                phase = [e_q(SEQ[LAST][0], SEQ[LAST][1], PASSES - 1)]
+                phase = [e_q(SEQ[LAST][0], SEQ[LAST][1], g) for g in every[LATE:]]
                 phase.extend([(("AV", m), add_bank, (c, m), (("ROT", c, m),), {}, {}) for m in range(2, M_TILES)])
         q_vector.extend([(("AB", m), add_bank, (LAST, m), (("ROT", LAST, m),), {}, {}) for m in range(1, M_TILES)])
 
@@ -346,8 +347,8 @@ def tile_attention_pa_kernel(tc, x, freqs_cos, freqs_sin, wq_bytes, wq_scale, wk
             if c + 1 < LAST:
                 q_tensor.extend([e_mm(c + 1, m, every) for m in range(M_TILES)])
             else:
-                q_tensor.extend([e_mm(LAST, m, every[:-1]) for m in range(M_TILES)])
-                q_tensor.extend([e_mm(LAST, m, every[-1:]) for m in range(M_TILES)])
+                q_tensor.extend([e_mm(LAST, m, every[:LATE]) for m in range(M_TILES)])
+                q_tensor.extend([e_mm(LAST, m, every[LATE:]) for m in range(M_TILES)])
             if w == "k" and n + 1 < CHUNKS:
                 q_tensor.append(e_pi(n + 1, 2))
             if w == "q" and n + 2 < CHUNKS:

@@ -71,9 +71,7 @@ def tile_attention_pa_kernel(tc, x, freqs_cos, freqs_sin, wq_bytes, wq_scale, wk
         sc = const.tile([P, PASSES, PACK], F32, name="sc")
         nc.scalar.dma_start(out=sc[:], in_=wq_scale.rearrange("(g p t) o -> p g (t o)", p=P, t=PACK))
         cos_sb = const.tile([P, M_TILES, HALF], BF16, name="cos_sb")
-        nc.scalar.dma_start(out=cos_sb[:], in_=freqs_cos.rearrange("(m p) i -> p m i", p=P))
         sin_sb = const.tile([P, M_TILES, HALF], BF16, name="sin_sb")
-        nc.scalar.dma_start(out=sin_sb[:], in_=freqs_sin.rearrange("(m p) i -> p m i", p=P))
 
         warm = const.tile([P, 2], F32, name="warm")
         nc.vector.memset(warm[:, 0:1], 0.0)
@@ -116,6 +114,10 @@ def tile_attention_pa_kernel(tc, x, freqs_cos, freqs_sin, wq_bytes, wq_scale, wk
                 xr["all"] = big.tile([P, M_TILES, D], BF16, name="xr", tag="big")
             xr[m] = xr["all"][:, m, :]
             nc.sync.dma_start(out=xr[m], in_=x_v[m])
+
+        def load_angles():
+            nc.sync.dma_start(out=cos_sb[:], in_=freqs_cos.rearrange("(m p) i -> p m i", p=P))
+            nc.sync.dma_start(out=sin_sb[:], in_=freqs_sin.rearrange("(m p) i -> p m i", p=P))
 
         def sin_table():
             nc.vector.tensor_copy(out=tab[:, :, 0], in_=cos_sb[:].unsqueeze(3).to_broadcast([P, M_TILES, HALF, 2]))
@@ -236,8 +238,8 @@ def tile_attention_pa_kernel(tc, x, freqs_cos, freqs_sin, wq_bytes, wq_scale, wk
             word = prod[c][:, 0, 1, 0:1]
             nc.vector.tensor_copy(out=word, in_=word)
 
-        def add_swapped(engine, c, m0, m1):
-            p1, p2 = [prod[c][:, m0:m1, u].rearrange("p m (j e) -> p m j e", e=2) for u in range(2)]
+        def add_swapped(engine, c, m0, m1, c0=0, c1=NW):
+            p1, p2 = [prod[c][:, m0:m1, u, c0:c1].rearrange("p m (j e) -> p m j e", e=2) for u in range(2)]
             engine.tensor_tensor(out=p1, in0=p1, in1=p2[:, :, :, ::-1], op=ALU.add)
 
         def add_chunk(c, m0=0, m1=M_TILES):
@@ -247,12 +249,12 @@ def tile_attention_pa_kernel(tc, x, freqs_cos, freqs_sin, wq_bytes, wq_scale, wk
             w, n = SEQ[c]
             nc.sync.dma_start(out=outs_3d[w][:, m0:m1, n * NW:(n + 1) * NW], in_=prod[c][:, m0:m1, 0])
 
-        def add_bank(c, m):
-            add_swapped(nc.vector, c, m, m + 1)
+        def add_bank(c, m, c0=0, c1=NW):
+            add_swapped(nc.vector, c, m, m + 1, c0, c1)
 
-        def store_bank(c, m):
+        def store_bank(c, m, c0=0, c1=NW):
             w, n = SEQ[c]
-            nc.sync.dma_start(out=outs_v[w][m][:, n * NW:(n + 1) * NW], in_=prod[c][:, m, 0])
+            nc.sync.dma_start(out=outs_v[w][m][:, n * NW + c0:n * NW + c1], in_=prod[c][:, m, 0, c0:c1])
 
         def src_of(w, n, g):
             if w == "k":
@@ -309,7 +311,7 @@ def tile_attention_pa_kernel(tc, x, freqs_cos, freqs_sin, wq_bytes, wq_scale, wk
         vk = [(n, g) for n in range(CHUNKS) for g in range(PASSES) if (n, g) not in K_ON_SCALAR and (n, g) not in K_ON_GPSIMD]
 
         first = [(n, g) for n in range(2) for g in every]
-        q_vector = [(("SIN",), sin_table, (), (), {}, {}), e_ki(0, 0)]
+        q_vector = [e_ki(0, 0), (("SIN",), sin_table, (), (("LA",),), {}, {})]
         for j in range(1, len(first)):
             q_vector.extend((e_ki(first[j][0], first[j][1]), e_q("k", first[j - 1][0], first[j - 1][1])))
         q_vector.extend((e_xq(0), e_xq(1), e_q("k", 1, PASSES - 1)))
@@ -327,7 +329,8 @@ def tile_attention_pa_kernel(tc, x, freqs_cos, freqs_sin, wq_bytes, wq_scale, wk
             if c + 1 == LAST:
                 phase = [e_q(SEQ[LAST][0], SEQ[LAST][1], g) for g in every[LATE:]]
                 phase.extend([(("AV", m), add_bank, (c, m), (("ROT", c, m),), {}, {}) for m in range(2, M_TILES)])
-        q_vector.extend([(("AB", m), add_bank, (LAST, m), (("ROT", LAST, m),), {}, {}) for m in range(1, M_TILES)])
+        ends = [(m, 0, NW) for m in range(M_TILES - 1)] + [(M_TILES - 1, 0, NW // 2), (M_TILES - 1, NW // 2, NW)]
+        q_vector.extend([(("AB", m, c0), add_bank, (LAST, m, c0, c1), (("ROT", LAST, m),), {}, {}) for m, c0, c1 in ends[1:]])
 
         def out_of(n, g):
             return e_ev(n, g) if g < PE_PASSES[n] else e_qd(n, g)
@@ -362,9 +365,9 @@ def tile_attention_pa_kernel(tc, x, freqs_cos, freqs_sin, wq_bytes, wq_scale, wk
         q_gpsimd.extend([e_ki(u[0], u[1]) for u in K_ON_GPSIMD])
         q_gpsimd.extend([(("ADD", c), add_chunk, (c,), (("TCH", c),), {}, {}) for c in range(LAST - 1)])
         q_gpsimd.append((("ADD", LAST - 1), add_chunk, (LAST - 1, 0, 2), (("TCH", LAST - 1),), {}, {}))
-        q_gpsimd.append((("AB", 0), add_chunk, (LAST, 0, 1), (("ROT", LAST, 0),), {}, {}))
+        q_gpsimd.append((("AB", 0, 0), add_chunk, (LAST, 0, 1), (("ROT", LAST, 0),), {}, {}))
 
-        q_sync = [e_lq(0, 0), e_lk(0, 0), e_lq(0, 1), e_lk(0, 1), e_lq(0, 2), e_lk(0, 2), e_lk(0, 3), e_lk(1, 0), e_lq(0, 3), e_lk(1, 1), e_lk(1, 2),
+        q_sync = [e_lq(0, 0), e_lk(0, 0), (("LA",), load_angles, (), (), {}, {}), e_lq(0, 1), e_lk(0, 1), e_lq(0, 2), e_lk(0, 2), e_lk(0, 3), e_lk(1, 0), e_lq(0, 3), e_lk(1, 1), e_lk(1, 2),
                   e_lx(0), e_lx(1), e_lk(1, 3), e_lx(2), e_lx(3), e_lq(1, 0), e_lk(2, 0), e_lq(1, 1), e_lk(2, 1), e_lk(2, 2), e_lq(1, 2), e_lq(1, 3), e_lk(2, 3)]
         q_sync.extend([e_lq(2, g) for g in range(PASSES)])
         for g in range(PASSES):
@@ -372,7 +375,7 @@ def tile_attention_pa_kernel(tc, x, freqs_cos, freqs_sin, wq_bytes, wq_scale, wk
         q_sync.extend([(("ST", c), store_chunk, (c,), (("ADD", c),), {}, {"big": 1}) for c in range(LAST - 1)])
         q_sync.append((("STa", LAST - 1), store_chunk, (LAST - 1, 2, M_TILES), (("AV", M_TILES - 1),), {}, {}))
         q_sync.append((("ST", LAST - 1), store_chunk, (LAST - 1, 0, 2), (("ADD", LAST - 1),), {}, {"big": 1}))
-        q_sync.extend([(("SB", m), store_bank, (LAST, m), (("AB", m),), {}, {}) for m in range(M_TILES)])
+        q_sync.extend([(("SB", m, c0), store_bank, (LAST, m, c0, c1), (("AB", m, c0),), {}, {}) for m, c0, c1 in ends])
 
         room = {"wqb": WQ_BUFS, "wkr": WK_BUFS, "big": BIG_BUFS, "wide": WIDE_BUFS, "il": BANKS, "acc": BANKS,
                 "gq": GQ_BUFS, "gk": GK_BUFS, "kc": CODE_BUFS["k"], "qc": CODE_BUFS["q"]}

@@ -37,8 +37,9 @@ BIG_BUFS = 3
 BANKS = 4
 PE_PASSES = (3, 3, 2, 2)
 K_ON_SCALAR = ((3, 3),)
-K_ON_GPSIMD = ((2, 2),)
+K_ON_GPSIMD = {(2, 2): NW, (2, 3): NW // 2}
 RUN = 8
+Q_ORDER = (1, 3, 2)
 LATE = 2
 STEP_KI = 2
 SEQ = tuple([(w, n) for n in range(CHUNKS) for w in ("k", "q")])
@@ -153,7 +154,7 @@ def tile_attention_pa_kernel(tc, x, freqs_cos, freqs_sin, wq_bytes, wq_scale, wk
             xs[m] = s
 
         def direct(copy, dst, src):
-            copy(out=dst[:].rearrange("p (c i) t -> p c t i", i=RUN), in_=src[:].rearrange("p t (c i) -> p c t i", i=RUN))
+            copy(out=dst.rearrange("p (c i) t -> p c t i", i=RUN), in_=src.rearrange("p t (c i) -> p c t i", i=RUN))
 
         def widen(n, g):
             wide = stage.tile([P, PACK, NW], BF16, name="wide", tag="wide", bufs=WIDE_BUFS)
@@ -188,15 +189,23 @@ def tile_attention_pa_kernel(tc, x, freqs_cos, freqs_sin, wq_bytes, wq_scale, wk
                 nc.scalar.copy(out=flat[:, b * 2 * NW:(b + 1) * 2 * NW], in_=il_t[(n, g)][b][:])
 
         def q_direct(n, g):
-            direct(nc.scalar.copy, new_gq(n, g), wide_t[(n, g)])
+            direct(nc.scalar.copy, new_gq(n, g)[:], wide_t[(n, g)][:])
 
-        def k_interleave(n, g):
-            gk = stage.tile([P, NW, PACK], BF16, name="gk", tag="gk", bufs=GK_BUFS, align_bytes=64)
-            if (n, g) in K_ON_GPSIMD:
-                nc.gpsimd.tensor_scalar(out=gk[:], in0=wkr[(n, g)][:].rearrange("p t c -> p c t"), scalar1=1.0, scalar2=0.0, op0=ALU.mult, op1=ALU.add)
+        def k_interleave(n, g, on_gpsimd=0, c0=0):
+            if c0 == 0:
+                grouped[("k", n, g)] = stage.tile([P, NW, PACK], BF16, name="gk", tag="gk", bufs=GK_BUFS, align_bytes=64)
+            gk = grouped[("k", n, g)]
+            if c0 < on_gpsimd:
+                nc.gpsimd.tensor_scalar(
+                    out=gk[:, c0:on_gpsimd, :],
+                    in0=wkr[(n, g)][:, :, c0:on_gpsimd].rearrange("p t c -> p c t"),
+                    scalar1=1.0,
+                    scalar2=0.0,
+                    op0=ALU.mult,
+                    op1=ALU.add,
+                )
             else:
-                direct(nc.scalar.copy if (n, g) in K_ON_SCALAR else nc.vector.tensor_copy, gk, wkr[(n, g)])
-            grouped[("k", n, g)] = gk
+                direct(nc.scalar.copy if (n, g) in K_ON_SCALAR else nc.vector.tensor_copy, gk[:, c0:, :], wkr[(n, g)][:, :, c0:])
 
         def quant(w, n, g):
             c = codes_pool.tile([P, NW], U32, name=w + "c", tag=w + "c", bufs=CODE_BUFS[w], align_bytes=64)
@@ -231,8 +240,7 @@ def tile_attention_pa_kernel(tc, x, freqs_cos, freqs_sin, wq_bytes, wq_scale, wk
             )
 
         def trigger(c):
-            w, n = SEQ[c + 1]
-            nc.gpsimd.tensor_copy(out=junk[:], in_=ops[(w, n, 0)][0][:, 0:1])
+            nc.gpsimd.tensor_copy(out=junk[:], in_=xc[M_TILES - 1][:, 0:1])
 
         def touch(c):
             word = prod[c][:, 0, 1, 0:1]
@@ -283,7 +291,15 @@ def tile_attention_pa_kernel(tc, x, freqs_cos, freqs_sin, wq_bytes, wq_scale, wk
             return (("QD", n, g), q_direct, (n, g), (("W", n, g),), {"gq": 1}, {"wide": 1})
 
         def e_ki(n, g):
-            return (("KI", n, g), k_interleave, (n, g), (("LK", n, g),), {"gk": 1}, {"wkr": 1})
+            width = K_ON_GPSIMD.get((n, g), 0)
+            if width == 0:
+                return (("KI", n, g), k_interleave, (n, g), (("LK", n, g),), {"gk": 1}, {"wkr": 1})
+            return (("KI", n, g), k_interleave, (n, g, width, width), (("KG", n, g),), {}, {"wkr": 1})
+
+        def e_kg(n, g):
+            width = K_ON_GPSIMD[(n, g)]
+            whole = width == NW
+            return (("KI" if whole else "KG", n, g), k_interleave, (n, g, width), (("LK", n, g),), {"gk": 1}, {"wkr": 1} if whole else {})
 
         def e_xt(m):
             return (("XT", m), x_transpose, (m,), (("LX", m),), {x_tag(m): 2}, {"big": 1} if m == M_TILES - 1 else {})
@@ -308,7 +324,7 @@ def tile_attention_pa_kernel(tc, x, freqs_cos, freqs_sin, wq_bytes, wq_scale, wk
             return (("ROT", c, m), rot, (c, m), (("MM", c, m, PASSES - 1),), {"big": 1} if m == 0 else {}, {("il" if c == LAST else "acc"): 1})
 
         every = tuple(range(PASSES))
-        vk = [(n, g) for n in range(CHUNKS) for g in range(PASSES) if (n, g) not in K_ON_SCALAR and (n, g) not in K_ON_GPSIMD]
+        vk = [(n, g) for n in range(CHUNKS) for g in range(PASSES) if (n, g) not in K_ON_SCALAR and K_ON_GPSIMD.get((n, g), 0) < NW]
 
         first = [(n, g) for n in range(2) for g in every]
         q_vector = [e_ki(0, 0), (("SIN",), sin_table, (), (("LA",),), {}, {})]
@@ -316,7 +332,7 @@ def tile_attention_pa_kernel(tc, x, freqs_cos, freqs_sin, wq_bytes, wq_scale, wk
             q_vector.extend((e_ki(first[j][0], first[j][1]), e_q("k", first[j - 1][0], first[j - 1][1])))
         q_vector.extend((e_xq(0), e_xq(1), e_q("k", 1, PASSES - 1)))
         rest = [u for u in vk if u not in first]
-        phase = [e_q("q", 0, g) for g in every[1:]] + [e_xq(2), e_xq(3), e_q("q", 0, 0)]
+        phase = [e_q("q", 0, g) for g in Q_ORDER] + [e_xq(2), e_xq(3), e_q("q", 0, 0)]
         for c in range(len(SEQ)):
             tch = [(("TCH", c - 1), touch, (c - 1,), (("ROT", c - 1, M_TILES - 1),), {}, {})] if c > 0 else []
             q_vector.extend((phase + tch) if c == LAST else (phase[:-1] + tch + phase[-1:]))
@@ -325,7 +341,7 @@ def tile_attention_pa_kernel(tc, x, freqs_cos, freqs_sin, wq_bytes, wq_scale, wk
             rest = rest[STEP_KI:]
             if c + 2 <= LAST and c + 2 > 2:
                 w, n = SEQ[c + 2]
-                phase.extend([e_q(w, n, g) for g in (every[1:LATE] if c + 2 == LAST else every[1:])] + [e_q(w, n, 0)])
+                phase.extend([e_q(w, n, g) for g in (every[1:LATE] if c + 2 == LAST else Q_ORDER)] + [e_q(w, n, 0)])
             if c + 1 == LAST:
                 phase = [e_q(SEQ[LAST][0], SEQ[LAST][1], g) for g in every[LATE:]]
                 phase.extend([(("AV", m), add_bank, (c, m), (("ROT", c, m),), {}, {}) for m in range(2, M_TILES)])
@@ -360,15 +376,14 @@ def tile_attention_pa_kernel(tc, x, freqs_cos, freqs_sin, wq_bytes, wq_scale, wk
         q_tensor = [e for e in q_tensor if e[0][0] != "PI" or e[0][2] < PE_PASSES[e[0][1]]]
 
         q_gpsimd = []
-        w, n = SEQ[1]
-        q_gpsimd.append((("TRG", 0), trigger, (0,), (("Q", w, n, 0),), {}, {}))
-        q_gpsimd.extend([e_ki(u[0], u[1]) for u in K_ON_GPSIMD])
+        q_gpsimd.append((("TRG", 0), trigger, (0,), (("XQ", M_TILES - 1),), {}, {}))
+        q_gpsimd.extend([e_kg(u[0], u[1]) for u in K_ON_GPSIMD])
         q_gpsimd.extend([(("ADD", c), add_chunk, (c,), (("TCH", c),), {}, {}) for c in range(LAST - 1)])
         q_gpsimd.append((("ADD", LAST - 1), add_chunk, (LAST - 1, 0, 2), (("TCH", LAST - 1),), {}, {}))
         q_gpsimd.append((("AB", 0, 0), add_chunk, (LAST, 0, 1), (("ROT", LAST, 0),), {}, {}))
 
         q_sync = [e_lq(0, 0), e_lk(0, 0), (("LA",), load_angles, (), (), {}, {}), e_lq(0, 1), e_lk(0, 1), e_lq(0, 2), e_lk(0, 2), e_lk(0, 3), e_lk(1, 0), e_lq(0, 3), e_lk(1, 1), e_lk(1, 2),
-                  e_lx(0), e_lx(1), e_lk(1, 3), e_lx(2), e_lx(3), e_lq(1, 0), e_lk(2, 0), e_lq(1, 1), e_lk(2, 1), e_lk(2, 2), e_lq(1, 2), e_lq(1, 3), e_lk(2, 3)]
+                  e_lx(0), e_lx(1), e_lk(1, 3), e_lx(2), e_lx(3), e_lq(1, 0), e_lk(2, 2), e_lk(2, 3), e_lq(1, 1), e_lq(1, 2), e_lk(2, 0), e_lq(1, 3), e_lk(2, 1)]
         q_sync.extend([e_lq(2, g) for g in range(PASSES)])
         for g in range(PASSES):
             q_sync.extend((e_lk(3, g), e_lq(3, g)))

@@ -39,7 +39,6 @@ PE_PASSES = (3, 3, 2, 2)
 K_ON_SCALAR = ((3, 3),)
 K_ON_GPSIMD = {(2, 2): NW, (2, 3): NW // 2}
 RUN = 8
-Q_ORDER = (1, 3, 2)
 LATE = 2
 STEP_KI = 2
 SEQ = tuple([(w, n) for n in range(CHUNKS) for w in ("k", "q")])
@@ -326,13 +325,16 @@ def tile_attention_pa_kernel(tc, x, freqs_cos, freqs_sin, wq_bytes, wq_scale, wk
         every = tuple(range(PASSES))
         vk = [(n, g) for n in range(CHUNKS) for g in range(PASSES) if (n, g) not in K_ON_SCALAR and K_ON_GPSIMD.get((n, g), 0) < NW]
 
+        def order_of(w, n):
+            return (1, 3, 2) if w == "q" and PE_PASSES[n] == PASSES - 1 else (1, 2, 3)
+
         first = [(n, g) for n in range(2) for g in every]
         q_vector = [e_ki(0, 0), (("SIN",), sin_table, (), (("LA",),), {}, {})]
         for j in range(1, len(first)):
             q_vector.extend((e_ki(first[j][0], first[j][1]), e_q("k", first[j - 1][0], first[j - 1][1])))
         q_vector.extend((e_xq(0), e_xq(1), e_q("k", 1, PASSES - 1)))
         rest = [u for u in vk if u not in first]
-        phase = [e_q("q", 0, g) for g in Q_ORDER] + [e_xq(2), e_xq(3), e_q("q", 0, 0)]
+        phase = [e_q("q", 0, g) for g in order_of("q", 0)] + [e_xq(2), e_xq(3), e_q("q", 0, 0)]
         for c in range(len(SEQ)):
             tch = [(("TCH", c - 1), touch, (c - 1,), (("ROT", c - 1, M_TILES - 1),), {}, {})] if c > 0 else []
             q_vector.extend((phase + tch) if c == LAST else (phase[:-1] + tch + phase[-1:]))
@@ -341,7 +343,7 @@ def tile_attention_pa_kernel(tc, x, freqs_cos, freqs_sin, wq_bytes, wq_scale, wk
             rest = rest[STEP_KI:]
             if c + 2 <= LAST and c + 2 > 2:
                 w, n = SEQ[c + 2]
-                phase.extend([e_q(w, n, g) for g in (every[1:LATE] if c + 2 == LAST else Q_ORDER)] + [e_q(w, n, 0)])
+                phase.extend([e_q(w, n, g) for g in (every[1:LATE] if c + 2 == LAST else order_of(w, n))] + [e_q(w, n, 0)])
             if c + 1 == LAST:
                 phase = [e_q(SEQ[LAST][0], SEQ[LAST][1], g) for g in every[LATE:]]
                 phase.extend([(("AV", m), add_bank, (c, m), (("ROT", c, m),), {}, {}) for m in range(2, M_TILES)])
@@ -355,8 +357,13 @@ def tile_attention_pa_kernel(tc, x, freqs_cos, freqs_sin, wq_bytes, wq_scale, wk
         for n in range(1, CHUNKS):
             q_scalar.extend((e_w(n, 0), e_w(n, 1)))
             q_scalar.extend([e_ki(u[0], u[1]) for u in K_ON_SCALAR if u[0] == n])
-            q_scalar.extend((e_w(n, 2), out_of(n, 0), out_of(n, 1)))
-            q_scalar.extend((e_w(n, 3), e_qd(n, 3), out_of(n, 2)) if n < CHUNKS - 1 else (e_w(n, 3), out_of(n, 2), e_qd(n, 3)))
+            q_scalar.extend((e_w(n, 2), out_of(n, 0)))
+            if PE_PASSES[n] == PASSES - 1:
+                q_scalar.extend((out_of(n, 1), e_w(n, 3), e_qd(n, 3), out_of(n, 2)))
+            elif n < CHUNKS - 1:
+                q_scalar.extend((e_w(n, 3), out_of(n, 1), e_qd(n, 2), e_qd(n, 3)))
+            else:
+                q_scalar.extend((out_of(n, 1), e_w(n, 3), e_qd(n, 2), e_qd(n, 3)))
 
         q_tensor = [e_pi(0, 0), e_pi(0, 1), e_pi(0, 2), e_xt(0), e_xt(1), e_xt(2), e_xt(3)]
         q_tensor.extend([e_mm(0, m, every) for m in range(M_TILES)])

@@ -40,6 +40,7 @@ K_ON_SCALAR = ((3, 3),)
 K_ON_GPSIMD = {(2, 2): NW, (2, 3): NW // 2}
 RUN = 8
 LATE = 2
+FIRST_KI = 3
 STEP_KI = 2
 SEQ = tuple([(w, n) for n in range(CHUNKS) for w in ("k", "q")])
 LAST = len(SEQ) - 1
@@ -333,14 +334,15 @@ def tile_attention_pa_kernel(tc, x, freqs_cos, freqs_sin, wq_bytes, wq_scale, wk
         for j in range(1, len(first)):
             q_vector.extend((e_ki(first[j][0], first[j][1]), e_q("k", first[j - 1][0], first[j - 1][1])))
         q_vector.extend((e_xq(0), e_xq(1), e_q("k", 1, PASSES - 1)))
-        rest = [u for u in vk if u not in first]
+        rest = [u for u in vk if u in K_ON_GPSIMD] + [u for u in vk if u not in first and u not in K_ON_GPSIMD]
         phase = [e_q("q", 0, g) for g in order_of("q", 0)] + [e_xq(2), e_xq(3), e_q("q", 0, 0)]
         for c in range(len(SEQ)):
             tch = [(("TCH", c - 1), touch, (c - 1,), (("ROT", c - 1, M_TILES - 1),), {}, {})] if c > 0 else []
             q_vector.extend((phase + tch) if c == LAST else (phase[:-1] + tch + phase[-1:]))
             q_vector.extend([e_rot(c, m) for m in range(M_TILES)])
-            phase = [e_ki(u[0], u[1]) for u in rest[:STEP_KI]]
-            rest = rest[STEP_KI:]
+            step = FIRST_KI if c == 0 else STEP_KI
+            phase = [e_ki(u[0], u[1]) for u in rest[:step]]
+            rest = rest[step:]
             if c + 2 <= LAST and c + 2 > 2:
                 w, n = SEQ[c + 2]
                 phase.extend([e_q(w, n, g) for g in (every[1:LATE] if c + 2 == LAST else order_of(w, n))] + [e_q(w, n, 0)])

from contextlib import ExitStack

import concourse.mybir as mybir
from concourse.masks import make_identity

F32 = mybir.dt.float32
BF16 = mybir.dt.bfloat16
U32 = mybir.dt.uint32
U8 = mybir.dt.uint8
FP8 = mybir.dt.float8_e4m3fn
FP8X4 = mybir.dt.float8_e4m3fn_x4
ALU = mybir.AluOpType
ACT = mybir.ActivationFunctionType

P = 128
S = 512
D = 2048
HD = 128
HALF = 64
PACK = 4
K_PASS = P * PACK
PASSES = D // K_PASS
M_TILES = S // P
NW = 512
CHUNKS = D // NW
HEADS_PER_CHUNK = NW // HD

FLOPS = 2 * 2 * S * D * D

WK_BUFS = 12
WQ_BUFS = 10
GK_BUFS = 8
GQ_BUFS = 6
WIDE_BUFS = 4
CODE_BUFS = {"k": 8, "q": 4}
BIG_BUFS = 3
BANKS = 4
PE_PASSES = (3, 3, 2, 2)
K_ON_SCALAR = ((3, 3),)
K_ON_GPSIMD = {(2, 2): NW, (2, 3): NW // 2}
RUN = 8
LATE = 2
FIRST_KI = 3
STEP_KI = 2
SEQ = tuple([(w, n) for n in range(CHUNKS) for w in ("k", "q")])
LAST = len(SEQ) - 1


def tile_attention_pa_kernel(tc, x, freqs_cos, freqs_sin, wq_bytes, wq_scale, wk, out_0, out_1):
    nc = tc.nc
    x_v = x.rearrange("b (m p) k -> (b m) p k", p=P)
    wqb_v = wq_bytes.rearrange("(g p t) n -> g p t n", p=P, t=PACK)
    wk_v = wk.rearrange("(g p t) n -> g p t n", p=P, t=PACK)
    outs_v = {
        "q": out_0.rearrange("b (m p) h d -> (b m) p (h d)", p=P),
        "k": out_1.rearrange("b (m p) h d -> (b m) p (h d)", p=P),
    }
    outs_3d = {
        "q": out_0.rearrange("b (m p) h d -> p (b m) (h d)", p=P),
        "k": out_1.rearrange("b (m p) h d -> p (b m) (h d)", p=P),
    }

    with ExitStack() as ctx:
        const = ctx.enter_context(tc.tile_pool(name="const", bufs=1))
        raw = ctx.enter_context(tc.tile_pool(name="raw", bufs=1))
        stage = ctx.enter_context(tc.tile_pool(name="stage", bufs=1))
        codes_pool = ctx.enter_context(tc.tile_pool(name="codes", bufs=1))
        big = ctx.enter_context(tc.tile_pool(name="big", bufs=BIG_BUFS))
        psum = ctx.enter_context(tc.psum_pool(name="psum", bufs=BANKS))
        ctx.enter_context(tc.manual_schedule())

        sc = const.tile([P, PASSES, PACK], F32, name="sc")
        nc.scalar.dma_start(out=sc[:], in_=wq_scale.rearrange("(g p t) o -> p g (t o)", p=P, t=PACK))
        cos_sb = const.tile([P, M_TILES, HALF], BF16, name="cos_sb")
        sin_sb = const.tile([P, M_TILES, HALF], BF16, name="sin_sb")

        warm = const.tile([P, 2], F32, name="warm")
        nc.vector.memset(warm[:, 0:1], 0.0)
        nc.scalar.activation(out=warm[:, 1:2], in_=warm[:, 0:1], func=ACT.Copy)

        junk = const.tile([P, 1], U32, name="junk")
        ident = const.tile([P, P], F32, name="ident")
        make_identity(nc, ident[:])
        ident_bf = const.tile([P, P], BF16, name="ident_bf")
        make_identity(nc, ident_bf[:])
        tab = const.tile([P, M_TILES, 2, HALF, 2], BF16, name="tab")

        wqb = {}
        wkr = {}
        xr = {}
        xt_tiles = {}
        xg_tiles = {}
        xc = {}
        xs = {}
        wide_t = {}
        il_t = {}
        grouped = {}
        ops = {}
        acc_t = {}
        prod = {}
        shape4 = [P, 2, HEADS_PER_CHUNK, HD]

        def load_wq(n, g):
            tq = raw.tile([P, PACK, NW], U8, name="wqb", tag="wqb", bufs=WQ_BUFS)
            nc.sync.dma_start(out=tq[:], in_=wqb_v[g][:, :, n * NW:(n + 1) * NW])
            wqb[(n, g)] = tq

        def load_wk(n, g):
            tk = raw.tile([P, PACK, NW], BF16, name="wkr", tag="wkr", bufs=WK_BUFS)
            nc.sync.dma_start(out=tk[:], in_=wk_v[g][:, :, n * NW:(n + 1) * NW])
            wkr[(n, g)] = tk

        def load_x(m):
            if m == 0:
                xr["all"] = big.tile([P, M_TILES, D], BF16, name="xr", tag="big")
            xr[m] = xr["all"][:, m, :]
            nc.sync.dma_start(out=xr[m], in_=x_v[m])

        def load_angles():
            nc.sync.dma_start(out=cos_sb[:], in_=freqs_cos.rearrange("(m p) i -> p m i", p=P))
            nc.sync.dma_start(out=sin_sb[:], in_=freqs_sin.rearrange("(m p) i -> p m i", p=P))

        def sin_table():
            nc.vector.tensor_copy(out=tab[:, :, 0], in_=cos_sb[:].unsqueeze(3).to_broadcast([P, M_TILES, HALF, 2]))
            nc.vector.tensor_copy(out=tab[:, :, 1, :, 0], in_=sin_sb[:])
            nc.vector.tensor_scalar(out=tab[:, :, 1, :, 1], in0=sin_sb[:], scalar1=-1.0, scalar2=None, op0=ALU.mult)

        def x_tag(m):
            return "il" if m == 2 else "acc"

        def x_transpose(m):
            words = xr[m].bitcast(F32)
            for half in range(2):
                xt = psum.tile([P, NW], F32, name="xt", tag=x_tag(m))
                for gl in range(2):
                    g = 2 * half + gl
                    for u in range(2):
                        j = 2 * gl + u
                        nc.tensor.transpose(xt[:, j * P:(j + 1) * P], words[:, 256 * g + u:256 * (g + 1):2], ident[:])
                xt_tiles[(m, half)] = xt

        def x_evac(m):
            xg = stage.tile([P, PASSES, P, PACK], BF16, name="xg", tag="gk", bufs=GK_BUFS, align_bytes=64)
            xg_tiles[m] = xg
            for half in range(2):
                dst = xg[:, 2 * half:2 * half + 2].rearrange("p g r t -> p (g r t)").bitcast(F32).rearrange("p (g r u) -> p g r u", g=2, u=2)
                nc.scalar.copy(out=dst, in_=xt_tiles[(m, half)][:].rearrange("p (g u r) -> p g r u", g=2, u=2))

        def x_quant(m):
            c = const.tile([P, PASSES * P], U32, name="xc_%d" % m, align_bytes=64)
            s = const.tile([P, PASSES * P], U8, name="xs_%d" % m, align_bytes=64)
            nc.vector.quantize_mx(out=c[:].bitcast(FP8X4), scales=s[:], in_=xg_tiles[m][:].rearrange("p g r t -> p (g r t)"))
            xc[m] = c
            xs[m] = s

        def direct(copy, dst, src):
            copy(out=dst.rearrange("p (c i) t -> p c t i", i=RUN), in_=src.rearrange("p t (c i) -> p c t i", i=RUN))

        def widen(n, g):
            wide = stage.tile([P, PACK, NW], BF16, name="wide", tag="wide", bufs=WIDE_BUFS)
            for t in range(PACK):
                nc.scalar.activation(out=wide[:, t, :], in_=wqb[(n, g)][:, t, :].bitcast(FP8), func=ACT.Copy, scale=sc[:, g, t:t + 1])
            wide_t[(n, g)] = wide

        def pe_interleave(n, g):
            wide = wide_t[(n, g)]
            banks = []
            for b in range(2):
                il = psum.tile([P, 2 * NW], BF16, name="il", tag="il")
                for h in range(2):
                    c0 = (2 * b + h) * P
                    nc.tensor.matmul(
                        out=il[:, h * NW:(h + 1) * NW].rearrange("p (c i t) -> p c t i", i=4, t=PACK),
                        lhsT=ident_bf[:],
                        rhs=wide[:, :, c0:c0 + P].rearrange("p t (c i) -> p c t i", i=4),
                        start=True,
                        stop=True,
                    )
                banks.append(il)
            il_t[(n, g)] = banks

        def new_gq(n, g):
            grouped[("q", n, g)] = stage.tile([P, NW, PACK], BF16, name="gq", tag="gq", bufs=GQ_BUFS, align_bytes=64)
            return grouped[("q", n, g)]

        def evac(n, g):
            flat = new_gq(n, g)[:].rearrange("p c t -> p (c t)")
            for b in range(2):
                nc.scalar.copy(out=flat[:, b * 2 * NW:(b + 1) * 2 * NW], in_=il_t[(n, g)][b][:])

        def q_direct(n, g):
            direct(nc.scalar.copy, new_gq(n, g)[:], wide_t[(n, g)][:])

        def k_interleave(n, g, on_gpsimd=0, c0=0):
            if c0 == 0:
                grouped[("k", n, g)] = stage.tile([P, NW, PACK], BF16, name="gk", tag="gk", bufs=GK_BUFS, align_bytes=64)
            gk = grouped[("k", n, g)]
            if c0 < on_gpsimd:
                nc.gpsimd.tensor_scalar(
                    out=gk[:, c0:on_gpsimd, :],
                    in0=wkr[(n, g)][:, :, c0:on_gpsimd].rearrange("p t c -> p c t"),
                    scalar1=1.0,
                    scalar2=0.0,
                    op0=ALU.mult,
                    op1=ALU.add,
                )
            else:
                direct(nc.scalar.copy if (n, g) in K_ON_SCALAR else nc.vector.tensor_copy, gk[:, c0:, :], wkr[(n, g)][:, :, c0:])

        def quant(w, n, g):
            c = codes_pool.tile([P, NW], U32, name=w + "c", tag=w + "c", bufs=CODE_BUFS[w], align_bytes=64)
            s = codes_pool.tile([P, NW], U8, name=w + "s", tag=w + "s", bufs=CODE_BUFS[w], align_bytes=64)
            nc.vector.quantize_mx(out=c[:].bitcast(FP8X4), scales=s[:], in_=grouped[(w, n, g)][:].rearrange("p c t -> p (c t)"))
            ops[(w, n, g)] = (c, s)

        def mm(c, m, gs):
            w, n = SEQ[c]
            if gs[0] == 0:
                acc_t[(c, m)] = psum.tile([P, NW], F32, name="acc", tag=("il" if c == LAST else "acc"))
            for g in gs:
                cd, s = ops[(w, n, g)]
                nc.tensor.matmul_mx(
                    out=acc_t[(c, m)][:],
                    lhsT=xc[m][:, g * P:(g + 1) * P].bitcast(FP8X4),
                    lhsT_scale=xs[m][:, g * P:(g + 1) * P],
                    rhs=cd[:].bitcast(FP8X4),
                    rhs_scale=s[:],
                    start=(g == 0),
                    stop=(g == PASSES - 1),
                )

        def rot(c, m):
            if m == 0:
                prod[c] = big.tile([P, M_TILES, 2, NW], F32, name="prod", tag="big")
            nc.vector.tensor_tensor(
                out=prod[c][:, m].rearrange("p u (h d) -> p u h d", d=HD),
                in0=acc_t[(c, m)][:].rearrange("p (h d) -> p h d", d=HD).unsqueeze(1).to_broadcast(shape4),
                in1=tab[:, m].rearrange("p u i e -> p u (i e)").unsqueeze(2).to_broadcast(shape4),
                op=ALU.mult,
            )

        def trigger(c):
            nc.gpsimd.tensor_copy(out=junk[:], in_=xc[M_TILES - 1][:, 0:1])

        def touch(c):
            word = prod[c][:, 0, 1, 0:1]
            nc.vector.tensor_copy(out=word, in_=word)

        def add_swapped(engine, c, m0, m1, c0=0, c1=NW):
            p1, p2 = [prod[c][:, m0:m1, u, c0:c1].rearrange("p m (j e) -> p m j e", e=2) for u in range(2)]
            engine.tensor_tensor(out=p1, in0=p1, in1=p2[:, :, :, ::-1], op=ALU.add)

        def add_chunk(c, m0=0, m1=M_TILES):
            add_swapped(nc.gpsimd, c, m0, m1)

        def store_chunk(c, m0=0, m1=M_TILES):
            w, n = SEQ[c]
            nc.sync.dma_start(out=outs_3d[w][:, m0:m1, n * NW:(n + 1) * NW], in_=prod[c][:, m0:m1, 0])

        def add_bank(c, m, c0=0, c1=NW):
            add_swapped(nc.vector, c, m, m + 1, c0, c1)

        def store_bank(c, m, c0=0, c1=NW):
            w, n = SEQ[c]
            nc.sync.dma_start(out=outs_v[w][m][:, n * NW + c0:n * NW + c1], in_=prod[c][:, m, 0, c0:c1])

        def src_of(w, n, g):
            if w == "k":
                return ("KI", n, g)
            return ("EV", n, g) if g < PE_PASSES[n] else ("QD", n, g)

        def e_lq(n, g):
            return (("LQ", n, g), load_wq, (n, g), (), {"wqb": 1}, {})

        def e_lk(n, g):
            return (("LK", n, g), load_wk, (n, g), (), {"wkr": 1}, {})

        def e_lx(m):
            return (("LX", m), load_x, (m,), (), {"big": 1} if m == 0 else {}, {})

        def e_w(n, g):
            return (("W", n, g), widen, (n, g), (("LQ", n, g),), {"wide": 1}, {"wqb": 1})

        def e_pi(n, g):
            return (("PI", n, g), pe_interleave, (n, g), (("W", n, g),), {"il": 2}, {"wide": 1})

        def e_ev(n, g):
            return (("EV", n, g), evac, (n, g), (("PI", n, g),), {"gq": 1}, {"il": 2})

        def e_qd(n, g):
            return (("QD", n, g), q_direct, (n, g), (("W", n, g),), {"gq": 1}, {"wide": 1})

        def e_ki(n, g):
            width = K_ON_GPSIMD.get((n, g), 0)
            if width == 0:
                return (("KI", n, g), k_interleave, (n, g), (("LK", n, g),), {"gk": 1}, {"wkr": 1})
            return (("KI", n, g), k_interleave, (n, g, width, width), (("KG", n, g),), {}, {"wkr": 1})

        def e_kg(n, g):
            width = K_ON_GPSIMD[(n, g)]
            whole = width == NW
            return (("KI" if whole else "KG", n, g), k_interleave, (n, g, width), (("LK", n, g),), {"gk": 1}, {"wkr": 1} if whole else {})

        def e_xt(m):
            return (("XT", m), x_transpose, (m,), (("LX", m),), {x_tag(m): 2}, {"big": 1} if m == M_TILES - 1 else {})

        def e_xe(m):
            return (("XE", m), x_evac, (m,), (("XT", m),), {"gk": 1}, {x_tag(m): 2})

        def e_xq(m):
            return (("XQ", m), x_quant, (m,), (("XE", m),), {}, {"gk": 1})

        def e_q(w, n, g):
            return (("Q", w, n, g), quant, (w, n, g), (src_of(w, n, g),), {w + "c": 1}, {"g" + w: 1})

        def e_mm(c, m, gs):
            w, n = SEQ[c]
            need = tuple([("Q", w, n, g) for g in gs]) + (("XQ", m),)
            takes = {("il" if c == LAST else "acc"): 1} if gs[0] == 0 else {}
            gives = {w + "c": len(gs)} if m == M_TILES - 1 else {}
            return (("MM", c, m, gs[-1]), mm, (c, m, gs), need, takes, gives)

        def e_rot(c, m):
            return (("ROT", c, m), rot, (c, m), (("MM", c, m, PASSES - 1),), {"big": 1} if m == 0 else {}, {("il" if c == LAST else "acc"): 1})

        every = tuple(range(PASSES))
        vk = [(n, g) for n in range(CHUNKS) for g in range(PASSES) if (n, g) not in K_ON_SCALAR and K_ON_GPSIMD.get((n, g), 0) < NW]

        def order_of(w, n):
            return (1, 3, 2) if w == "q" and PE_PASSES[n] == PASSES - 1 else (1, 2, 3)

        first = [(n, g) for n in range(2) for g in every]
        q_vector = [e_ki(0, 0), (("SIN",), sin_table, (), (("LA",),), {}, {})]
        for j in range(1, len(first)):
            q_vector.extend((e_ki(first[j][0], first[j][1]), e_q("k", first[j - 1][0], first[j - 1][1])))
        q_vector.extend((e_xq(0), e_xq(1), e_q("k", 1, PASSES - 1)))
        rest = [u for u in vk if u in K_ON_GPSIMD] + [u for u in vk if u not in first and u not in K_ON_GPSIMD]
        phase = [e_q("q", 0, g) for g in order_of("q", 0)] + [e_xq(2), e_xq(3), e_q("q", 0, 0)]
        for c in range(len(SEQ)):
            tch = [(("TCH", c - 1), touch, (c - 1,), (("ROT", c - 1, M_TILES - 1),), {}, {})] if c > 0 else []
            q_vector.extend((phase + tch) if c == LAST else (phase[:-1] + tch + phase[-1:]))
            q_vector.extend([e_rot(c, m) for m in range(M_TILES)])
            step = FIRST_KI if c == 0 else STEP_KI
            phase = [e_ki(u[0], u[1]) for u in rest[:step]]
            rest = rest[step:]
            if c + 2 <= LAST and c + 2 > 2:
                w, n = SEQ[c + 2]
                phase.extend([e_q(w, n, g) for g in (every[1:LATE] if c + 2 == LAST else order_of(w, n))] + [e_q(w, n, 0)])
            if c + 1 == LAST:
                phase = [e_q(SEQ[LAST][0], SEQ[LAST][1], g) for g in every[LATE:]]
                phase.extend([(("AV", m), add_bank, (c, m), (("ROT", c, m),), {}, {}) for m in range(2, M_TILES)])
        ends = [(m, 0, NW) for m in range(M_TILES - 1)] + [(M_TILES - 1, 0, NW // 2), (M_TILES - 1, NW // 2, NW)]
        q_vector.extend([(("AB", m, c0), add_bank, (LAST, m, c0, c1), (("ROT", LAST, m),), {}, {}) for m, c0, c1 in ends[1:]])

        def out_of(n, g):
            return e_ev(n, g) if g < PE_PASSES[n] else e_qd(n, g)

        q_scalar = [e_w(0, 0), e_w(0, 1), e_w(0, 2), out_of(0, 0), out_of(0, 1), e_w(0, 3), out_of(0, 2), e_xe(0), e_xe(1), e_qd(0, 3), e_xe(2), e_xe(3)]
        for n in range(1, CHUNKS):
            q_scalar.extend((e_w(n, 0), e_w(n, 1)))
            q_scalar.extend([e_ki(u[0], u[1]) for u in K_ON_SCALAR if u[0] == n])
            q_scalar.extend((e_w(n, 2), out_of(n, 0)))
            if PE_PASSES[n] == PASSES - 1:
                q_scalar.extend((out_of(n, 1), e_w(n, 3), e_qd(n, 3), out_of(n, 2)))
            elif n < CHUNKS - 1:
                q_scalar.extend((e_w(n, 3), out_of(n, 1), e_qd(n, 2), e_qd(n, 3)))
            else:
                q_scalar.extend((out_of(n, 1), e_w(n, 3), e_qd(n, 2), e_qd(n, 3)))

        q_tensor = [e_pi(0, 0), e_pi(0, 1), e_pi(0, 2), e_xt(0), e_xt(1), e_xt(2), e_xt(3)]
        q_tensor.extend([e_mm(0, m, every) for m in range(M_TILES)])
        q_tensor.extend((e_pi(1, 0), e_pi(1, 1)))
        for c in range(LAST):
            w, n = SEQ[c]
            if c + 1 < LAST:
                q_tensor.extend([e_mm(c + 1, m, every) for m in range(M_TILES)])
            else:
                q_tensor.extend([e_mm(LAST, m, every[:LATE]) for m in range(M_TILES)])
                q_tensor.extend([e_mm(LAST, m, every[LATE:]) for m in range(M_TILES)])
            if w == "k" and n + 1 < CHUNKS:
                q_tensor.append(e_pi(n + 1, 2))
            if w == "q" and n + 2 < CHUNKS:
                q_tensor.extend((e_pi(n + 2, 0), e_pi(n + 2, 1)))

        q_tensor = [e for e in q_tensor if e[0][0] != "PI" or e[0][2] < PE_PASSES[e[0][1]]]

        q_gpsimd = []
        q_gpsimd.append((("TRG", 0), trigger, (0,), (("XQ", M_TILES - 1),), {}, {}))
        q_gpsimd.extend([e_kg(u[0], u[1]) for u in K_ON_GPSIMD])
        q_gpsimd.extend([(("ADD", c), add_chunk, (c,), (("TCH", c),), {}, {}) for c in range(LAST - 1)])
        q_gpsimd.append((("ADD", LAST - 1), add_chunk, (LAST - 1, 0, 2), (("TCH", LAST - 1),), {}, {}))
        q_gpsimd.append((("AB", 0, 0), add_chunk, (LAST, 0, 1), (("ROT", LAST, 0),), {}, {}))

        q_sync = [e_lq(0, 0), e_lk(0, 0), (("LA",), load_angles, (), (), {}, {}), e_lq(0, 1), e_lk(0, 1), e_lq(0, 2), e_lk(0, 2), e_lk(0, 3), e_lk(1, 0), e_lq(0, 3), e_lk(1, 1), e_lk(1, 2),
                  e_lx(0), e_lx(1), e_lk(1, 3), e_lx(2), e_lx(3), e_lq(1, 0), e_lk(2, 2), e_lk(2, 3), e_lq(1, 1), e_lq(1, 2), e_lk(2, 0), e_lq(1, 3), e_lk(2, 1)]
        q_sync.extend([e_lq(2, g) for g in range(PASSES)])
        for g in range(PASSES):
            q_sync.extend((e_lk(3, g), e_lq(3, g)))
        q_sync.extend([(("ST", c), store_chunk, (c,), (("ADD", c),), {}, {"big": 1}) for c in range(LAST - 1)])
        q_sync.append((("STa", LAST - 1), store_chunk, (LAST - 1, 2, M_TILES), (("AV", M_TILES - 1),), {}, {}))
        q_sync.append((("ST", LAST - 1), store_chunk, (LAST - 1, 0, 2), (("ADD", LAST - 1),), {}, {"big": 1}))
        q_sync.extend([(("SB", m, c0), store_bank, (LAST, m, c0, c1), (("AB", m, c0),), {}, {}) for m, c0, c1 in ends])

        room = {"wqb": WQ_BUFS, "wkr": WK_BUFS, "big": BIG_BUFS, "wide": WIDE_BUFS, "il": BANKS, "acc": BANKS,
                "gq": GQ_BUFS, "gk": GK_BUFS, "kc": CODE_BUFS["k"], "qc": CODE_BUFS["q"]}
        queues = [q_sync, q_scalar, q_tensor, q_vector, q_gpsimd]
        at = [0] * len(queues)
        written = set()
        moved = True
        while moved:
            moved = False
            for j in range(len(queues)):
                while at[j] < len(queues[j]):
                    key, fn, args, need, takes, gives = queues[j][at[j]]
                    if not all([k in written for k in need]) or not all([room[t] >= takes[t] for t in takes]):
                        break
                    fn(*args)
                    written.add(key)
                    for t in takes:
                        room[t] -= takes[t]
                    for t in gives:
                        room[t] += gives[t]
                    at[j] += 1
                    moved = True
        assert all([at[j] == len(queues[j]) for j in range(len(queues))])
